import numpy as np
import ml_dtypes


def mxq(x, axis, fmt="e4m3"):
    dtype, down = {"e4m3": (ml_dtypes.float8_e4m3fn, 7), "e5m2": (ml_dtypes.float8_e5m2, 14)}[fmt]
    v = np.moveaxis(np.asarray(x, np.float32).astype(ml_dtypes.bfloat16).astype(np.float64), axis, -1)
    blocks = v.reshape(v.shape[:-1] + (-1, 32))
    amax = np.abs(blocks).max(-1, keepdims=True)
    byte = np.maximum(np.where(amax > 0, np.frexp(amax)[1] - 1 + 127, 0) - down, 1)
    scale = np.exp2(byte - 127.0)
    codes = (blocks / scale).astype(np.float32).astype(dtype).astype(np.float64)
    return np.moveaxis((codes * scale).reshape(v.shape), -1, axis)


WIDE = False


def mx_kscale(k):
    if not WIDE:
        return np.ones(k)
    levels = np.array([10, -10, 5, -5, 0])
    a = np.random.permutation(np.resize(levels, k // 512 * 4)).reshape(k // 512, 4)
    idx = np.arange(k)
    return np.exp2(a[idx // 512, idx % 128 // 32])


BF16 = ml_dtypes.bfloat16


def bf(x):
    return np.asarray(x, np.float32).astype(BF16)


def f64(x):
    return np.asarray(x).astype(np.float64)


N, E, DIM = 6144, 1024, 512
LN_EPS = 1e-5
DENSITY = 0.005
BARE = 0.02


def layernorm(x, g, b):
    m = x.mean(-1, keepdims=True)
    v = np.square(x - m).mean(-1, keepdims=True)
    return (x - m) * (1.0 / np.sqrt(v + LN_EPS)) * g + b


def draw_incidence():
    inc = np.random.random((N, E)) < DENSITY
    inc[np.random.random(N) < BARE, :] = False
    inc[:, np.random.random(E) < BARE] = False
    return bf(inc)


def setup_inputs():
    t = mx_kscale(DIM)
    return {
        "x_0": bf(np.random.standard_normal((N, DIM))),
        "x_1_new": bf(np.random.standard_normal((E, DIM)) * 1.3 * t),
        "incidence_1": draw_incidence(),
        "Wn": bf(np.random.standard_normal((DIM, DIM)) * 2.0 / np.sqrt(DIM) / t[:, None]),
        "bn": bf(np.random.standard_normal(DIM) * 0.3),
        "ln1_g": bf(1.0 + 0.1 * np.random.standard_normal(DIM)),
        "ln1_b": bf(0.1 * np.random.standard_normal(DIM)),
        "gate_local": bf(0.8 + 0.4 * np.random.random(1)),
    }


def reference(x_0, x_1_new, incidence_1, Wn, bn, ln1_g, ln1_b, gate_local):
    H = f64(incidence_1)
    D_v = np.maximum(H.sum(1, keepdims=True), 1.0)
    D_e = np.maximum(H.sum(0, keepdims=True), 1.0)
    H_norm = H / np.sqrt(D_v) / np.sqrt(D_e)
    msg = mxq(H_norm, 1, "e4m3") @ mxq(f64(x_1_new), 0, "e4m3")
    upd = (mxq(msg, 1, "e4m3") @ mxq(f64(Wn), 0, "e4m3")) + f64(bn)
    return layernorm(f64(x_0) + np.tanh(f64(gate_local)) * upd, f64(ln1_g), f64(ln1_b))

@@ -1,0 +1,383 @@
+from contextlib import ExitStack
+
+import concourse.mybir as mybir
+from concourse.masks import make_identity
+
+FLOPS = 2 * 6144 * 1024 * 512 + 2 * 6144 * 512 * 512
+
+F32 = mybir.dt.float32
+BF16 = mybir.dt.bfloat16
+U32 = mybir.dt.uint32
+U8 = mybir.dt.uint8
+FP8X4 = mybir.dt.float8_e4m3fn_x4
+ALU = mybir.AluOpType
+ACT = mybir.ActivationFunctionType
+AX = mybir.AxisListType
+
+P = 128
+N_NODES = 6144
+N_EDGES = 1024
+DIM = 512
+A = 4
+CHUNK = P * A
+N_CHUNKS = N_NODES // CHUNK
+LN_EPS = 1e-5
+NW = 2
+GP_PLANES = (6, 7)
+
+
+def tile_hypergraphgpslayer_pa_t_kernel(
+    tc, x_0, x_1_new, incidence_1, Wn, bn, ln1_g, ln1_b, gate_local, out
+):
+    nc = tc.nc
+    with ExitStack() as ctx:
+        const = ctx.enter_context(tc.tile_pool(name="const", bufs=1))
+        keep = ctx.enter_context(tc.tile_pool(name="keep", bufs=1))
+        small = ctx.enter_context(tc.tile_pool(name="small", bufs=4))
+        xyp = ctx.enter_context(tc.tile_pool(name="xyp", bufs=3))
+        work = ctx.enter_context(tc.tile_pool(name="work", bufs=2))
+        psum = ctx.enter_context(tc.psum_pool(name="psum", bufs=1))
+
+        ones_w = const.tile([P, NW], BF16)
+        nc.vector.memset(ones_w[:], 1.0)
+        ones_m = const.tile([P, P], BF16)
+        nc.vector.memset(ones_m[:], 1.0)
+        ident = const.tile([P, P], F32)
+        make_identity(nc, ident[:])
+        vecs = const.tile([P, 3, DIM], BF16)
+        nc.vector.memset(vecs[:], 0.0)
+        nc.scalar.dma_start(out=vecs[0:1, 0, :], in_=bn.unsqueeze(0))
+        nc.scalar.dma_start(out=vecs[0:1, 1, :], in_=ln1_g.unsqueeze(0))
+        nc.scalar.dma_start(out=vecs[0:1, 2, :], in_=ln1_b.unsqueeze(0))
+        gt = const.tile([P, 1], BF16)
+        nc.scalar.dma_start(out=gt[:], in_=gate_local.partition_broadcast(P))
+        gcol = const.tile([P, 1], F32)
+        nc.scalar.activation(out=gcol[:], in_=gt[:], func=ACT.Tanh)
+
+        x1cod = const.tile([P, 2, DIM], U32, align_bytes=64)
+        x1sc = const.tile([P, 2, DIM], U8, align_bytes=64)
+        wcod = const.tile([P, DIM], U32, align_bytes=64)
+        wsc = const.tile([P, DIM], U8, align_bytes=64)
+        c_bc = const.tile([P, DIM], F32)
+        beta_bc = const.tile([P, DIM], F32)
+        b4 = const.tile([P, 8], F32)
+        av_all = const.tile([P, N_CHUNKS * A], F32)
+
+        g_ps = psum.tile([P, DIM], F32, name="g_ps")
+        de_ps = psum.tile([P, DIM], F32, name="de_ps")
+
+        hnat = [keep.tile([P, A, N_EDGES], BF16, name="hnat%d" % c) for c in range(N_CHUNKS)]
+
+        for c in range(N_CHUNKS):
+            nc.sync.dma_start(
+                out=hnat[c][:],
+                in_=incidence_1[c * CHUNK : (c + 1) * CHUNK, :].rearrange("(p a) e -> p a e", a=A),
+            )
+        x1raw = work.tile([P, 8, DIM], BF16, tag="cp", name="x1raw")
+        nc.sync.dma_start(
+            out=x1raw[:].rearrange("p (w e) d -> p w (e d)", e=2),
+            in_=x_1_new.rearrange("(w p e) d -> p w (e d)", w=4, p=P, e=2),
+        )
+        wraw = work.tile([P, 4, DIM], BF16, tag="msgg", name="wraw", align_bytes=64)
+        nc.sync.dma_start(out=wraw[:], in_=Wn.rearrange("(t p) n -> p t n", p=P))
+
+        xys = {}
+
+        def residual(c):
+            x0c = xyp.tile([P, A, DIM], BF16, name="x0c")
+            nc.sync.dma_start(
+                out=x0c[:],
+                in_=x_0[c * CHUNK : (c + 1) * CHUNK, :].rearrange("(p a) d -> p a d", a=A),
+            )
+            xy = xyp.tile([P, A, DIM], F32, name="xy")
+            nc.gpsimd.tensor_tensor(
+                out=xy[:],
+                in0=x0c[:],
+                in1=c_bc[:].unsqueeze(1).to_broadcast([P, A, DIM]),
+                op=ALU.add,
+            )
+            xys[c] = xy
+
+        with tc.tile_pool(name="tree", bufs=1) as tree:
+            for c in range(N_CHUNKS):
+                hc = hnat[c]
+                for j in range(8):
+                    col = (c * 8 + j) * NW
+                    for a in range(A):
+                        nc.tensor.matmul(
+                            out=de_ps[:, col : col + NW],
+                            lhsT=hc[:, a, P * j : P * j + P],
+                            rhs=ones_w[:],
+                            start=(a == 0),
+                            stop=(a == A - 1),
+                        )
+                dv = small.tile([P, A], F32, name="dv")
+                if c % 3 == 2:
+                    for a in range(A):
+                        junk1 = tree.tile([P, N_EDGES], BF16, name="junk1")
+                        nc.scalar.activation(
+                            out=junk1[:], in_=hc[:, a, :], func=ACT.Copy, accum_out=dv[:, a : a + 1]
+                        )
+                else:
+                    width = N_EDGES // 2
+                    src = hc
+                    while width >= 32:
+                        dst = tree.tile([P, A, width], BF16, name="tr%d" % width)
+                        nc.vector.tensor_tensor(
+                            out=dst[:],
+                            in0=src[:, :, 0:width],
+                            in1=src[:, :, width : 2 * width],
+                            op=ALU.add,
+                        )
+                        src = dst
+                        width //= 2
+                    nc.vector.tensor_reduce(out=dv[:], in_=src[:], axis=AX.X, op=ALU.add)
+                dvm = small.tile([P, A], F32, name="dvm")
+                nc.vector.tensor_scalar_max(out=dvm[:], in0=dv[:], scalar1=1.0)
+                dvs = small.tile([P, A], F32, name="dvs")
+                nc.scalar.activation(out=dvs[:], in_=dvm[:], func=ACT.Sqrt)
+                nc.vector.reciprocal(out=av_all[:, A * c : A * c + A], in_=dvs[:])
+                if c == 1:
+                    bn_ps = psum.tile([P, DIM], F32, tag="pb", bufs=2, name="bn_ps")
+                    nc.tensor.matmul(
+                        out=bn_ps[:], lhsT=ones_m[:], rhs=vecs[:, 0, :], start=True, stop=True
+                    )
+                    nc.vector.tensor_scalar(
+                        out=c_bc[:], in0=bn_ps[:], scalar1=gcol[:], scalar2=None, op0=ALU.mult
+                    )
+                    nc.tensor.matmul(
+                        out=g_ps[:], lhsT=ones_m[:], rhs=vecs[:, 1, :], start=True, stop=True
+                    )
+                    be_ps = psum.tile([P, DIM], F32, tag="pb", bufs=2, name="be_ps")
+                    nc.tensor.matmul(
+                        out=be_ps[:], lhsT=ones_m[:], rhs=vecs[:, 2, :], start=True, stop=True
+                    )
+                    nc.scalar.copy(out=beta_bc[:], in_=be_ps[:])
+                    sel = []
+                    for h in range(2):
+                        for eo in range(2):
+                            s = const.tile([P, P], F32, name="sel%d%d" % (h, eo))
+                            nc.gpsimd.memset(s[:], 0.0)
+                            nc.gpsimd.tensor_copy(
+                                out=s[:, 64 * h : 64 * h + 64],
+                                in_=ident[:].rearrange("p (q e) -> p e q", e=2)[:, eo, :],
+                            )
+                            sel.append(s)
+
+            de = small.tile([P, 8], F32, name="de")
+            nc.vector.tensor_reduce(
+                out=de[:],
+                in_=de_ps[:, 0 : N_CHUNKS * 8 * NW].rearrange(
+                    "p (c j w) -> p j c w", c=N_CHUNKS, j=8, w=NW
+                )[:, :, :, 0],
+                axis=AX.X,
+                op=ALU.add,
+            )
+            nc.vector.tensor_scalar_max(out=de[:], in0=de[:], scalar1=1.0)
+            des = small.tile([P, 8], F32, name="des")
+            nc.scalar.activation(out=des[:], in_=de[:], func=ACT.Sqrt)
+            bnat = small.tile([P, 8], F32, name="bnat")
+            nc.vector.reciprocal(out=bnat[:], in_=des[:])
+            bnat_v = bnat[:].rearrange("p (w h) -> p h w", h=2)
+            b4_ps = psum.tile([P, 2, 4], F32, tag="pb", bufs=2, name="b4_ps")
+            for eo in range(2):
+                for h in range(2):
+                    nc.tensor.matmul(
+                        out=b4_ps[:, eo, :],
+                        lhsT=sel[2 * h + eo][:],
+                        rhs=bnat_v[:, h, :],
+                        start=(h == 0),
+                        stop=(h == 1),
+                    )
+            nc.vector.tensor_copy(
+                out=b4[:].rearrange("p (w e) -> p w e", e=2),
+                in_=b4_ps[:].rearrange("p e w -> p w e"),
+            )
+
+        state = {}
+
+        def stage_a(c):
+            ab_ps = psum.tile([P, A, P], F32, tag="pb", bufs=2, name="ab_ps")
+            for a in range(A):
+                col = A * c + a
+                nc.tensor.transpose(
+                    ab_ps[:, a, :], av_all[:, col : col + 1].to_broadcast([P, P]), ident[:]
+                )
+            abc = work.tile([P, CHUNK], F32, name="abc")
+            nc.scalar.copy(out=abc[:], in_=ab_ps[:].rearrange("p a n -> p (a n)"))
+            cp = work.tile([P, 2, 4, CHUNK], BF16, tag="cp", name="cp")
+            for i in range(8):
+                if i in GP_PLANES:
+                    nc.gpsimd.tensor_scalar(
+                        out=cp[:, i // 4, i % 4, :],
+                        in0=abc[:],
+                        scalar1=b4[:, i : i + 1],
+                        scalar2=0.0,
+                        op0=ALU.mult,
+                        op1=ALU.add,
+                    )
+                else:
+                    nc.scalar.activation(
+                        out=cp[:, i // 4, i % 4, :],
+                        in_=abc[:],
+                        func=ACT.Copy,
+                        scale=b4[:, i : i + 1],
+                    )
+            hng = work.tile([P, 2, CHUNK, 4], BF16, tag="hng", name="hng", align_bytes=64)
+            for a in range(A):
+                cols = slice(P * a, P * a + P)
+                ht = psum.tile([P, 4, P], F32, tag="ht", bufs=2, name="ht")
+                hw = hnat[c][:, a, :].bitcast(F32)
+                for wb in range(4):
+                    nc.tensor.transpose(ht[:, wb, :], hw[:, P * wb : P * wb + P], ident[:])
+                ht_b = (
+                    ht[:]
+                    .rearrange("p w n -> p (w n)")
+                    .bitcast(BF16)
+                    .rearrange("p (w n e) -> p w n e", w=4, n=P, e=2)
+                )
+                for g in range(2):
+                    nc.vector.tensor_tensor(
+                        out=hng[:, g, cols, :].rearrange("p n (u e) -> p n u e", u=2),
+                        in0=ht_b[:, 2 * g : 2 * g + 2].rearrange("p u n e -> p n u e"),
+                        in1=cp[:, g, :, cols].rearrange("p (u e) n -> p n u e", u=2),
+                        op=ALU.mult,
+                    )
+            hcod = work.tile([P, 2, CHUNK], U32, name="hcod", align_bytes=64)
+            hsc = work.tile([P, 2, CHUNK], U8, name="hsc", align_bytes=64)
+            nc.vector.quantize_mx(
+                out=hcod[:].rearrange("p g n -> p (g n)").bitcast(FP8X4),
+                scales=hsc[:].rearrange("p g n -> p (g n)"),
+                in_=hng[:].rearrange("p g n t -> p (g n t)"),
+            )
+            state[c] = (hcod, hsc)
+
+        def stage_b(c):
+            hcod, hsc = state[c]
+            xy = xys[c]
+            msgg = work.tile([P, CHUNK, 4], BF16, tag="msgg", name="msgg", align_bytes=64)
+            for a in range(A):
+                cols = slice(P * a, P * a + P)
+                m1 = psum.tile([P, 4, P], F32, tag="m1", bufs=2, name="m1")
+                for tb in range(4):
+                    for g in range(2):
+                        nc.tensor.matmul_mx(
+                            out=m1[:, tb, :],
+                            lhsT=x1cod[:, g, P * tb : P * tb + P].bitcast(FP8X4),
+                            lhsT_scale=x1sc[:, g, P * tb : P * tb + P],
+                            rhs=hcod[:, g, cols].bitcast(FP8X4),
+                            rhs_scale=hsc[:, g, cols],
+                            start=(g == 0),
+                            stop=(g == 1),
+                        )
+                nc.scalar.copy(out=msgg[:, cols, :], in_=m1[:].rearrange("p t n -> p n t"))
+            mcod = work.tile([P, CHUNK], U32, name="mcod", align_bytes=64)
+            msc = work.tile([P, CHUNK], U8, name="msc", align_bytes=64)
+            nc.vector.quantize_mx(
+                out=mcod[:].bitcast(FP8X4),
+                scales=msc[:],
+                in_=msgg[:].rearrange("p n t -> p (n t)"),
+            )
+            sy = small.tile([P, A], F32, name="sy")
+            for a in range(A):
+                cols = slice(P * a, P * a + P)
+                m2 = psum.tile([P, DIM], F32, tag="pb", bufs=2, name="m2")
+                nc.tensor.matmul_mx(
+                    out=m2[:],
+                    lhsT=mcod[:, cols].bitcast(FP8X4),
+                    lhsT_scale=msc[:, cols],
+                    rhs=wcod[:].bitcast(FP8X4),
+                    rhs_scale=wsc[:],
+                    start=True,
+                    stop=True,
+                )
+                nc.vector.scalar_tensor_tensor(
+                    out=xy[:, a, :],
+                    in0=m2[:],
+                    scalar=gcol[:],
+                    in1=xy[:, a, :],
+                    op0=ALU.mult,
+                    op1=ALU.add,
+                    accum_out=sy[:, a : a + 1],
+                )
+            nm = small.tile([P, A], F32, name="nm")
+            nc.vector.tensor_scalar_mul(out=nm[:], in0=sy[:], scalar1=-1.0 / DIM)
+            state[c] = nm
+
+        def stage_c(c):
+            nm = state[c]
+            xy = xys[c]
+            ss = small.tile([P, A], F32, name="ss")
+            for a in range(A):
+                junk = work.tile([P, DIM], BF16, name="junk")
+                nc.scalar.activation(
+                    out=junk[:],
+                    in_=xy[:, a, :],
+                    func=ACT.Square,
+                    bias=nm[:, a : a + 1],
+                    scale=1.0,
+                    accum_out=ss[:, a : a + 1],
+                )
+            vv = small.tile([P, A], F32, name="vv")
+            nc.vector.tensor_scalar(
+                out=vv[:], in0=ss[:], scalar1=1.0 / DIM, scalar2=LN_EPS, op0=ALU.mult, op1=ALU.add
+            )
+            sd = small.tile([P, A], F32, name="sd")
+            nc.scalar.activation(out=sd[:], in_=vv[:], func=ACT.Sqrt)
+            rs = small.tile([P, A], F32, name="rs")
+            nc.vector.reciprocal(out=rs[:], in_=sd[:])
+            nmrs = small.tile([P, A], F32, name="nmrs")
+            nc.vector.tensor_tensor(out=nmrs[:], in0=nm[:], in1=rs[:], op=ALU.mult)
+            for a in range(A):
+                nc.scalar.activation(
+                    out=xy[:, a, :],
+                    in_=xy[:, a, :],
+                    func=ACT.Identity,
+                    bias=nmrs[:, a : a + 1],
+                    scale=rs[:, a : a + 1],
+                )
+            nc.vector.tensor_tensor(
+                out=xy[:],
+                in0=xy[:],
+                in1=g_ps[:].unsqueeze(1).to_broadcast([P, A, DIM]),
+                op=ALU.mult,
+            )
+            nc.gpsimd.tensor_tensor(
+                out=xy[:],
+                in0=xy[:],
+                in1=beta_bc[:].unsqueeze(1).to_broadcast([P, A, DIM]),
+                op=ALU.add,
+            )
+            nc.sync.dma_start(
+                out=out[c * CHUNK : (c + 1) * CHUNK, :].rearrange("(p a) d -> p a d", a=A),
+                in_=xy[:],
+            )
+
+        x1g = work.tile([P, 2, DIM, 4], BF16, tag="hng", name="x1g", align_bytes=64)
+        for g in range(2):
+            nc.vector.tensor_copy(
+                out=x1g[:, g], in_=x1raw[:, 4 * g : 4 * g + 4, :].rearrange("p t d -> p d t")
+            )
+        wg = work.tile([P, DIM, 4], BF16, tag="msgg", name="wg", align_bytes=64)
+        nc.vector.tensor_copy(out=wg[:], in_=wraw[:].rearrange("p t n -> p n t"))
+        nc.vector.quantize_mx(
+            out=x1cod[:].rearrange("p g d -> p (g d)").bitcast(FP8X4),
+            scales=x1sc[:].rearrange("p g d -> p (g d)"),
+            in_=x1g[:].rearrange("p g d t -> p (g d t)"),
+        )
+        nc.vector.quantize_mx(
+            out=wcod[:].bitcast(FP8X4),
+            scales=wsc[:],
+            in_=wg[:].rearrange("p n t -> p (n t)"),
+        )
+
+        residual(0)
+        stage_a(0)
+        for c in range(N_CHUNKS):
+            if c + 1 < N_CHUNKS:
+                residual(c + 1)
+                stage_a(c + 1)
+            stage_b(c)
+            if c >= 1:
+                stage_c(c - 1)
+        stage_c(N_CHUNKS - 1)

@@ -1,5 +1,6 @@
 from contextlib import ExitStack
 
+import concourse.bass as bass
 import concourse.mybir as mybir
 from concourse.masks import make_identity
 
@@ -23,7 +24,6 @@ CHUNK = P * A
 N_CHUNKS = N_NODES // CHUNK
 LN_EPS = 1e-5
 NW = 2
-GP_PLANES = (6, 7)
 
 
 def tile_hypergraphgpslayer_pa_t_kernel(
@@ -34,73 +34,98 @@ def tile_hypergraphgpslayer_pa_t_kernel(
         const = ctx.enter_context(tc.tile_pool(name="const", bufs=1))
         keep = ctx.enter_context(tc.tile_pool(name="keep", bufs=1))
         small = ctx.enter_context(tc.tile_pool(name="small", bufs=4))
-        xyp = ctx.enter_context(tc.tile_pool(name="xyp", bufs=3))
-        work = ctx.enter_context(tc.tile_pool(name="work", bufs=2))
         psum = ctx.enter_context(tc.psum_pool(name="psum", bufs=1))
 
+        ident = const.tile([P, P], F32)
+        make_identity(nc, ident[:])
         ones_w = const.tile([P, NW], BF16)
         nc.vector.memset(ones_w[:], 1.0)
         ones_m = const.tile([P, P], BF16)
         nc.vector.memset(ones_m[:], 1.0)
-        ident = const.tile([P, P], F32)
-        make_identity(nc, ident[:])
-        vecs = const.tile([P, 3, DIM], BF16)
-        nc.vector.memset(vecs[:], 0.0)
-        nc.scalar.dma_start(out=vecs[0:1, 0, :], in_=bn.unsqueeze(0))
-        nc.scalar.dma_start(out=vecs[0:1, 1, :], in_=ln1_g.unsqueeze(0))
-        nc.scalar.dma_start(out=vecs[0:1, 2, :], in_=ln1_b.unsqueeze(0))
-        gt = const.tile([P, 1], BF16)
-        nc.scalar.dma_start(out=gt[:], in_=gate_local.partition_broadcast(P))
-        gcol = const.tile([P, 1], F32)
-        nc.scalar.activation(out=gcol[:], in_=gt[:], func=ACT.Tanh)
+        sel = []
+        for h in range(2):
+            for eo in range(2):
+                s = const.tile([P, P], F32, name="sel%d%d" % (h, eo))
+                nc.vector.memset(s[:], 0.0)
+                nc.vector.tensor_copy(
+                    out=s[:, 64 * h : 64 * h + 64],
+                    in_=ident[:].rearrange("p (q e) -> p e q", e=2)[:, eo, :],
+                )
+                sel.append(s)
 
         x1cod = const.tile([P, 2, DIM], U32, align_bytes=64)
         x1sc = const.tile([P, 2, DIM], U8, align_bytes=64)
         wcod = const.tile([P, DIM], U32, align_bytes=64)
         wsc = const.tile([P, DIM], U8, align_bytes=64)
         c_bc = const.tile([P, DIM], F32)
-        beta_bc = const.tile([P, DIM], F32)
+        gcol = const.tile([P, 1], F32)
         b4 = const.tile([P, 8], F32)
-        av_all = const.tile([P, N_CHUNKS * A], F32)
 
         g_ps = psum.tile([P, DIM], F32, name="g_ps")
+        b_ps = psum.tile([P, DIM], F32, name="b_ps")
         de_ps = psum.tile([P, DIM], F32, name="de_ps")
 
-        hnat = [keep.tile([P, A, N_EDGES], BF16, name="hnat%d" % c) for c in range(N_CHUNKS)]
+        htg = [
+            keep.tile([P, 2, CHUNK, 4], BF16, name="htg%d" % c, align_bytes=64)
+            for c in range(N_CHUNKS)
+        ]
+        abc = [keep.tile([P, CHUNK], F32, name="abc%d" % c) for c in range(N_CHUNKS)]
 
-        for c in range(N_CHUNKS):
+        with ExitStack() as ph1:
+            hpool = ph1.enter_context(tc.tile_pool(name="hpool", bufs=3))
+            setup = ph1.enter_context(tc.tile_pool(name="setup", bufs=1))
+            tree = ph1.enter_context(tc.tile_pool(name="tree", bufs=2))
+
+            x1raw = setup.tile([P, 8, DIM], BF16)
             nc.sync.dma_start(
-                out=hnat[c][:],
-                in_=incidence_1[c * CHUNK : (c + 1) * CHUNK, :].rearrange("(p a) e -> p a e", a=A),
+                out=x1raw[:].rearrange("p (w e) d -> p w (e d)", e=2),
+                in_=x_1_new.rearrange("(w p e) d -> p w (e d)", w=4, p=P, e=2),
             )
-        x1raw = work.tile([P, 8, DIM], BF16, tag="cp", name="x1raw")
-        nc.sync.dma_start(
-            out=x1raw[:].rearrange("p (w e) d -> p w (e d)", e=2),
-            in_=x_1_new.rearrange("(w p e) d -> p w (e d)", w=4, p=P, e=2),
-        )
-        wraw = work.tile([P, 4, DIM], BF16, tag="msgg", name="wraw", align_bytes=64)
-        nc.sync.dma_start(out=wraw[:], in_=Wn.rearrange("(t p) n -> p t n", p=P))
+            wraw = setup.tile([P, 4, DIM], BF16)
+            nc.sync.dma_start(out=wraw[:], in_=Wn.rearrange("(t p) n -> p t n", p=P))
+            vecs = setup.tile([P, 3, DIM], BF16)
+            nc.vector.memset(vecs[:], 0.0)
+            nc.scalar.dma_start(out=vecs[0:1, 0, :], in_=bn.unsqueeze(0))
+            nc.scalar.dma_start(out=vecs[0:1, 1, :], in_=ln1_g.unsqueeze(0))
+            nc.scalar.dma_start(out=vecs[0:1, 2, :], in_=ln1_b.unsqueeze(0))
+            gt = setup.tile([P, 1], BF16)
+            nc.scalar.dma_start(out=gt[:], in_=gate_local.partition_broadcast(P))
+            nc.scalar.activation(out=gcol[:], in_=gt[:], func=ACT.Tanh)
 
-        xys = {}
-
-        def residual(c):
-            x0c = xyp.tile([P, A, DIM], BF16, name="x0c")
-            nc.sync.dma_start(
-                out=x0c[:],
-                in_=x_0[c * CHUNK : (c + 1) * CHUNK, :].rearrange("(p a) d -> p a d", a=A),
+            bn_ps = psum.tile([P, DIM], F32, tag="pb", bufs=2, name="bn_ps")
+            nc.tensor.matmul(out=bn_ps[:], lhsT=ones_m[:], rhs=vecs[:, 0, :], start=True, stop=True)
+            nc.tensor.matmul(out=g_ps[:], lhsT=ones_m[:], rhs=vecs[:, 1, :], start=True, stop=True)
+            nc.tensor.matmul(out=b_ps[:], lhsT=ones_m[:], rhs=vecs[:, 2, :], start=True, stop=True)
+            nc.vector.tensor_scalar(
+                out=c_bc[:], in0=bn_ps[:], scalar1=gcol[:], scalar2=None, op0=ALU.mult
             )
-            xy = xyp.tile([P, A, DIM], F32, name="xy")
-            nc.gpsimd.tensor_tensor(
-                out=xy[:],
-                in0=x0c[:],
-                in1=c_bc[:].unsqueeze(1).to_broadcast([P, A, DIM]),
-                op=ALU.add,
-            )
-            xys[c] = xy
 
-        with tc.tile_pool(name="tree", bufs=1) as tree:
+            x1g = setup.tile([P, 2, DIM, 4], BF16, align_bytes=64)
+            for g in range(2):
+                nc.vector.tensor_copy(
+                    out=x1g[:, g], in_=x1raw[:, 4 * g : 4 * g + 4, :].rearrange("p t d -> p d t")
+                )
+            wg = setup.tile([P, DIM, 4], BF16, align_bytes=64)
+            nc.vector.tensor_copy(out=wg[:], in_=wraw[:].rearrange("p t n -> p n t"))
+            nc.vector.quantize_mx(
+                out=x1cod[:].rearrange("p g d -> p (g d)").bitcast(FP8X4),
+                scales=x1sc[:].rearrange("p g d -> p (g d)"),
+                in_=x1g[:].rearrange("p g d t -> p (g d t)"),
+            )
+            nc.vector.quantize_mx(
+                out=wcod[:].bitcast(FP8X4),
+                scales=wsc[:],
+                in_=wg[:].rearrange("p n t -> p (n t)"),
+            )
+
             for c in range(N_CHUNKS):
-                hc = hnat[c]
+                hc = hpool.tile([P, A, N_EDGES], BF16, name="hc")
+                nc.sync.dma_start(
+                    out=hc[:],
+                    in_=incidence_1[c * CHUNK : (c + 1) * CHUNK, :].rearrange(
+                        "(p a) e -> p a e", a=A
+                    ),
+                )
                 for j in range(8):
                     col = (c * 8 + j) * NW
                     for a in range(A):
@@ -111,58 +136,43 @@ def tile_hypergraphgpslayer_pa_t_kernel(
                             start=(a == 0),
                             stop=(a == A - 1),
                         )
+                htg_w = (
+                    htg[c][:]
+                    .rearrange("p g n t -> p (g n t)")
+                    .bitcast(F32)
+                    .rearrange("p (g n u) -> p g n u", g=2, n=CHUNK, u=2)
+                )
+                for a in range(A):
+                    tp = psum.tile([P, 4, P], F32, tag="pa", bufs=3, name="tp")
+                    hw = hc[:, a, :].bitcast(F32)
+                    for wb in range(4):
+                        nc.tensor.transpose(tp[:, wb, :], hw[:, P * wb : P * wb + P], ident[:])
+                    nc.scalar.copy(
+                        out=htg_w[:, :, P * a : P * a + P, :],
+                        in_=tp[:].rearrange("p (g u) n -> p g n u", g=2),
+                    )
+                width = N_EDGES // 2
+                src = hc
+                while width >= 32:
+                    dst = tree.tile([P, A, width], BF16, name="tr%d" % width)
+                    nc.vector.tensor_tensor(
+                        out=dst[:], in0=src[:, :, 0:width], in1=src[:, :, width : 2 * width], op=ALU.add
+                    )
+                    src = dst
+                    width //= 2
                 dv = small.tile([P, A], F32, name="dv")
-                if c % 3 == 2:
-                    for a in range(A):
-                        junk1 = tree.tile([P, N_EDGES], BF16, name="junk1")
-                        nc.scalar.activation(
-                            out=junk1[:], in_=hc[:, a, :], func=ACT.Copy, accum_out=dv[:, a : a + 1]
-                        )
-                else:
-                    width = N_EDGES // 2
-                    src = hc
-                    while width >= 32:
-                        dst = tree.tile([P, A, width], BF16, name="tr%d" % width)
-                        nc.vector.tensor_tensor(
-                            out=dst[:],
-                            in0=src[:, :, 0:width],
-                            in1=src[:, :, width : 2 * width],
-                            op=ALU.add,
-                        )
-                        src = dst
-                        width //= 2
-                    nc.vector.tensor_reduce(out=dv[:], in_=src[:], axis=AX.X, op=ALU.add)
-                dvm = small.tile([P, A], F32, name="dvm")
-                nc.vector.tensor_scalar_max(out=dvm[:], in0=dv[:], scalar1=1.0)
+                nc.vector.tensor_reduce(out=dv[:], in_=src[:], axis=AX.X, op=ALU.add)
+                nc.vector.tensor_scalar_max(out=dv[:], in0=dv[:], scalar1=1.0)
                 dvs = small.tile([P, A], F32, name="dvs")
-                nc.scalar.activation(out=dvs[:], in_=dvm[:], func=ACT.Sqrt)
-                nc.vector.reciprocal(out=av_all[:, A * c : A * c + A], in_=dvs[:])
-                if c == 1:
-                    bn_ps = psum.tile([P, DIM], F32, tag="pb", bufs=2, name="bn_ps")
-                    nc.tensor.matmul(
-                        out=bn_ps[:], lhsT=ones_m[:], rhs=vecs[:, 0, :], start=True, stop=True
+                nc.scalar.activation(out=dvs[:], in_=dv[:], func=ACT.Sqrt)
+                av = small.tile([P, A], F32, name="av")
+                nc.vector.reciprocal(out=av[:], in_=dvs[:])
+                ab_ps = psum.tile([P, A, P], F32, tag="pb", bufs=2, name="ab_ps")
+                for a in range(A):
+                    nc.tensor.transpose(
+                        ab_ps[:, a, :], av[:, a : a + 1].to_broadcast([P, P]), ident[:]
                     )
-                    nc.vector.tensor_scalar(
-                        out=c_bc[:], in0=bn_ps[:], scalar1=gcol[:], scalar2=None, op0=ALU.mult
-                    )
-                    nc.tensor.matmul(
-                        out=g_ps[:], lhsT=ones_m[:], rhs=vecs[:, 1, :], start=True, stop=True
-                    )
-                    be_ps = psum.tile([P, DIM], F32, tag="pb", bufs=2, name="be_ps")
-                    nc.tensor.matmul(
-                        out=be_ps[:], lhsT=ones_m[:], rhs=vecs[:, 2, :], start=True, stop=True
-                    )
-                    nc.scalar.copy(out=beta_bc[:], in_=be_ps[:])
-                    sel = []
-                    for h in range(2):
-                        for eo in range(2):
-                            s = const.tile([P, P], F32, name="sel%d%d" % (h, eo))
-                            nc.gpsimd.memset(s[:], 0.0)
-                            nc.gpsimd.tensor_copy(
-                                out=s[:, 64 * h : 64 * h + 64],
-                                in_=ident[:].rearrange("p (q e) -> p e q", e=2)[:, eo, :],
-                            )
-                            sel.append(s)
+                nc.scalar.copy(out=abc[c][:], in_=ab_ps[:].rearrange("p a n -> p (a n)"))
 
             de = small.tile([P, 8], F32, name="de")
             nc.vector.tensor_reduce(
@@ -194,71 +204,47 @@ def tile_hypergraphgpslayer_pa_t_kernel(
                 in_=b4_ps[:].rearrange("p e w -> p w e"),
             )
 
-        state = {}
+        work = ctx.enter_context(tc.tile_pool(name="work", bufs=2))
+        xyp = ctx.enter_context(tc.tile_pool(name="xyp", bufs=3))
+        for c in range(N_CHUNKS):
+            rows = slice(c * CHUNK, (c + 1) * CHUNK)
+            x0c = work.tile([P, A, DIM], BF16, name="x0c")
+            nc.sync.dma_start(out=x0c[:], in_=x_0[rows, :].rearrange("(p a) d -> p a d", a=A))
+            xy = xyp.tile([P, A, DIM], F32, name="xy")
+            nc.gpsimd.tensor_tensor(
+                out=xy[:],
+                in0=x0c[:],
+                in1=c_bc[:].unsqueeze(1).to_broadcast([P, A, DIM]),
+                op=ALU.add,
+            )
 
-        def stage_a(c):
-            ab_ps = psum.tile([P, A, P], F32, tag="pb", bufs=2, name="ab_ps")
-            for a in range(A):
-                col = A * c + a
-                nc.tensor.transpose(
-                    ab_ps[:, a, :], av_all[:, col : col + 1].to_broadcast([P, P]), ident[:]
-                )
-            abc = work.tile([P, CHUNK], F32, name="abc")
-            nc.scalar.copy(out=abc[:], in_=ab_ps[:].rearrange("p a n -> p (a n)"))
-            cp = work.tile([P, 2, 4, CHUNK], BF16, tag="cp", name="cp")
-            for i in range(8):
-                if i in GP_PLANES:
-                    nc.gpsimd.tensor_scalar(
-                        out=cp[:, i // 4, i % 4, :],
-                        in0=abc[:],
-                        scalar1=b4[:, i : i + 1],
-                        scalar2=0.0,
-                        op0=ALU.mult,
-                        op1=ALU.add,
-                    )
-                else:
+            cp = work.tile([P, 2, 4, CHUNK], BF16, name="cp")
+            for g in range(2):
+                for t in range(4):
                     nc.scalar.activation(
-                        out=cp[:, i // 4, i % 4, :],
-                        in_=abc[:],
+                        out=cp[:, g, t, :],
+                        in_=abc[c][:],
                         func=ACT.Copy,
-                        scale=b4[:, i : i + 1],
+                        scale=b4[:, 4 * g + t : 4 * g + t + 1],
                     )
-            hng = work.tile([P, 2, CHUNK, 4], BF16, tag="hng", name="hng", align_bytes=64)
-            for a in range(A):
-                cols = slice(P * a, P * a + P)
-                ht = psum.tile([P, 4, P], F32, tag="ht", bufs=2, name="ht")
-                hw = hnat[c][:, a, :].bitcast(F32)
-                for wb in range(4):
-                    nc.tensor.transpose(ht[:, wb, :], hw[:, P * wb : P * wb + P], ident[:])
-                ht_b = (
-                    ht[:]
-                    .rearrange("p w n -> p (w n)")
-                    .bitcast(BF16)
-                    .rearrange("p (w n e) -> p w n e", w=4, n=P, e=2)
+            for g in range(2):
+                nc.vector.tensor_tensor(
+                    out=htg[c][:, g],
+                    in0=htg[c][:, g],
+                    in1=cp[:, g].rearrange("p t n -> p n t"),
+                    op=ALU.mult,
                 )
-                for g in range(2):
-                    nc.vector.tensor_tensor(
-                        out=hng[:, g, cols, :].rearrange("p n (u e) -> p n u e", u=2),
-                        in0=ht_b[:, 2 * g : 2 * g + 2].rearrange("p u n e -> p n u e"),
-                        in1=cp[:, g, :, cols].rearrange("p (u e) n -> p n u e", u=2),
-                        op=ALU.mult,
-                    )
             hcod = work.tile([P, 2, CHUNK], U32, name="hcod", align_bytes=64)
             hsc = work.tile([P, 2, CHUNK], U8, name="hsc", align_bytes=64)
             nc.vector.quantize_mx(
                 out=hcod[:].rearrange("p g n -> p (g n)").bitcast(FP8X4),
                 scales=hsc[:].rearrange("p g n -> p (g n)"),
-                in_=hng[:].rearrange("p g n t -> p (g n t)"),
+                in_=htg[c][:].rearrange("p g n t -> p (g n t)"),
             )
-            state[c] = (hcod, hsc)
-
-        def stage_b(c):
-            hcod, hsc = state[c]
-            xy = xys[c]
-            msgg = work.tile([P, CHUNK, 4], BF16, tag="msgg", name="msgg", align_bytes=64)
+            msgg = work.tile([P, CHUNK, 4], BF16, name="msgg", align_bytes=64)
             for a in range(A):
                 cols = slice(P * a, P * a + P)
-                m1 = psum.tile([P, 4, P], F32, tag="m1", bufs=2, name="m1")
+                m1 = psum.tile([P, 4, P], F32, tag="pa", bufs=3, name="m1")
                 for tb in range(4):
                     for g in range(2):
                         nc.tensor.matmul_mx(
@@ -302,11 +288,6 @@ def tile_hypergraphgpslayer_pa_t_kernel(
                 )
             nm = small.tile([P, A], F32, name="nm")
             nc.vector.tensor_scalar_mul(out=nm[:], in0=sy[:], scalar1=-1.0 / DIM)
-            state[c] = nm
-
-        def stage_c(c):
-            nm = state[c]
-            xy = xys[c]
             ss = small.tile([P, A], F32, name="ss")
             for a in range(A):
                 junk = work.tile([P, DIM], BF16, name="junk")
@@ -326,58 +307,21 @@ def tile_hypergraphgpslayer_pa_t_kernel(
             nc.scalar.activation(out=sd[:], in_=vv[:], func=ACT.Sqrt)
             rs = small.tile([P, A], F32, name="rs")
             nc.vector.reciprocal(out=rs[:], in_=sd[:])
-            nmrs = small.tile([P, A], F32, name="nmrs")
-            nc.vector.tensor_tensor(out=nmrs[:], in0=nm[:], in1=rs[:], op=ALU.mult)
             for a in range(A):
-                nc.scalar.activation(
+                nc.vector.scalar_tensor_tensor(
                     out=xy[:, a, :],
-                    in_=xy[:, a, :],
-                    func=ACT.Identity,
-                    bias=nmrs[:, a : a + 1],
-                    scale=rs[:, a : a + 1],
+                    in0=xy[:, a, :],
+                    scalar=nm[:, a : a + 1],
+                    in1=g_ps[:],
+                    op0=ALU.add,
+                    op1=ALU.mult,
                 )
-            nc.vector.tensor_tensor(
-                out=xy[:],
-                in0=xy[:],
-                in1=g_ps[:].unsqueeze(1).to_broadcast([P, A, DIM]),
-                op=ALU.mult,
-            )
-            nc.gpsimd.tensor_tensor(
-                out=xy[:],
-                in0=xy[:],
-                in1=beta_bc[:].unsqueeze(1).to_broadcast([P, A, DIM]),
-                op=ALU.add,
-            )
-            nc.sync.dma_start(
-                out=out[c * CHUNK : (c + 1) * CHUNK, :].rearrange("(p a) d -> p a d", a=A),
-                in_=xy[:],
-            )
-
-        x1g = work.tile([P, 2, DIM, 4], BF16, tag="hng", name="x1g", align_bytes=64)
-        for g in range(2):
-            nc.vector.tensor_copy(
-                out=x1g[:, g], in_=x1raw[:, 4 * g : 4 * g + 4, :].rearrange("p t d -> p d t")
-            )
-        wg = work.tile([P, DIM, 4], BF16, tag="msgg", name="wg", align_bytes=64)
-        nc.vector.tensor_copy(out=wg[:], in_=wraw[:].rearrange("p t n -> p n t"))
-        nc.vector.quantize_mx(
-            out=x1cod[:].rearrange("p g d -> p (g d)").bitcast(FP8X4),
-            scales=x1sc[:].rearrange("p g d -> p (g d)"),
-            in_=x1g[:].rearrange("p g d t -> p (g d t)"),
-        )
-        nc.vector.quantize_mx(
-            out=wcod[:].bitcast(FP8X4),
-            scales=wsc[:],
-            in_=wg[:].rearrange("p n t -> p (n t)"),
-        )
-
-        residual(0)
-        stage_a(0)
-        for c in range(N_CHUNKS):
-            if c + 1 < N_CHUNKS:
-                residual(c + 1)
-                stage_a(c + 1)
-            stage_b(c)
-            if c >= 1:
-                stage_c(c - 1)
-        stage_c(N_CHUNKS - 1)
+                nc.vector.scalar_tensor_tensor(
+                    out=xy[:, a, :],
+                    in0=xy[:, a, :],
+                    scalar=rs[:, a : a + 1],
+                    in1=b_ps[:],
+                    op0=ALU.mult,
+                    op1=ALU.add,
+                )
+            nc.sync.dma_start(out=out[rows, :].rearrange("(p a) d -> p a d", a=A), in_=xy[:])

@@ -1,6 +1,5 @@
 from contextlib import ExitStack
 
-import concourse.bass as bass
 import concourse.mybir as mybir
 from concourse.masks import make_identity
 
@@ -34,36 +33,38 @@ def tile_hypergraphgpslayer_pa_t_kernel(
         const = ctx.enter_context(tc.tile_pool(name="const", bufs=1))
         keep = ctx.enter_context(tc.tile_pool(name="keep", bufs=1))
         small = ctx.enter_context(tc.tile_pool(name="small", bufs=4))
+        work = ctx.enter_context(tc.tile_pool(name="work", bufs=2))
         psum = ctx.enter_context(tc.psum_pool(name="psum", bufs=1))
 
-        ident = const.tile([P, P], F32)
-        make_identity(nc, ident[:])
         ones_w = const.tile([P, NW], BF16)
         nc.vector.memset(ones_w[:], 1.0)
         ones_m = const.tile([P, P], BF16)
         nc.vector.memset(ones_m[:], 1.0)
-        sel = []
-        for h in range(2):
-            for eo in range(2):
-                s = const.tile([P, P], F32, name="sel%d%d" % (h, eo))
-                nc.vector.memset(s[:], 0.0)
-                nc.vector.tensor_copy(
-                    out=s[:, 64 * h : 64 * h + 64],
-                    in_=ident[:].rearrange("p (q e) -> p e q", e=2)[:, eo, :],
-                )
-                sel.append(s)
+        ident = const.tile([P, P], F32)
+        make_identity(nc, ident[:])
+        ident_bf = const.tile([P, P], BF16)
+        make_identity(nc, ident_bf[:])
+        vecs = const.tile([P, 2, DIM], BF16)
+        nc.vector.memset(vecs[:], 0.0)
+        nc.scalar.dma_start(out=vecs[0:1, 0, :], in_=ln1_g.unsqueeze(0))
+        nc.scalar.dma_start(out=vecs[0:1, 1, :], in_=ln1_b.unsqueeze(0))
+        bn_rows = const.tile([P, P], BF16)
+        nc.vector.memset(bn_rows[:], 0.0)
+        nc.scalar.dma_start(out=bn_rows[0:4, :], in_=bn.rearrange("(r q) -> r q", q=P))
+        gt = const.tile([P, 1], BF16)
+        nc.scalar.dma_start(out=gt[:], in_=gate_local.partition_broadcast(P))
+        gcol = const.tile([P, 1], F32)
+        nc.scalar.activation(out=gcol[:], in_=gt[:], func=ACT.Tanh)
 
         x1cod = const.tile([P, 2, DIM], U32, align_bytes=64)
         x1sc = const.tile([P, 2, DIM], U8, align_bytes=64)
         wcod = const.tile([P, DIM], U32, align_bytes=64)
         wsc = const.tile([P, DIM], U8, align_bytes=64)
-        c_bc = const.tile([P, DIM], F32)
-        gcol = const.tile([P, 1], F32)
+        ccol = const.tile([P, 4], F32)
         b4 = const.tile([P, 8], F32)
 
         g_ps = psum.tile([P, DIM], F32, name="g_ps")
-        b_ps = psum.tile([P, DIM], F32, name="b_ps")
-        de_ps = psum.tile([P, DIM], F32, name="de_ps")
+        be_ps = psum.tile([P, DIM], F32, name="be_ps")
 
         htg = [
             keep.tile([P, 2, CHUNK, 4], BF16, name="htg%d" % c, align_bytes=64)
@@ -73,50 +74,8 @@ def tile_hypergraphgpslayer_pa_t_kernel(
 
         with ExitStack() as ph1:
             hpool = ph1.enter_context(tc.tile_pool(name="hpool", bufs=3))
-            setup = ph1.enter_context(tc.tile_pool(name="setup", bufs=1))
-            tree = ph1.enter_context(tc.tile_pool(name="tree", bufs=2))
-
-            x1raw = setup.tile([P, 8, DIM], BF16)
-            nc.sync.dma_start(
-                out=x1raw[:].rearrange("p (w e) d -> p w (e d)", e=2),
-                in_=x_1_new.rearrange("(w p e) d -> p w (e d)", w=4, p=P, e=2),
-            )
-            wraw = setup.tile([P, 4, DIM], BF16)
-            nc.sync.dma_start(out=wraw[:], in_=Wn.rearrange("(t p) n -> p t n", p=P))
-            vecs = setup.tile([P, 3, DIM], BF16)
-            nc.vector.memset(vecs[:], 0.0)
-            nc.scalar.dma_start(out=vecs[0:1, 0, :], in_=bn.unsqueeze(0))
-            nc.scalar.dma_start(out=vecs[0:1, 1, :], in_=ln1_g.unsqueeze(0))
-            nc.scalar.dma_start(out=vecs[0:1, 2, :], in_=ln1_b.unsqueeze(0))
-            gt = setup.tile([P, 1], BF16)
-            nc.scalar.dma_start(out=gt[:], in_=gate_local.partition_broadcast(P))
-            nc.scalar.activation(out=gcol[:], in_=gt[:], func=ACT.Tanh)
-
-            bn_ps = psum.tile([P, DIM], F32, tag="pb", bufs=2, name="bn_ps")
-            nc.tensor.matmul(out=bn_ps[:], lhsT=ones_m[:], rhs=vecs[:, 0, :], start=True, stop=True)
-            nc.tensor.matmul(out=g_ps[:], lhsT=ones_m[:], rhs=vecs[:, 1, :], start=True, stop=True)
-            nc.tensor.matmul(out=b_ps[:], lhsT=ones_m[:], rhs=vecs[:, 2, :], start=True, stop=True)
-            nc.vector.tensor_scalar(
-                out=c_bc[:], in0=bn_ps[:], scalar1=gcol[:], scalar2=None, op0=ALU.mult
-            )
-
-            x1g = setup.tile([P, 2, DIM, 4], BF16, align_bytes=64)
-            for g in range(2):
-                nc.vector.tensor_copy(
-                    out=x1g[:, g], in_=x1raw[:, 4 * g : 4 * g + 4, :].rearrange("p t d -> p d t")
-                )
-            wg = setup.tile([P, DIM, 4], BF16, align_bytes=64)
-            nc.vector.tensor_copy(out=wg[:], in_=wraw[:].rearrange("p t n -> p n t"))
-            nc.vector.quantize_mx(
-                out=x1cod[:].rearrange("p g d -> p (g d)").bitcast(FP8X4),
-                scales=x1sc[:].rearrange("p g d -> p (g d)"),
-                in_=x1g[:].rearrange("p g d t -> p (g d t)"),
-            )
-            nc.vector.quantize_mx(
-                out=wcod[:].bitcast(FP8X4),
-                scales=wsc[:],
-                in_=wg[:].rearrange("p n t -> p (n t)"),
-            )
+            tree = ph1.enter_context(tc.tile_pool(name="tree", bufs=1))
+            de_ps = psum.tile([P, DIM], F32, tag="pc", bufs=2, name="de_ps")
 
             for c in range(N_CHUNKS):
                 hc = hpool.tile([P, A, N_EDGES], BF16, name="hc")
@@ -143,7 +102,7 @@ def tile_hypergraphgpslayer_pa_t_kernel(
                     .rearrange("p (g n u) -> p g n u", g=2, n=CHUNK, u=2)
                 )
                 for a in range(A):
-                    tp = psum.tile([P, 4, P], F32, tag="pa", bufs=3, name="tp")
+                    tp = psum.tile([P, 4, P], F32, tag="pa", bufs=2, name="tp")
                     hw = hc[:, a, :].bitcast(F32)
                     for wb in range(4):
                         nc.tensor.transpose(tp[:, wb, :], hw[:, P * wb : P * wb + P], ident[:])
@@ -173,6 +132,36 @@ def tile_hypergraphgpslayer_pa_t_kernel(
                         ab_ps[:, a, :], av[:, a : a + 1].to_broadcast([P, P]), ident[:]
                     )
                 nc.scalar.copy(out=abc[c][:], in_=ab_ps[:].rearrange("p a n -> p (a n)"))
+                if c == 1:
+                    nc.tensor.matmul(
+                        out=g_ps[:], lhsT=ones_m[:], rhs=vecs[:, 0, :], start=True, stop=True
+                    )
+                    nc.tensor.matmul(
+                        out=be_ps[:], lhsT=ones_m[:], rhs=vecs[:, 1, :], start=True, stop=True
+                    )
+                    bnt_ps = psum.tile([P, P], BF16, tag="pb", bufs=2, name="bnt_ps")
+                    nc.tensor.transpose(bnt_ps[:], bn_rows[:], ident_bf[:])
+                    nc.vector.tensor_scalar(
+                        out=ccol[:], in0=bnt_ps[:, 0:4], scalar1=gcol[:], scalar2=None, op0=ALU.mult
+                    )
+                    sel = []
+                    for h in range(2):
+                        for eo in range(2):
+                            s = const.tile([P, P], F32, name="sel%d%d" % (h, eo))
+                            nc.gpsimd.memset(s[:], 0.0)
+                            nc.gpsimd.tensor_copy(
+                                out=s[:, 64 * h : 64 * h + 64],
+                                in_=ident[:].rearrange("p (q e) -> p e q", e=2)[:, eo, :],
+                            )
+                            sel.append(s)
+
+            x1raw = work.tile([P, 8, DIM], BF16, tag="cp", name="x1raw")
+            nc.sync.dma_start(
+                out=x1raw[:].rearrange("p (w e) d -> p w (e d)", e=2),
+                in_=x_1_new.rearrange("(w p e) d -> p w (e d)", w=4, p=P, e=2),
+            )
+            wraw = work.tile([P, 4, DIM], BF16, tag="msgg", name="wraw", align_bytes=64)
+            nc.sync.dma_start(out=wraw[:], in_=Wn.rearrange("(t p) n -> p t n", p=P))
 
             de = small.tile([P, 8], F32, name="de")
             nc.vector.tensor_reduce(
@@ -204,29 +193,48 @@ def tile_hypergraphgpslayer_pa_t_kernel(
                 in_=b4_ps[:].rearrange("p e w -> p w e"),
             )
 
-        work = ctx.enter_context(tc.tile_pool(name="work", bufs=2))
-        xyp = ctx.enter_context(tc.tile_pool(name="xyp", bufs=3))
+        late = ctx.enter_context(tc.tile_pool(name="late", bufs=2))
+
+        def scale_planes(c):
+            cp = work.tile([P, 2, 4, CHUNK], BF16, tag="cp", name="cp")
+            for i in range(8):
+                nc.gpsimd.tensor_scalar(
+                    out=cp[:, i // 4, i % 4, :],
+                    in0=abc[c][:],
+                    scalar1=b4[:, i : i + 1],
+                    scalar2=0.0,
+                    op0=ALU.mult,
+                    op1=ALU.add,
+                )
+            return cp
+
+        cps = {0: scale_planes(0)}
+
+        x1g = late.tile([P, 2, DIM, 4], BF16, tag="vt", name="x1g", align_bytes=64)
+        for g in range(2):
+            nc.vector.tensor_copy(
+                out=x1g[:, g], in_=x1raw[:, 4 * g : 4 * g + 4, :].rearrange("p t d -> p d t")
+            )
+        wg = work.tile([P, DIM, 4], BF16, tag="msgg", name="wg", align_bytes=64)
+        nc.vector.tensor_copy(out=wg[:], in_=wraw[:].rearrange("p t n -> p n t"))
+        nc.vector.quantize_mx(
+            out=x1cod[:].rearrange("p g d -> p (g d)").bitcast(FP8X4),
+            scales=x1sc[:].rearrange("p g d -> p (g d)"),
+            in_=x1g[:].rearrange("p g d t -> p (g d t)"),
+        )
+        nc.vector.quantize_mx(
+            out=wcod[:].bitcast(FP8X4),
+            scales=wsc[:],
+            in_=wg[:].rearrange("p n t -> p (n t)"),
+        )
+
         for c in range(N_CHUNKS):
             rows = slice(c * CHUNK, (c + 1) * CHUNK)
-            x0c = work.tile([P, A, DIM], BF16, name="x0c")
+            x0c = late.tile([P, A, DIM], BF16, name="x0c", bufs=3)
             nc.sync.dma_start(out=x0c[:], in_=x_0[rows, :].rearrange("(p a) d -> p a d", a=A))
-            xy = xyp.tile([P, A, DIM], F32, name="xy")
-            nc.gpsimd.tensor_tensor(
-                out=xy[:],
-                in0=x0c[:],
-                in1=c_bc[:].unsqueeze(1).to_broadcast([P, A, DIM]),
-                op=ALU.add,
-            )
-
-            cp = work.tile([P, 2, 4, CHUNK], BF16, name="cp")
-            for g in range(2):
-                for t in range(4):
-                    nc.scalar.activation(
-                        out=cp[:, g, t, :],
-                        in_=abc[c][:],
-                        func=ACT.Copy,
-                        scale=b4[:, 4 * g + t : 4 * g + t + 1],
-                    )
+            cp = cps[c]
+            if c + 1 < N_CHUNKS:
+                cps[c + 1] = scale_planes(c + 1)
             for g in range(2):
                 nc.vector.tensor_tensor(
                     out=htg[c][:, g],
@@ -241,10 +249,10 @@ def tile_hypergraphgpslayer_pa_t_kernel(
                 scales=hsc[:].rearrange("p g n -> p (g n)"),
                 in_=htg[c][:].rearrange("p g n t -> p (g n t)"),
             )
-            msgg = work.tile([P, CHUNK, 4], BF16, name="msgg", align_bytes=64)
+            msgg = work.tile([P, CHUNK, 4], BF16, tag="msgg", name="msgg", align_bytes=64)
             for a in range(A):
                 cols = slice(P * a, P * a + P)
-                m1 = psum.tile([P, 4, P], F32, tag="pa", bufs=3, name="m1")
+                m1 = psum.tile([P, 4, P], F32, tag="pc", bufs=2, name="m1")
                 for tb in range(4):
                     for g in range(2):
                         nc.tensor.matmul_mx(
@@ -264,36 +272,57 @@ def tile_hypergraphgpslayer_pa_t_kernel(
                 scales=msc[:],
                 in_=msgg[:].rearrange("p n t -> p (n t)"),
             )
-            sy = small.tile([P, A], F32, name="sy")
-            for a in range(A):
-                cols = slice(P * a, P * a + P)
-                m2 = psum.tile([P, DIM], F32, tag="pb", bufs=2, name="m2")
+            vt = late.tile([P, 4, CHUNK], F32, tag="vt", name="vt", align_bytes=64)
+            for db in range(4):
+                u_ps = psum.tile([P, CHUNK], F32, tag="pb", bufs=2, name="u_ps")
                 nc.tensor.matmul_mx(
-                    out=m2[:],
-                    lhsT=mcod[:, cols].bitcast(FP8X4),
-                    lhsT_scale=msc[:, cols],
-                    rhs=wcod[:].bitcast(FP8X4),
-                    rhs_scale=wsc[:],
+                    out=u_ps[:],
+                    lhsT=wcod[:, P * db : P * db + P].bitcast(FP8X4),
+                    lhsT_scale=wsc[:, P * db : P * db + P],
+                    rhs=mcod[:].bitcast(FP8X4),
+                    rhs_scale=msc[:],
                     start=True,
                     stop=True,
                 )
-                nc.vector.scalar_tensor_tensor(
-                    out=xy[:, a, :],
-                    in0=m2[:],
-                    scalar=gcol[:],
-                    in1=xy[:, a, :],
-                    op0=ALU.mult,
-                    op1=ALU.add,
-                    accum_out=sy[:, a : a + 1],
+                nc.scalar.activation(
+                    out=vt[:, db, :],
+                    in_=u_ps[:],
+                    func=ACT.Identity,
+                    bias=ccol[:, db : db + 1],
+                    scale=gcol[:],
                 )
+            y = late.tile([P, A, DIM], F32, name="y")
+            sy = small.tile([P, A], F32, name="sy")
             nm = small.tile([P, A], F32, name="nm")
-            nc.vector.tensor_scalar_mul(out=nm[:], in0=sy[:], scalar1=-1.0 / DIM)
             ss = small.tile([P, A], F32, name="ss")
+            for a in range(A):
+                y_ps = psum.tile([P, DIM], F32, tag="pa", bufs=2, name="y_ps")
+                for db in range(4):
+                    dcols = slice(P * db, P * db + P)
+                    nc.tensor.matmul(
+                        out=y_ps[:, dcols],
+                        lhsT=vt[:, db, P * a : P * a + P],
+                        rhs=ident[:],
+                        is_transpose=True,
+                        start=True,
+                        stop=False,
+                    )
+                    nc.tensor.matmul(
+                        out=y_ps[:, dcols],
+                        lhsT=ident_bf[:],
+                        rhs=x0c[:, a, dcols],
+                        start=False,
+                        stop=True,
+                    )
+                nc.scalar.activation(
+                    out=y[:, a, :], in_=y_ps[:], func=ACT.Copy, accum_out=sy[:, a : a + 1]
+                )
+            nc.vector.tensor_scalar_mul(out=nm[:], in0=sy[:], scalar1=-1.0 / DIM)
             for a in range(A):
                 junk = work.tile([P, DIM], BF16, name="junk")
                 nc.scalar.activation(
                     out=junk[:],
-                    in_=xy[:, a, :],
+                    in_=y[:, a, :],
                     func=ACT.Square,
                     bias=nm[:, a : a + 1],
                     scale=1.0,
@@ -309,19 +338,19 @@ def tile_hypergraphgpslayer_pa_t_kernel(
             nc.vector.reciprocal(out=rs[:], in_=sd[:])
             for a in range(A):
                 nc.vector.scalar_tensor_tensor(
-                    out=xy[:, a, :],
-                    in0=xy[:, a, :],
+                    out=y[:, a, :],
+                    in0=y[:, a, :],
                     scalar=nm[:, a : a + 1],
                     in1=g_ps[:],
                     op0=ALU.add,
                     op1=ALU.mult,
                 )
                 nc.vector.scalar_tensor_tensor(
-                    out=xy[:, a, :],
-                    in0=xy[:, a, :],
+                    out=y[:, a, :],
+                    in0=y[:, a, :],
                     scalar=rs[:, a : a + 1],
-                    in1=b_ps[:],
+                    in1=be_ps[:],
                     op0=ALU.mult,
                     op1=ALU.add,
                 )
-            nc.sync.dma_start(out=out[rows, :].rearrange("(p a) d -> p a d", a=A), in_=xy[:])
+            nc.sync.dma_start(out=out[rows, :].rearrange("(p a) d -> p a d", a=A), in_=y[:])

@@ -23,6 +23,7 @@ CHUNK = P * A
 N_CHUNKS = N_NODES // CHUNK
 LN_EPS = 1e-5
 NW = 2
+SCALAR_PLANES = (0, 1, 2)
 
 
 def tile_hypergraphgpslayer_pa_t_kernel(
@@ -198,14 +199,21 @@ def tile_hypergraphgpslayer_pa_t_kernel(
         def scale_planes(c):
             cp = work.tile([P, 2, 4, CHUNK], BF16, tag="cp", name="cp")
             for i in range(8):
-                nc.gpsimd.tensor_scalar(
-                    out=cp[:, i // 4, i % 4, :],
-                    in0=abc[c][:],
-                    scalar1=b4[:, i : i + 1],
-                    scalar2=0.0,
-                    op0=ALU.mult,
-                    op1=ALU.add,
-                )
+                if i in SCALAR_PLANES:
+                    nc.scalar.activation(
+                        out=cp[:, i // 4, i % 4, :],
+                        in_=abc[c][:],
+                        func=ACT.Copy,
+                        scale=b4[:, i : i + 1],
+                    )
+                else:
+                    nc.vector.tensor_scalar(
+                        out=cp[:, i // 4, i % 4, :],
+                        in0=abc[c][:],
+                        scalar1=b4[:, i : i + 1],
+                        scalar2=None,
+                        op0=ALU.mult,
+                    )
             return cp
 
         cps = {0: scale_planes(0)}

@@ -24,6 +24,8 @@ N_CHUNKS = N_NODES // CHUNK
 LN_EPS = 1e-5
 NW = 2
 SCALAR_PLANES = (0, 1, 2)
+ROWS_EARLY = 11
+TR_EARLY = 8
 
 
 def tile_hypergraphgpslayer_pa_t_kernel(
@@ -32,6 +34,7 @@ def tile_hypergraphgpslayer_pa_t_kernel(
     nc = tc.nc
     with ExitStack() as ctx:
         const = ctx.enter_context(tc.tile_pool(name="const", bufs=1))
+        big = ctx.enter_context(tc.tile_pool(name="big", bufs=1))
         keep = ctx.enter_context(tc.tile_pool(name="keep", bufs=1))
         small = ctx.enter_context(tc.tile_pool(name="small", bufs=4))
         work = ctx.enter_context(tc.tile_pool(name="work", bufs=2))
@@ -41,10 +44,22 @@ def tile_hypergraphgpslayer_pa_t_kernel(
         nc.vector.memset(ones_w[:], 1.0)
         ones_m = const.tile([P, P], BF16)
         nc.vector.memset(ones_m[:], 1.0)
+        mhalf = const.tile([P, 8], F32)
+        nc.vector.memset(mhalf[:], -0.5)
         ident = const.tile([P, P], F32)
         make_identity(nc, ident[:])
         ident_bf = const.tile([P, P], BF16)
         make_identity(nc, ident_bf[:])
+        sel = []
+        for h in range(2):
+            for eo in range(2):
+                s = const.tile([P, P], F32, name="sel%d%d" % (h, eo))
+                nc.gpsimd.memset(s[:], 0.0)
+                nc.gpsimd.tensor_copy(
+                    out=s[:, 64 * h : 64 * h + 64],
+                    in_=ident[:].rearrange("p (q e) -> p e q", e=2)[:, eo, :],
+                )
+                sel.append(s)
         vecs = const.tile([P, 2, DIM], BF16)
         nc.vector.memset(vecs[:], 0.0)
         nc.scalar.dma_start(out=vecs[0:1, 0, :], in_=ln1_g.unsqueeze(0))
@@ -56,198 +71,204 @@ def tile_hypergraphgpslayer_pa_t_kernel(
         nc.scalar.dma_start(out=gt[:], in_=gate_local.partition_broadcast(P))
         gcol = const.tile([P, 1], F32)
         nc.scalar.activation(out=gcol[:], in_=gt[:], func=ACT.Tanh)
+        ccol = const.tile([P, 4], F32)
+        bnt_ps = psum.tile([P, P], BF16, tag="pe", name="bnt_ps")
+        nc.tensor.transpose(bnt_ps[:], bn_rows[:], ident_bf[:])
+        nc.vector.tensor_scalar(
+            out=ccol[:], in0=bnt_ps[:, 0:4], scalar1=gcol[:], scalar2=None, op0=ALU.mult
+        )
 
         x1cod = const.tile([P, 2, DIM], U32, align_bytes=64)
         x1sc = const.tile([P, 2, DIM], U8, align_bytes=64)
         wcod = const.tile([P, DIM], U32, align_bytes=64)
         wsc = const.tile([P, DIM], U8, align_bytes=64)
-        ccol = const.tile([P, 4], F32)
         b4 = const.tile([P, 8], F32)
 
-        g_ps = psum.tile([P, DIM], F32, name="g_ps")
-        be_ps = psum.tile([P, DIM], F32, name="be_ps")
-
-        htg = [
-            keep.tile([P, 2, CHUNK, 4], BF16, name="htg%d" % c, align_bytes=64)
-            for c in range(N_CHUNKS)
-        ]
-        abc = [keep.tile([P, CHUNK], F32, name="abc%d" % c) for c in range(N_CHUNKS)]
-
-        with ExitStack() as ph1:
-            hpool = ph1.enter_context(tc.tile_pool(name="hpool", bufs=3))
-            tree = ph1.enter_context(tc.tile_pool(name="tree", bufs=1))
-            de_ps = psum.tile([P, DIM], F32, tag="pc", bufs=2, name="de_ps")
-
-            for c in range(N_CHUNKS):
-                hc = hpool.tile([P, A, N_EDGES], BF16, name="hc")
-                nc.sync.dma_start(
-                    out=hc[:],
-                    in_=incidence_1[c * CHUNK : (c + 1) * CHUNK, :].rearrange(
-                        "(p a) e -> p a e", a=A
-                    ),
-                )
-                for j in range(8):
-                    col = (c * 8 + j) * NW
-                    for a in range(A):
-                        nc.tensor.matmul(
-                            out=de_ps[:, col : col + NW],
-                            lhsT=hc[:, a, P * j : P * j + P],
-                            rhs=ones_w[:],
-                            start=(a == 0),
-                            stop=(a == A - 1),
-                        )
-                htg_w = (
-                    htg[c][:]
-                    .rearrange("p g n t -> p (g n t)")
-                    .bitcast(F32)
-                    .rearrange("p (g n u) -> p g n u", g=2, n=CHUNK, u=2)
-                )
-                for a in range(A):
-                    tp = psum.tile([P, 4, P], F32, tag="pa", bufs=2, name="tp")
-                    hw = hc[:, a, :].bitcast(F32)
-                    for wb in range(4):
-                        nc.tensor.transpose(tp[:, wb, :], hw[:, P * wb : P * wb + P], ident[:])
-                    nc.scalar.copy(
-                        out=htg_w[:, :, P * a : P * a + P, :],
-                        in_=tp[:].rearrange("p (g u) n -> p g n u", g=2),
-                    )
-                width = N_EDGES // 2
-                src = hc
-                while width >= 32:
-                    dst = tree.tile([P, A, width], BF16, name="tr%d" % width)
-                    nc.vector.tensor_tensor(
-                        out=dst[:], in0=src[:, :, 0:width], in1=src[:, :, width : 2 * width], op=ALU.add
-                    )
-                    src = dst
-                    width //= 2
-                dv = small.tile([P, A], F32, name="dv")
-                nc.vector.tensor_reduce(out=dv[:], in_=src[:], axis=AX.X, op=ALU.add)
-                nc.vector.tensor_scalar_max(out=dv[:], in0=dv[:], scalar1=1.0)
-                dvs = small.tile([P, A], F32, name="dvs")
-                nc.scalar.activation(out=dvs[:], in_=dv[:], func=ACT.Sqrt)
-                av = small.tile([P, A], F32, name="av")
-                nc.vector.reciprocal(out=av[:], in_=dvs[:])
-                ab_ps = psum.tile([P, A, P], F32, tag="pb", bufs=2, name="ab_ps")
-                for a in range(A):
-                    nc.tensor.transpose(
-                        ab_ps[:, a, :], av[:, a : a + 1].to_broadcast([P, P]), ident[:]
-                    )
-                nc.scalar.copy(out=abc[c][:], in_=ab_ps[:].rearrange("p a n -> p (a n)"))
-                if c == 1:
-                    nc.tensor.matmul(
-                        out=g_ps[:], lhsT=ones_m[:], rhs=vecs[:, 0, :], start=True, stop=True
-                    )
-                    nc.tensor.matmul(
-                        out=be_ps[:], lhsT=ones_m[:], rhs=vecs[:, 1, :], start=True, stop=True
-                    )
-                    bnt_ps = psum.tile([P, P], BF16, tag="pb", bufs=2, name="bnt_ps")
-                    nc.tensor.transpose(bnt_ps[:], bn_rows[:], ident_bf[:])
-                    nc.vector.tensor_scalar(
-                        out=ccol[:], in0=bnt_ps[:, 0:4], scalar1=gcol[:], scalar2=None, op0=ALU.mult
-                    )
-                    sel = []
-                    for h in range(2):
-                        for eo in range(2):
-                            s = const.tile([P, P], F32, name="sel%d%d" % (h, eo))
-                            nc.gpsimd.memset(s[:], 0.0)
-                            nc.gpsimd.tensor_copy(
-                                out=s[:, 64 * h : 64 * h + 64],
-                                in_=ident[:].rearrange("p (q e) -> p e q", e=2)[:, eo, :],
-                            )
-                            sel.append(s)
-
-            x1raw = work.tile([P, 8, DIM], BF16, tag="cp", name="x1raw")
-            nc.sync.dma_start(
-                out=x1raw[:].rearrange("p (w e) d -> p w (e d)", e=2),
-                in_=x_1_new.rearrange("(w p e) d -> p w (e d)", w=4, p=P, e=2),
-            )
-            wraw = work.tile([P, 4, DIM], BF16, tag="msgg", name="wraw", align_bytes=64)
-            nc.sync.dma_start(out=wraw[:], in_=Wn.rearrange("(t p) n -> p t n", p=P))
-
-            de = small.tile([P, 8], F32, name="de")
-            nc.vector.tensor_reduce(
-                out=de[:],
-                in_=de_ps[:, 0 : N_CHUNKS * 8 * NW].rearrange(
-                    "p (c j w) -> p j c w", c=N_CHUNKS, j=8, w=NW
-                )[:, :, :, 0],
-                axis=AX.X,
-                op=ALU.add,
-            )
-            nc.vector.tensor_scalar_max(out=de[:], in0=de[:], scalar1=1.0)
-            des = small.tile([P, 8], F32, name="des")
-            nc.scalar.activation(out=des[:], in_=de[:], func=ACT.Sqrt)
-            bnat = small.tile([P, 8], F32, name="bnat")
-            nc.vector.reciprocal(out=bnat[:], in_=des[:])
-            bnat_v = bnat[:].rearrange("p (w h) -> p h w", h=2)
-            b4_ps = psum.tile([P, 2, 4], F32, tag="pb", bufs=2, name="b4_ps")
-            for eo in range(2):
-                for h in range(2):
-                    nc.tensor.matmul(
-                        out=b4_ps[:, eo, :],
-                        lhsT=sel[2 * h + eo][:],
-                        rhs=bnat_v[:, h, :],
-                        start=(h == 0),
-                        stop=(h == 1),
-                    )
-            nc.vector.tensor_copy(
-                out=b4[:].rearrange("p (w e) -> p w e", e=2),
-                in_=b4_ps[:].rearrange("p e w -> p w e"),
-            )
-
-        late = ctx.enter_context(tc.tile_pool(name="late", bufs=2))
-
-        def scale_planes(c):
-            cp = work.tile([P, 2, 4, CHUNK], BF16, tag="cp", name="cp")
-            for i in range(8):
-                if i in SCALAR_PLANES:
-                    nc.scalar.activation(
-                        out=cp[:, i // 4, i % 4, :],
-                        in_=abc[c][:],
-                        func=ACT.Copy,
-                        scale=b4[:, i : i + 1],
-                    )
-                else:
-                    nc.vector.tensor_scalar(
-                        out=cp[:, i // 4, i % 4, :],
-                        in0=abc[c][:],
-                        scalar1=b4[:, i : i + 1],
-                        scalar2=None,
-                        op0=ALU.mult,
-                    )
-            return cp
-
-        cps = {0: scale_planes(0)}
-
-        x1g = late.tile([P, 2, DIM, 4], BF16, tag="vt", name="x1g", align_bytes=64)
-        for g in range(2):
-            nc.vector.tensor_copy(
-                out=x1g[:, g], in_=x1raw[:, 4 * g : 4 * g + 4, :].rearrange("p t d -> p d t")
-            )
-        wg = work.tile([P, DIM, 4], BF16, tag="msgg", name="wg", align_bytes=64)
-        nc.vector.tensor_copy(out=wg[:], in_=wraw[:].rearrange("p t n -> p n t"))
-        nc.vector.quantize_mx(
-            out=x1cod[:].rearrange("p g d -> p (g d)").bitcast(FP8X4),
-            scales=x1sc[:].rearrange("p g d -> p (g d)"),
-            in_=x1g[:].rearrange("p g d t -> p (g d t)"),
-        )
-        nc.vector.quantize_mx(
-            out=wcod[:].bitcast(FP8X4),
-            scales=wsc[:],
-            in_=wg[:].rearrange("p n t -> p (n t)"),
-        )
-
+        hc = []
         for c in range(N_CHUNKS):
-            rows = slice(c * CHUNK, (c + 1) * CHUNK)
-            x0c = late.tile([P, A, DIM], BF16, name="x0c", bufs=3)
-            nc.sync.dma_start(out=x0c[:], in_=x_0[rows, :].rearrange("(p a) d -> p a d", a=A))
-            cp = cps[c]
-            if c + 1 < N_CHUNKS:
-                cps[c + 1] = scale_planes(c + 1)
+            t = big.tile([P, A, N_EDGES], BF16, tag="big%d" % c, name="hc%d" % c, align_bytes=64)
+            nc.sync.dma_start(
+                out=t[:],
+                in_=incidence_1[c * CHUNK : (c + 1) * CHUNK, :].rearrange("(p a) e -> p a e", a=A),
+            )
+            hc.append(t)
+        x1raw = work.tile([P, 8, DIM], BF16, tag="cp", name="x1raw")
+        nc.sync.dma_start(
+            out=x1raw[:].rearrange("p (w e) d -> p w (e d)", e=2),
+            in_=x_1_new.rearrange("(w p e) d -> p w (e d)", w=4, p=P, e=2),
+        )
+        wraw = work.tile([P, 4, DIM], BF16, tag="msgg", name="wraw", align_bytes=64)
+        nc.sync.dma_start(out=wraw[:], in_=Wn.rearrange("(t p) n -> p t n", p=P))
+
+        x0cs = {}
+
+        def load_x0(c):
+            if c < N_CHUNKS:
+                t = work.tile([P, A, DIM], BF16, name="x0c", bufs=3)
+                nc.sync.dma_start(
+                    out=t[:],
+                    in_=x_0[c * CHUNK : (c + 1) * CHUNK, :].rearrange("(p a) d -> p a d", a=A),
+                )
+                x0cs[c] = t
+
+        load_x0(0)
+        load_x0(1)
+
+        de_ps = psum.tile([P, DIM], F32, tag="pd", name="de_ps")
+        htg = {}
+        tps = {}
+        avs = {}
+        abc = {}
+
+        def col_sums(c):
+            for j in range(8):
+                col = (c * 8 + j) * NW
+                for a in range(A):
+                    nc.tensor.matmul(
+                        out=de_ps[:, col : col + NW],
+                        lhsT=hc[c][:, a, P * j : P * j + P],
+                        rhs=ones_w[:],
+                        start=(a == 0),
+                        stop=(a == A - 1),
+                    )
+
+        def row_sums(c):
+            dv = small.tile([P, A], F32, name="dv")
+            for a in range(A):
+                junk1 = work.tile([P, N_EDGES], BF16, name="junk1")
+                nc.vector.tensor_scalar(
+                    out=junk1[:],
+                    in0=hc[c][:, a, :],
+                    scalar1=1.0,
+                    scalar2=None,
+                    op0=ALU.mult,
+                    op1=ALU.add,
+                    accum_out=dv[:, a : a + 1],
+                )
+            dvm = small.tile([P, A], F32, name="dvm")
+            nc.vector.tensor_scalar_max(out=dvm[:], in0=dv[:], scalar1=1.0)
+            av = small.tile([P, A], F32, name="av", bufs=N_CHUNKS)
+            nc.gpsimd.tensor_tensor(out=av[:], in0=dvm[:], in1=mhalf[:, 0:A], op=ALU.pow)
+            avs[c] = av
+
+        def transposes(c):
+            tps[c] = []
+            for a in range(A):
+                q = (A * c + a) % 6
+                tp = psum.tile([P, 4, P], F32, tag=("pa", "pb", "pc")[q // 2], bufs=2, name="tp")
+                hw = hc[c][:, a, :].bitcast(F32)
+                for wb in range(4):
+                    nc.tensor.transpose(tp[:, wb, :], hw[:, P * wb : P * wb + P], ident[:])
+                tps[c].append(tp)
+
+        def exits(c):
+            t = big.tile([P, 2, CHUNK, 4], BF16, tag="big%d" % c, name="htg%d" % c, align_bytes=64)
+            htg[c] = t
+            t_w = (
+                t[:]
+                .rearrange("p g n t -> p (g n t)")
+                .bitcast(F32)
+                .rearrange("p (g n u) -> p g n u", g=2, n=CHUNK, u=2)
+            )
+            for a in range(A):
+                nc.scalar.copy(
+                    out=t_w[:, :, P * a : P * a + P, :],
+                    in_=tps[c][a][:].rearrange("p (g u) n -> p g n u", g=2),
+                )
+
+        def spread_a(c):
+            ab_ps = psum.tile([P, A, P], F32, tag="pe", name="ab_ps")
+            for a in range(A):
+                nc.tensor.transpose(
+                    ab_ps[:, a, :], avs[c][:, a : a + 1].to_broadcast([P, P]), ident[:]
+                )
+            t = keep.tile([P, CHUNK], F32, name="abc%d" % c)
+            nc.scalar.copy(out=t[:], in_=ab_ps[:].rearrange("p a n -> p (a n)"))
+            abc[c] = t
+
+        n_tr = 0
+        for c in range(N_CHUNKS):
+            col_sums(c)
+            if c < ROWS_EARLY:
+                row_sums(c)
+            if c >= 1 and n_tr < TR_EARLY:
+                transposes(n_tr)
+                exits(n_tr)
+                n_tr += 1
+            if c == 8:
+                for z in range(3):
+                    spread_a(z)
+
+        de = small.tile([P, 8], F32, name="de")
+        nc.vector.tensor_reduce(
+            out=de[:],
+            in_=de_ps[:, 0 : N_CHUNKS * 8 * NW].rearrange(
+                "p (c j w) -> p j c w", c=N_CHUNKS, j=8, w=NW
+            )[:, :, :, 0],
+            axis=AX.X,
+            op=ALU.add,
+        )
+        dem = small.tile([P, 8], F32, name="dem")
+        nc.vector.tensor_scalar_max(out=dem[:], in0=de[:], scalar1=1.0)
+        bnat = small.tile([P, 8], F32, name="bnat")
+        nc.gpsimd.tensor_tensor(out=bnat[:], in0=dem[:], in1=mhalf[:], op=ALU.pow)
+        bnat_v = bnat[:].rearrange("p (w h) -> p h w", h=2)
+        b4_ps = psum.tile([P, 2, 4], F32, tag="pe", name="b4_ps")
+        for eo in range(2):
+            for h in range(2):
+                nc.tensor.matmul(
+                    out=b4_ps[:, eo, :],
+                    lhsT=sel[2 * h + eo][:],
+                    rhs=bnat_v[:, h, :],
+                    start=(h == 0),
+                    stop=(h == 1),
+                )
+        nc.vector.tensor_copy(
+            out=b4[:].rearrange("p (w e) -> p w e", e=2),
+            in_=b4_ps[:].rearrange("p e w -> p w e"),
+        )
+
+        cps = {}
+        hq = {}
+        msgs = {}
+        mq = {}
+        vts = {}
+        ys = {}
+        stat = {}
+
+        def plane(c, i):
+            if c not in cps:
+                cps[c] = work.tile([P, 2, 4, CHUNK], BF16, tag="cp", name="cp")
+            if i in SCALAR_PLANES:
+                nc.scalar.activation(
+                    out=cps[c][:, i // 4, i % 4, :],
+                    in_=abc[c][:],
+                    func=ACT.Copy,
+                    scale=b4[:, i : i + 1],
+                )
+            else:
+                nc.vector.tensor_scalar(
+                    out=cps[c][:, i // 4, i % 4, :],
+                    in0=abc[c][:],
+                    scalar1=b4[:, i : i + 1],
+                    scalar2=None,
+                    op0=ALU.mult,
+                )
+
+        def planes(c, on_scalar):
+            if c < N_CHUNKS:
+                for i in range(8):
+                    if (i in SCALAR_PLANES) == on_scalar:
+                        plane(c, i)
+
+        def mask_quant(c):
+            if c >= N_CHUNKS:
+                return
             for g in range(2):
                 nc.vector.tensor_tensor(
                     out=htg[c][:, g],
                     in0=htg[c][:, g],
-                    in1=cp[:, g].rearrange("p t n -> p n t"),
+                    in1=cps[c][:, g].rearrange("p t n -> p n t"),
                     op=ALU.mult,
                 )
             hcod = work.tile([P, 2, CHUNK], U32, name="hcod", align_bytes=64)
@@ -257,6 +278,12 @@ def tile_hypergraphgpslayer_pa_t_kernel(
                 scales=hsc[:].rearrange("p g n -> p (g n)"),
                 in_=htg[c][:].rearrange("p g n t -> p (g n t)"),
             )
+            hq[c] = (hcod, hsc)
+
+        def first_product(c):
+            if c >= N_CHUNKS:
+                return
+            hcod, hsc = hq[c]
             msgg = work.tile([P, CHUNK, 4], BF16, tag="msgg", name="msgg", align_bytes=64)
             for a in range(A):
                 cols = slice(P * a, P * a + P)
@@ -273,14 +300,19 @@ def tile_hypergraphgpslayer_pa_t_kernel(
                             stop=(g == 1),
                         )
                 nc.scalar.copy(out=msgg[:, cols, :], in_=m1[:].rearrange("p t n -> p n t"))
+            msgs[c] = msgg
+
+        def second_product(c):
+            if c < 0 or c >= N_CHUNKS:
+                return
             mcod = work.tile([P, CHUNK], U32, name="mcod", align_bytes=64)
             msc = work.tile([P, CHUNK], U8, name="msc", align_bytes=64)
             nc.vector.quantize_mx(
                 out=mcod[:].bitcast(FP8X4),
                 scales=msc[:],
-                in_=msgg[:].rearrange("p n t -> p (n t)"),
+                in_=msgs[c][:].rearrange("p n t -> p (n t)"),
             )
-            vt = late.tile([P, 4, CHUNK], F32, tag="vt", name="vt", align_bytes=64)
+            vt = work.tile([P, 4, CHUNK], F32, tag="vt", name="vt", align_bytes=64)
             for db in range(4):
                 u_ps = psum.tile([P, CHUNK], F32, tag="pb", bufs=2, name="u_ps")
                 nc.tensor.matmul_mx(
@@ -299,17 +331,20 @@ def tile_hypergraphgpslayer_pa_t_kernel(
                     bias=ccol[:, db : db + 1],
                     scale=gcol[:],
                 )
-            y = late.tile([P, A, DIM], F32, name="y")
+            vts[c] = vt
+
+        def residual(c):
+            if c < 0 or c >= N_CHUNKS:
+                return
+            y = big.tile([P, A, DIM], F32, tag="big%d" % c, name="y%d" % c, align_bytes=64)
             sy = small.tile([P, A], F32, name="sy")
-            nm = small.tile([P, A], F32, name="nm")
-            ss = small.tile([P, A], F32, name="ss")
             for a in range(A):
                 y_ps = psum.tile([P, DIM], F32, tag="pa", bufs=2, name="y_ps")
                 for db in range(4):
                     dcols = slice(P * db, P * db + P)
                     nc.tensor.matmul(
                         out=y_ps[:, dcols],
-                        lhsT=vt[:, db, P * a : P * a + P],
+                        lhsT=vts[c][:, db, P * a : P * a + P],
                         rhs=ident[:],
                         is_transpose=True,
                         start=True,
@@ -318,21 +353,34 @@ def tile_hypergraphgpslayer_pa_t_kernel(
                     nc.tensor.matmul(
                         out=y_ps[:, dcols],
                         lhsT=ident_bf[:],
-                        rhs=x0c[:, a, dcols],
+                        rhs=x0cs[c][:, a, dcols],
                         start=False,
                         stop=True,
                     )
                 nc.scalar.activation(
                     out=y[:, a, :], in_=y_ps[:], func=ACT.Copy, accum_out=sy[:, a : a + 1]
                 )
-            nc.vector.tensor_scalar_mul(out=nm[:], in0=sy[:], scalar1=-1.0 / DIM)
+            ys[c] = y
+            stat[c] = [sy]
+
+        def neg_mean(c):
+            if c < 0 or c >= N_CHUNKS:
+                return
+            nm = small.tile([P, A], F32, name="nm")
+            nc.vector.tensor_scalar_mul(out=nm[:], in0=stat[c][0][:], scalar1=-1.0 / DIM)
+            stat[c].append(nm)
+
+        def squares(c):
+            if c < 0 or c >= N_CHUNKS:
+                return
+            ss = small.tile([P, A], F32, name="ss")
             for a in range(A):
                 junk = work.tile([P, DIM], BF16, name="junk")
                 nc.scalar.activation(
                     out=junk[:],
-                    in_=y[:, a, :],
+                    in_=ys[c][:, a, :],
                     func=ACT.Square,
-                    bias=nm[:, a : a + 1],
+                    bias=stat[c][1][:, a : a + 1],
                     scale=1.0,
                     accum_out=ss[:, a : a + 1],
                 )
@@ -340,25 +388,87 @@ def tile_hypergraphgpslayer_pa_t_kernel(
             nc.vector.tensor_scalar(
                 out=vv[:], in0=ss[:], scalar1=1.0 / DIM, scalar2=LN_EPS, op0=ALU.mult, op1=ALU.add
             )
-            sd = small.tile([P, A], F32, name="sd")
-            nc.scalar.activation(out=sd[:], in_=vv[:], func=ACT.Sqrt)
             rs = small.tile([P, A], F32, name="rs")
-            nc.vector.reciprocal(out=rs[:], in_=sd[:])
-            for a in range(A):
+            nc.gpsimd.tensor_tensor(out=rs[:], in0=vv[:], in1=mhalf[:, 0:A], op=ALU.pow)
+            stat[c].append(rs)
+
+        def gain_shift(c, tiles):
+            if c < 0 or c >= N_CHUNKS:
+                return
+            y = ys[c]
+            for a in tiles:
                 nc.vector.scalar_tensor_tensor(
                     out=y[:, a, :],
                     in0=y[:, a, :],
-                    scalar=nm[:, a : a + 1],
+                    scalar=stat[c][1][:, a : a + 1],
                     in1=g_ps[:],
                     op0=ALU.add,
                     op1=ALU.mult,
                 )
+            for a in tiles:
                 nc.vector.scalar_tensor_tensor(
                     out=y[:, a, :],
                     in0=y[:, a, :],
-                    scalar=rs[:, a : a + 1],
+                    scalar=stat[c][2][:, a : a + 1],
                     in1=be_ps[:],
                     op0=ALU.mult,
                     op1=ALU.add,
                 )
-            nc.sync.dma_start(out=out[rows, :].rearrange("(p a) d -> p a d", a=A), in_=y[:])
+
+        def store(c):
+            if c < 0 or c >= N_CHUNKS:
+                return
+            nc.sync.dma_start(
+                out=out[c * CHUNK : (c + 1) * CHUNK, :].rearrange("(p a) d -> p a d", a=A),
+                in_=ys[c][:],
+            )
+
+        planes(0, True)
+        planes(0, False)
+
+        x1g = work.tile([P, 2, DIM, 4], BF16, tag="vt", name="x1g", align_bytes=64)
+        for g in range(2):
+            nc.vector.tensor_copy(
+                out=x1g[:, g], in_=x1raw[:, 4 * g : 4 * g + 4, :].rearrange("p t d -> p d t")
+            )
+        wg = work.tile([P, DIM, 4], BF16, tag="msgg", name="wg", align_bytes=64)
+        nc.vector.tensor_copy(out=wg[:], in_=wraw[:].rearrange("p t n -> p n t"))
+        nc.vector.quantize_mx(
+            out=x1cod[:].rearrange("p g d -> p (g d)").bitcast(FP8X4),
+            scales=x1sc[:].rearrange("p g d -> p (g d)"),
+            in_=x1g[:].rearrange("p g d t -> p (g d t)"),
+        )
+        nc.vector.quantize_mx(
+            out=wcod[:].bitcast(FP8X4),
+            scales=wsc[:],
+            in_=wg[:].rearrange("p n t -> p (n t)"),
+        )
+        planes(1, True)
+        planes(1, False)
+
+        for c in range(ROWS_EARLY, N_CHUNKS):
+            row_sums(c)
+        for c in range(TR_EARLY, N_CHUNKS):
+            transposes(c)
+            exits(c)
+        for c in range(3, N_CHUNKS):
+            spread_a(c)
+
+        g_ps = psum.tile([P, DIM], F32, tag="pd", name="g_ps")
+        nc.tensor.matmul(out=g_ps[:], lhsT=ones_m[:], rhs=vecs[:, 0, :], start=True, stop=True)
+        be_ps = psum.tile([P, DIM], F32, tag="pe", name="be_ps")
+        nc.tensor.matmul(out=be_ps[:], lhsT=ones_m[:], rhs=vecs[:, 1, :], start=True, stop=True)
+
+        for i in range(N_CHUNKS + 2):
+            second_product(i - 1)
+            mask_quant(i)
+            squares(i - 2)
+            planes(i + 2, False)
+            residual(i - 1)
+            first_product(i)
+            gain_shift(i - 2, (0, 1))
+            neg_mean(i - 1)
+            gain_shift(i - 2, (2, 3))
+            store(i - 2)
+            planes(i + 2, True)
+            load_x0(i + 2)

@@ -23,7 +23,7 @@ CHUNK = P * A
 N_CHUNKS = N_NODES // CHUNK
 LN_EPS = 1e-5
 NW = 2
-SCALAR_PLANES = (0, 1, 2)
+SCALAR_PLANES = ()
 ROWS_EARLY = 11
 TR_EARLY = 8
 

@@ -23,9 +23,6 @@ CHUNK = P * A
 N_CHUNKS = N_NODES // CHUNK
 LN_EPS = 1e-5
 NW = 2
-SCALAR_PLANES = ()
-ROWS_EARLY = 11
-TR_EARLY = 8
 
 
 def tile_hypergraphgpslayer_pa_t_kernel(
@@ -72,7 +69,7 @@ def tile_hypergraphgpslayer_pa_t_kernel(
         gcol = const.tile([P, 1], F32)
         nc.scalar.activation(out=gcol[:], in_=gt[:], func=ACT.Tanh)
         ccol = const.tile([P, 4], F32)
-        bnt_ps = psum.tile([P, P], BF16, tag="pe", name="bnt_ps")
+        bnt_ps = psum.tile([P, P], BF16, tag="pb", bufs=3, name="bnt_ps")
         nc.tensor.transpose(bnt_ps[:], bn_rows[:], ident_bf[:])
         nc.vector.tensor_scalar(
             out=ccol[:], in0=bnt_ps[:, 0:4], scalar1=gcol[:], scalar2=None, op0=ALU.mult
@@ -114,9 +111,7 @@ def tile_hypergraphgpslayer_pa_t_kernel(
         load_x0(0)
         load_x0(1)
 
-        de_ps = psum.tile([P, DIM], F32, tag="pd", name="de_ps")
-        htg = {}
-        tps = {}
+        de_ps = psum.tile([P, DIM], F32, tag="pa", bufs=4, name="de_ps")
         avs = {}
         abc = {}
 
@@ -136,48 +131,28 @@ def tile_hypergraphgpslayer_pa_t_kernel(
             dv = small.tile([P, A], F32, name="dv")
             for a in range(A):
                 junk1 = work.tile([P, N_EDGES], BF16, name="junk1")
-                nc.vector.tensor_scalar(
-                    out=junk1[:],
-                    in0=hc[c][:, a, :],
-                    scalar1=1.0,
-                    scalar2=None,
-                    op0=ALU.mult,
-                    op1=ALU.add,
-                    accum_out=dv[:, a : a + 1],
-                )
+                if c % 3 == 2:
+                    nc.scalar.activation(
+                        out=junk1[:], in_=hc[c][:, a, :], func=ACT.Copy, accum_out=dv[:, a : a + 1]
+                    )
+                else:
+                    nc.vector.tensor_scalar(
+                        out=junk1[:],
+                        in0=hc[c][:, a, :],
+                        scalar1=1.0,
+                        scalar2=None,
+                        op0=ALU.mult,
+                        op1=ALU.add,
+                        accum_out=dv[:, a : a + 1],
+                    )
             dvm = small.tile([P, A], F32, name="dvm")
             nc.vector.tensor_scalar_max(out=dvm[:], in0=dv[:], scalar1=1.0)
             av = small.tile([P, A], F32, name="av", bufs=N_CHUNKS)
             nc.gpsimd.tensor_tensor(out=av[:], in0=dvm[:], in1=mhalf[:, 0:A], op=ALU.pow)
             avs[c] = av
 
-        def transposes(c):
-            tps[c] = []
-            for a in range(A):
-                q = (A * c + a) % 6
-                tp = psum.tile([P, 4, P], F32, tag=("pa", "pb", "pc")[q // 2], bufs=2, name="tp")
-                hw = hc[c][:, a, :].bitcast(F32)
-                for wb in range(4):
-                    nc.tensor.transpose(tp[:, wb, :], hw[:, P * wb : P * wb + P], ident[:])
-                tps[c].append(tp)
-
-        def exits(c):
-            t = big.tile([P, 2, CHUNK, 4], BF16, tag="big%d" % c, name="htg%d" % c, align_bytes=64)
-            htg[c] = t
-            t_w = (
-                t[:]
-                .rearrange("p g n t -> p (g n t)")
-                .bitcast(F32)
-                .rearrange("p (g n u) -> p g n u", g=2, n=CHUNK, u=2)
-            )
-            for a in range(A):
-                nc.scalar.copy(
-                    out=t_w[:, :, P * a : P * a + P, :],
-                    in_=tps[c][a][:].rearrange("p (g u) n -> p g n u", g=2),
-                )
-
         def spread_a(c):
-            ab_ps = psum.tile([P, A, P], F32, tag="pe", name="ab_ps")
+            ab_ps = psum.tile([P, A, P], F32, tag="pb", bufs=3, name="ab_ps")
             for a in range(A):
                 nc.tensor.transpose(
                     ab_ps[:, a, :], avs[c][:, a : a + 1].to_broadcast([P, P]), ident[:]
@@ -186,18 +161,11 @@ def tile_hypergraphgpslayer_pa_t_kernel(
             nc.scalar.copy(out=t[:], in_=ab_ps[:].rearrange("p a n -> p (a n)"))
             abc[c] = t
 
-        n_tr = 0
         for c in range(N_CHUNKS):
             col_sums(c)
-            if c < ROWS_EARLY:
-                row_sums(c)
-            if c >= 1 and n_tr < TR_EARLY:
-                transposes(n_tr)
-                exits(n_tr)
-                n_tr += 1
-            if c == 8:
-                for z in range(3):
-                    spread_a(z)
+            row_sums(c)
+            if c >= 2:
+                spread_a(c - 2)
 
         de = small.tile([P, 8], F32, name="de")
         nc.vector.tensor_reduce(
@@ -213,7 +181,7 @@ def tile_hypergraphgpslayer_pa_t_kernel(
         bnat = small.tile([P, 8], F32, name="bnat")
         nc.gpsimd.tensor_tensor(out=bnat[:], in0=dem[:], in1=mhalf[:], op=ALU.pow)
         bnat_v = bnat[:].rearrange("p (w h) -> p h w", h=2)
-        b4_ps = psum.tile([P, 2, 4], F32, tag="pe", name="b4_ps")
+        b4_ps = psum.tile([P, 2, 4], F32, tag="pb", bufs=3, name="b4_ps")
         for eo in range(2):
             for h in range(2):
                 nc.tensor.matmul(
@@ -236,47 +204,48 @@ def tile_hypergraphgpslayer_pa_t_kernel(
         ys = {}
         stat = {}
 
-        def plane(c, i):
-            if c not in cps:
-                cps[c] = work.tile([P, 2, 4, CHUNK], BF16, tag="cp", name="cp")
-            if i in SCALAR_PLANES:
-                nc.scalar.activation(
-                    out=cps[c][:, i // 4, i % 4, :],
-                    in_=abc[c][:],
-                    func=ACT.Copy,
-                    scale=b4[:, i : i + 1],
-                )
-            else:
-                nc.vector.tensor_scalar(
-                    out=cps[c][:, i // 4, i % 4, :],
-                    in0=abc[c][:],
-                    scalar1=b4[:, i : i + 1],
-                    scalar2=None,
-                    op0=ALU.mult,
-                )
-
-        def planes(c, on_scalar):
+        def planes(c):
             if c < N_CHUNKS:
+                cps[c] = work.tile([P, 2, 4, CHUNK], BF16, tag="cp", name="cp")
                 for i in range(8):
-                    if (i in SCALAR_PLANES) == on_scalar:
-                        plane(c, i)
+                    nc.gpsimd.tensor_scalar(
+                        out=cps[c][:, i // 4, i % 4, :],
+                        in0=abc[c][:],
+                        scalar1=b4[:, i : i + 1],
+                        scalar2=0.0,
+                        op0=ALU.mult,
+                        op1=ALU.add,
+                    )
 
         def mask_quant(c):
             if c >= N_CHUNKS:
                 return
-            for g in range(2):
-                nc.vector.tensor_tensor(
-                    out=htg[c][:, g],
-                    in0=htg[c][:, g],
-                    in1=cps[c][:, g].rearrange("p t n -> p n t"),
-                    op=ALU.mult,
+            hng = work.tile([P, 2, CHUNK, 4], BF16, name="hng", align_bytes=64)
+            for a in range(A):
+                cols = slice(P * a, P * a + P)
+                ht = psum.tile([P, 4, P], F32, tag="pa", bufs=4, name="ht")
+                hw = hc[c][:, a, :].bitcast(F32)
+                for wb in range(4):
+                    nc.tensor.transpose(ht[:, wb, :], hw[:, P * wb : P * wb + P], ident[:])
+                ht_b = (
+                    ht[:]
+                    .rearrange("p w n -> p (w n)")
+                    .bitcast(BF16)
+                    .rearrange("p (w n e) -> p w n e", w=4, n=P, e=2)
                 )
+                for g in range(2):
+                    nc.vector.tensor_tensor(
+                        out=hng[:, g, cols, :].rearrange("p n (u e) -> p n u e", u=2),
+                        in0=ht_b[:, 2 * g : 2 * g + 2].rearrange("p u n e -> p n u e"),
+                        in1=cps[c][:, g, :, cols].rearrange("p (u e) n -> p n u e", u=2),
+                        op=ALU.mult,
+                    )
             hcod = work.tile([P, 2, CHUNK], U32, name="hcod", align_bytes=64)
             hsc = work.tile([P, 2, CHUNK], U8, name="hsc", align_bytes=64)
             nc.vector.quantize_mx(
                 out=hcod[:].rearrange("p g n -> p (g n)").bitcast(FP8X4),
                 scales=hsc[:].rearrange("p g n -> p (g n)"),
-                in_=htg[c][:].rearrange("p g n t -> p (g n t)"),
+                in_=hng[:].rearrange("p g n t -> p (g n t)"),
             )
             hq[c] = (hcod, hsc)
 
@@ -287,7 +256,7 @@ def tile_hypergraphgpslayer_pa_t_kernel(
             msgg = work.tile([P, CHUNK, 4], BF16, tag="msgg", name="msgg", align_bytes=64)
             for a in range(A):
                 cols = slice(P * a, P * a + P)
-                m1 = psum.tile([P, 4, P], F32, tag="pc", bufs=2, name="m1")
+                m1 = psum.tile([P, 4, P], F32, tag="pb", bufs=3, name="m1")
                 for tb in range(4):
                     for g in range(2):
                         nc.tensor.matmul_mx(
@@ -314,7 +283,7 @@ def tile_hypergraphgpslayer_pa_t_kernel(
             )
             vt = work.tile([P, 4, CHUNK], F32, tag="vt", name="vt", align_bytes=64)
             for db in range(4):
-                u_ps = psum.tile([P, CHUNK], F32, tag="pb", bufs=2, name="u_ps")
+                u_ps = psum.tile([P, CHUNK], F32, tag="pb", bufs=3, name="u_ps")
                 nc.tensor.matmul_mx(
                     out=u_ps[:],
                     lhsT=wcod[:, P * db : P * db + P].bitcast(FP8X4),
@@ -339,7 +308,7 @@ def tile_hypergraphgpslayer_pa_t_kernel(
             y = big.tile([P, A, DIM], F32, tag="big%d" % c, name="y%d" % c, align_bytes=64)
             sy = small.tile([P, A], F32, name="sy")
             for a in range(A):
-                y_ps = psum.tile([P, DIM], F32, tag="pa", bufs=2, name="y_ps")
+                y_ps = psum.tile([P, DIM], F32, tag="pa", bufs=4, name="y_ps")
                 for db in range(4):
                     dcols = slice(P * db, P * db + P)
                     nc.tensor.matmul(
@@ -401,7 +370,7 @@ def tile_hypergraphgpslayer_pa_t_kernel(
                     out=y[:, a, :],
                     in0=y[:, a, :],
                     scalar=stat[c][1][:, a : a + 1],
-                    in1=g_ps[:],
+                    in1=gb_ps[:, 0, :],
                     op0=ALU.add,
                     op1=ALU.mult,
                 )
@@ -410,7 +379,7 @@ def tile_hypergraphgpslayer_pa_t_kernel(
                     out=y[:, a, :],
                     in0=y[:, a, :],
                     scalar=stat[c][2][:, a : a + 1],
-                    in1=be_ps[:],
+                    in1=gb_ps[:, 1, :],
                     op0=ALU.mult,
                     op1=ALU.add,
                 )
@@ -423,8 +392,7 @@ def tile_hypergraphgpslayer_pa_t_kernel(
                 in_=ys[c][:],
             )
 
-        planes(0, True)
-        planes(0, False)
+        planes(0)
 
         x1g = work.tile([P, 2, DIM, 4], BF16, tag="vt", name="x1g", align_bytes=64)
         for g in range(2):
@@ -443,32 +411,26 @@ def tile_hypergraphgpslayer_pa_t_kernel(
             scales=wsc[:],
             in_=wg[:].rearrange("p n t -> p (n t)"),
         )
-        planes(1, True)
-        planes(1, False)
+        planes(1)
 
-        for c in range(ROWS_EARLY, N_CHUNKS):
-            row_sums(c)
-        for c in range(TR_EARLY, N_CHUNKS):
-            transposes(c)
-            exits(c)
-        for c in range(3, N_CHUNKS):
-            spread_a(c)
+        spread_a(N_CHUNKS - 2)
+        spread_a(N_CHUNKS - 1)
 
-        g_ps = psum.tile([P, DIM], F32, tag="pd", name="g_ps")
-        nc.tensor.matmul(out=g_ps[:], lhsT=ones_m[:], rhs=vecs[:, 0, :], start=True, stop=True)
-        be_ps = psum.tile([P, DIM], F32, tag="pe", name="be_ps")
-        nc.tensor.matmul(out=be_ps[:], lhsT=ones_m[:], rhs=vecs[:, 1, :], start=True, stop=True)
+        gb_ps = psum.tile([P, 2, DIM], BF16, tag="pk", name="gb_ps")
+        for r in range(2):
+            nc.tensor.matmul(
+                out=gb_ps[:, r, :], lhsT=ones_m[:], rhs=vecs[:, r, :], start=True, stop=True
+            )
 
         for i in range(N_CHUNKS + 2):
             second_product(i - 1)
             mask_quant(i)
             squares(i - 2)
-            planes(i + 2, False)
+            planes(i + 2)
             residual(i - 1)
             first_product(i)
             gain_shift(i - 2, (0, 1))
             neg_mean(i - 1)
             gain_shift(i - 2, (2, 3))
             store(i - 2)
-            planes(i + 2, True)
             load_x0(i + 2)

@@ -23,6 +23,9 @@ CHUNK = P * A
 N_CHUNKS = N_NODES // CHUNK
 LN_EPS = 1e-5
 NW = 2
+SCALAR_PLANES = (0, 1, 2)
+ROWS_EARLY = 11
+TR_EARLY = 8
 
 
 def tile_hypergraphgpslayer_pa_t_kernel(
@@ -33,7 +36,7 @@ def tile_hypergraphgpslayer_pa_t_kernel(
         const = ctx.enter_context(tc.tile_pool(name="const", bufs=1))
         big = ctx.enter_context(tc.tile_pool(name="big", bufs=1))
         keep = ctx.enter_context(tc.tile_pool(name="keep", bufs=1))
-        small = ctx.enter_context(tc.tile_pool(name="small", bufs=4))
+        small = ctx.enter_context(tc.tile_pool(name="small", bufs=8))
         work = ctx.enter_context(tc.tile_pool(name="work", bufs=2))
         psum = ctx.enter_context(tc.psum_pool(name="psum", bufs=1))
 
@@ -69,7 +72,7 @@ def tile_hypergraphgpslayer_pa_t_kernel(
         gcol = const.tile([P, 1], F32)
         nc.scalar.activation(out=gcol[:], in_=gt[:], func=ACT.Tanh)
         ccol = const.tile([P, 4], F32)
-        bnt_ps = psum.tile([P, P], BF16, tag="pb", bufs=3, name="bnt_ps")
+        bnt_ps = psum.tile([P, P], BF16, tag="pe", name="bnt_ps")
         nc.tensor.transpose(bnt_ps[:], bn_rows[:], ident_bf[:])
         nc.vector.tensor_scalar(
             out=ccol[:], in0=bnt_ps[:, 0:4], scalar1=gcol[:], scalar2=None, op0=ALU.mult
@@ -111,7 +114,9 @@ def tile_hypergraphgpslayer_pa_t_kernel(
         load_x0(0)
         load_x0(1)
 
-        de_ps = psum.tile([P, DIM], F32, tag="pa", bufs=4, name="de_ps")
+        de_ps = psum.tile([P, DIM], F32, tag="pd", name="de_ps")
+        htg = {}
+        tps = {}
         avs = {}
         abc = {}
 
@@ -131,28 +136,48 @@ def tile_hypergraphgpslayer_pa_t_kernel(
             dv = small.tile([P, A], F32, name="dv")
             for a in range(A):
                 junk1 = work.tile([P, N_EDGES], BF16, name="junk1")
-                if c % 3 == 2:
-                    nc.scalar.activation(
-                        out=junk1[:], in_=hc[c][:, a, :], func=ACT.Copy, accum_out=dv[:, a : a + 1]
-                    )
-                else:
-                    nc.vector.tensor_scalar(
-                        out=junk1[:],
-                        in0=hc[c][:, a, :],
-                        scalar1=1.0,
-                        scalar2=None,
-                        op0=ALU.mult,
-                        op1=ALU.add,
-                        accum_out=dv[:, a : a + 1],
-                    )
+                nc.vector.tensor_scalar(
+                    out=junk1[:],
+                    in0=hc[c][:, a, :],
+                    scalar1=1.0,
+                    scalar2=None,
+                    op0=ALU.mult,
+                    op1=ALU.add,
+                    accum_out=dv[:, a : a + 1],
+                )
             dvm = small.tile([P, A], F32, name="dvm")
             nc.vector.tensor_scalar_max(out=dvm[:], in0=dv[:], scalar1=1.0)
             av = small.tile([P, A], F32, name="av", bufs=N_CHUNKS)
             nc.gpsimd.tensor_tensor(out=av[:], in0=dvm[:], in1=mhalf[:, 0:A], op=ALU.pow)
             avs[c] = av
 
+        def transposes(c):
+            tps[c] = []
+            for a in range(A):
+                q = (A * c + a) % 6
+                tp = psum.tile([P, 4, P], F32, tag=("pa", "pb", "pc")[q // 2], bufs=2, name="tp")
+                hw = hc[c][:, a, :].bitcast(F32)
+                for wb in range(4):
+                    nc.tensor.transpose(tp[:, wb, :], hw[:, P * wb : P * wb + P], ident[:])
+                tps[c].append(tp)
+
+        def exits(c):
+            t = big.tile([P, 2, CHUNK, 4], BF16, tag="big%d" % c, name="htg%d" % c, align_bytes=64)
+            htg[c] = t
+            t_w = (
+                t[:]
+                .rearrange("p g n t -> p (g n t)")
+                .bitcast(F32)
+                .rearrange("p (g n u) -> p g n u", g=2, n=CHUNK, u=2)
+            )
+            for a in range(A):
+                nc.scalar.copy(
+                    out=t_w[:, :, P * a : P * a + P, :],
+                    in_=tps[c][a][:].rearrange("p (g u) n -> p g n u", g=2),
+                )
+
         def spread_a(c):
-            ab_ps = psum.tile([P, A, P], F32, tag="pb", bufs=3, name="ab_ps")
+            ab_ps = psum.tile([P, A, P], F32, tag="pe", name="ab_ps")
             for a in range(A):
                 nc.tensor.transpose(
                     ab_ps[:, a, :], avs[c][:, a : a + 1].to_broadcast([P, P]), ident[:]
@@ -161,11 +186,18 @@ def tile_hypergraphgpslayer_pa_t_kernel(
             nc.scalar.copy(out=t[:], in_=ab_ps[:].rearrange("p a n -> p (a n)"))
             abc[c] = t
 
+        n_tr = 0
         for c in range(N_CHUNKS):
             col_sums(c)
-            row_sums(c)
-            if c >= 2:
-                spread_a(c - 2)
+            if c < ROWS_EARLY:
+                row_sums(c)
+            if c >= 1 and n_tr < TR_EARLY:
+                transposes(n_tr)
+                exits(n_tr)
+                n_tr += 1
+            if c == 8:
+                for z in range(3):
+                    spread_a(z)
 
         de = small.tile([P, 8], F32, name="de")
         nc.vector.tensor_reduce(
@@ -181,7 +213,7 @@ def tile_hypergraphgpslayer_pa_t_kernel(
         bnat = small.tile([P, 8], F32, name="bnat")
         nc.gpsimd.tensor_tensor(out=bnat[:], in0=dem[:], in1=mhalf[:], op=ALU.pow)
         bnat_v = bnat[:].rearrange("p (w h) -> p h w", h=2)
-        b4_ps = psum.tile([P, 2, 4], F32, tag="pb", bufs=3, name="b4_ps")
+        b4_ps = psum.tile([P, 2, 4], F32, tag="pe", name="b4_ps")
         for eo in range(2):
             for h in range(2):
                 nc.tensor.matmul(
@@ -204,48 +236,47 @@ def tile_hypergraphgpslayer_pa_t_kernel(
         ys = {}
         stat = {}
 
-        def planes(c):
-            if c < N_CHUNKS:
+        def plane(c, i):
+            if c not in cps:
                 cps[c] = work.tile([P, 2, 4, CHUNK], BF16, tag="cp", name="cp")
+            if i in SCALAR_PLANES:
+                nc.scalar.activation(
+                    out=cps[c][:, i // 4, i % 4, :],
+                    in_=abc[c][:],
+                    func=ACT.Copy,
+                    scale=b4[:, i : i + 1],
+                )
+            else:
+                nc.vector.tensor_scalar(
+                    out=cps[c][:, i // 4, i % 4, :],
+                    in0=abc[c][:],
+                    scalar1=b4[:, i : i + 1],
+                    scalar2=None,
+                    op0=ALU.mult,
+                )
+
+        def planes(c, on_scalar):
+            if c < N_CHUNKS:
                 for i in range(8):
-                    nc.gpsimd.tensor_scalar(
-                        out=cps[c][:, i // 4, i % 4, :],
-                        in0=abc[c][:],
-                        scalar1=b4[:, i : i + 1],
-                        scalar2=0.0,
-                        op0=ALU.mult,
-                        op1=ALU.add,
-                    )
+                    if (i in SCALAR_PLANES) == on_scalar:
+                        plane(c, i)
 
         def mask_quant(c):
             if c >= N_CHUNKS:
                 return
-            hng = work.tile([P, 2, CHUNK, 4], BF16, name="hng", align_bytes=64)
-            for a in range(A):
-                cols = slice(P * a, P * a + P)
-                ht = psum.tile([P, 4, P], F32, tag="pa", bufs=4, name="ht")
-                hw = hc[c][:, a, :].bitcast(F32)
-                for wb in range(4):
-                    nc.tensor.transpose(ht[:, wb, :], hw[:, P * wb : P * wb + P], ident[:])
-                ht_b = (
-                    ht[:]
-                    .rearrange("p w n -> p (w n)")
-                    .bitcast(BF16)
-                    .rearrange("p (w n e) -> p w n e", w=4, n=P, e=2)
+            for g in range(2):
+                nc.vector.tensor_tensor(
+                    out=htg[c][:, g],
+                    in0=htg[c][:, g],
+                    in1=cps[c][:, g].rearrange("p t n -> p n t"),
+                    op=ALU.mult,
                 )
-                for g in range(2):
-                    nc.vector.tensor_tensor(
-                        out=hng[:, g, cols, :].rearrange("p n (u e) -> p n u e", u=2),
-                        in0=ht_b[:, 2 * g : 2 * g + 2].rearrange("p u n e -> p n u e"),
-                        in1=cps[c][:, g, :, cols].rearrange("p (u e) n -> p n u e", u=2),
-                        op=ALU.mult,
-                    )
             hcod = work.tile([P, 2, CHUNK], U32, name="hcod", align_bytes=64)
             hsc = work.tile([P, 2, CHUNK], U8, name="hsc", align_bytes=64)
             nc.vector.quantize_mx(
                 out=hcod[:].rearrange("p g n -> p (g n)").bitcast(FP8X4),
                 scales=hsc[:].rearrange("p g n -> p (g n)"),
-                in_=hng[:].rearrange("p g n t -> p (g n t)"),
+                in_=htg[c][:].rearrange("p g n t -> p (g n t)"),
             )
             hq[c] = (hcod, hsc)
 
@@ -256,7 +287,7 @@ def tile_hypergraphgpslayer_pa_t_kernel(
             msgg = work.tile([P, CHUNK, 4], BF16, tag="msgg", name="msgg", align_bytes=64)
             for a in range(A):
                 cols = slice(P * a, P * a + P)
-                m1 = psum.tile([P, 4, P], F32, tag="pb", bufs=3, name="m1")
+                m1 = psum.tile([P, 4, P], F32, tag="pc", bufs=2, name="m1")
                 for tb in range(4):
                     for g in range(2):
                         nc.tensor.matmul_mx(
@@ -283,7 +314,7 @@ def tile_hypergraphgpslayer_pa_t_kernel(
             )
             vt = work.tile([P, 4, CHUNK], F32, tag="vt", name="vt", align_bytes=64)
             for db in range(4):
-                u_ps = psum.tile([P, CHUNK], F32, tag="pb", bufs=3, name="u_ps")
+                u_ps = psum.tile([P, CHUNK], F32, tag="pb", bufs=2, name="u_ps")
                 nc.tensor.matmul_mx(
                     out=u_ps[:],
                     lhsT=wcod[:, P * db : P * db + P].bitcast(FP8X4),
@@ -308,7 +339,7 @@ def tile_hypergraphgpslayer_pa_t_kernel(
             y = big.tile([P, A, DIM], F32, tag="big%d" % c, name="y%d" % c, align_bytes=64)
             sy = small.tile([P, A], F32, name="sy")
             for a in range(A):
-                y_ps = psum.tile([P, DIM], F32, tag="pa", bufs=4, name="y_ps")
+                y_ps = psum.tile([P, DIM], F32, tag="pa", bufs=2, name="y_ps")
                 for db in range(4):
                     dcols = slice(P * db, P * db + P)
                     nc.tensor.matmul(
@@ -370,7 +401,7 @@ def tile_hypergraphgpslayer_pa_t_kernel(
                     out=y[:, a, :],
                     in0=y[:, a, :],
                     scalar=stat[c][1][:, a : a + 1],
-                    in1=gb_ps[:, 0, :],
+                    in1=g_ps[:],
                     op0=ALU.add,
                     op1=ALU.mult,
                 )
@@ -379,7 +410,7 @@ def tile_hypergraphgpslayer_pa_t_kernel(
                     out=y[:, a, :],
                     in0=y[:, a, :],
                     scalar=stat[c][2][:, a : a + 1],
-                    in1=gb_ps[:, 1, :],
+                    in1=be_ps[:],
                     op0=ALU.mult,
                     op1=ALU.add,
                 )
@@ -392,7 +423,8 @@ def tile_hypergraphgpslayer_pa_t_kernel(
                 in_=ys[c][:],
             )
 
-        planes(0)
+        planes(0, True)
+        planes(0, False)
 
         x1g = work.tile([P, 2, DIM, 4], BF16, tag="vt", name="x1g", align_bytes=64)
         for g in range(2):
@@ -411,26 +443,32 @@ def tile_hypergraphgpslayer_pa_t_kernel(
             scales=wsc[:],
             in_=wg[:].rearrange("p n t -> p (n t)"),
         )
-        planes(1)
+        planes(1, True)
+        planes(1, False)
 
-        spread_a(N_CHUNKS - 2)
-        spread_a(N_CHUNKS - 1)
+        for c in range(ROWS_EARLY, N_CHUNKS):
+            row_sums(c)
+        for c in range(TR_EARLY, N_CHUNKS):
+            transposes(c)
+            exits(c)
+        for c in range(3, N_CHUNKS):
+            spread_a(c)
 
-        gb_ps = psum.tile([P, 2, DIM], BF16, tag="pk", name="gb_ps")
-        for r in range(2):
-            nc.tensor.matmul(
-                out=gb_ps[:, r, :], lhsT=ones_m[:], rhs=vecs[:, r, :], start=True, stop=True
-            )
+        g_ps = psum.tile([P, DIM], F32, tag="pd", name="g_ps")
+        nc.tensor.matmul(out=g_ps[:], lhsT=ones_m[:], rhs=vecs[:, 0, :], start=True, stop=True)
+        be_ps = psum.tile([P, DIM], F32, tag="pe", name="be_ps")
+        nc.tensor.matmul(out=be_ps[:], lhsT=ones_m[:], rhs=vecs[:, 1, :], start=True, stop=True)
 
-        for i in range(N_CHUNKS + 2):
+        for i in range(N_CHUNKS + 4):
             second_product(i - 1)
             mask_quant(i)
             squares(i - 2)
-            planes(i + 2)
+            planes(i + 2, False)
             residual(i - 1)
             first_product(i)
-            gain_shift(i - 2, (0, 1))
+            gain_shift(i - 4, (0, 1))
             neg_mean(i - 1)
-            gain_shift(i - 2, (2, 3))
-            store(i - 2)
+            gain_shift(i - 4, (2, 3))
+            store(i - 4)
+            planes(i + 2, True)
             load_x0(i + 2)

@@ -340,22 +340,17 @@ def tile_hypergraphgpslayer_pa_t_kernel(
             sy = small.tile([P, A], F32, name="sy")
             for a in range(A):
                 y_ps = psum.tile([P, DIM], F32, tag="pa", bufs=2, name="y_ps")
+                nc.tensor.matmul(
+                    out=y_ps[:], lhsT=ident_bf[:], rhs=x0cs[c][:, a, :], start=True, stop=False
+                )
                 for db in range(4):
-                    dcols = slice(P * db, P * db + P)
                     nc.tensor.matmul(
-                        out=y_ps[:, dcols],
+                        out=y_ps[:, P * db : P * db + P],
                         lhsT=vts[c][:, db, P * a : P * a + P],
                         rhs=ident[:],
                         is_transpose=True,
-                        start=True,
-                        stop=False,
-                    )
-                    nc.tensor.matmul(
-                        out=y_ps[:, dcols],
-                        lhsT=ident_bf[:],
-                        rhs=x0cs[c][:, a, dcols],
                         start=False,
-                        stop=True,
+                        stop=(db == 3),
                     )
                 nc.scalar.activation(
                     out=y[:, a, :], in_=y_ps[:], func=ACT.Copy, accum_out=sy[:, a : a + 1]

@@ -23,9 +23,8 @@ CHUNK = P * A
 N_CHUNKS = N_NODES // CHUNK
 LN_EPS = 1e-5
 NW = 2
-SCALAR_PLANES = (0, 1, 2)
-ROWS_EARLY = 11
-TR_EARLY = 8
+ROWS_ON_SCALAR = (3,)
+PLANES_ON_SCALAR = (1, 3)
 
 
 def tile_hypergraphgpslayer_pa_t_kernel(
@@ -35,7 +34,6 @@ def tile_hypergraphgpslayer_pa_t_kernel(
     with ExitStack() as ctx:
         const = ctx.enter_context(tc.tile_pool(name="const", bufs=1))
         big = ctx.enter_context(tc.tile_pool(name="big", bufs=1))
-        keep = ctx.enter_context(tc.tile_pool(name="keep", bufs=1))
         small = ctx.enter_context(tc.tile_pool(name="small", bufs=8))
         work = ctx.enter_context(tc.tile_pool(name="work", bufs=2))
         psum = ctx.enter_context(tc.psum_pool(name="psum", bufs=1))
@@ -50,16 +48,6 @@ def tile_hypergraphgpslayer_pa_t_kernel(
         make_identity(nc, ident[:])
         ident_bf = const.tile([P, P], BF16)
         make_identity(nc, ident_bf[:])
-        sel = []
-        for h in range(2):
-            for eo in range(2):
-                s = const.tile([P, P], F32, name="sel%d%d" % (h, eo))
-                nc.gpsimd.memset(s[:], 0.0)
-                nc.gpsimd.tensor_copy(
-                    out=s[:, 64 * h : 64 * h + 64],
-                    in_=ident[:].rearrange("p (q e) -> p e q", e=2)[:, eo, :],
-                )
-                sel.append(s)
         vecs = const.tile([P, 2, DIM], BF16)
         nc.vector.memset(vecs[:], 0.0)
         nc.scalar.dma_start(out=vecs[0:1, 0, :], in_=ln1_g.unsqueeze(0))
@@ -71,28 +59,27 @@ def tile_hypergraphgpslayer_pa_t_kernel(
         nc.scalar.dma_start(out=gt[:], in_=gate_local.partition_broadcast(P))
         gcol = const.tile([P, 1], F32)
         nc.scalar.activation(out=gcol[:], in_=gt[:], func=ACT.Tanh)
-        ccol = const.tile([P, 4], F32)
-        bnt_ps = psum.tile([P, P], BF16, tag="pe", name="bnt_ps")
-        nc.tensor.transpose(bnt_ps[:], bn_rows[:], ident_bf[:])
-        nc.vector.tensor_scalar(
-            out=ccol[:], in0=bnt_ps[:, 0:4], scalar1=gcol[:], scalar2=None, op0=ALU.mult
-        )
 
         x1cod = const.tile([P, 2, DIM], U32, align_bytes=64)
         x1sc = const.tile([P, 2, DIM], U8, align_bytes=64)
         wcod = const.tile([P, DIM], U32, align_bytes=64)
         wsc = const.tile([P, DIM], U8, align_bytes=64)
-        b4 = const.tile([P, 8], F32)
+        b_all = const.tile([P, N_EDGES], F32)
+        gb = const.tile([P, 2, DIM], F32)
 
         hc = []
-        for c in range(N_CHUNKS):
+
+        def load_h(c):
             t = big.tile([P, A, N_EDGES], BF16, tag="big%d" % c, name="hc%d" % c, align_bytes=64)
             nc.sync.dma_start(
                 out=t[:],
                 in_=incidence_1[c * CHUNK : (c + 1) * CHUNK, :].rearrange("(p a) e -> p a e", a=A),
             )
             hc.append(t)
-        x1raw = work.tile([P, 8, DIM], BF16, tag="cp", name="x1raw")
+
+        for c in range(N_CHUNKS):
+            load_h(c)
+        x1raw = work.tile([P, 8, DIM], BF16, tag="htg", name="x1raw", align_bytes=64)
         nc.sync.dma_start(
             out=x1raw[:].rearrange("p (w e) d -> p w (e d)", e=2),
             in_=x_1_new.rearrange("(w p e) d -> p w (e d)", w=4, p=P, e=2),
@@ -114,11 +101,19 @@ def tile_hypergraphgpslayer_pa_t_kernel(
         load_x0(0)
         load_x0(1)
 
+        ccol = const.tile([P, 4], F32)
+        bnt_ps = psum.tile([P, P], BF16, tag="pe", name="bnt_ps")
+        nc.tensor.transpose(bnt_ps[:], bn_rows[:], ident_bf[:])
+        nc.vector.tensor_scalar(
+            out=ccol[:], in0=bnt_ps[:, 0:4], scalar1=gcol[:], scalar2=None, op0=ALU.mult
+        )
+        for k in range(2):
+            gb_ps = psum.tile([P, DIM], F32, tag="pb", bufs=2, name="gb_ps")
+            nc.tensor.matmul(out=gb_ps[:], lhsT=ones_m[:], rhs=vecs[:, k, :], start=True, stop=True)
+            nc.scalar.copy(out=gb[:, k, :], in_=gb_ps[:])
+
         de_ps = psum.tile([P, DIM], F32, tag="pd", name="de_ps")
-        htg = {}
-        tps = {}
         avs = {}
-        abc = {}
 
         def col_sums(c):
             for j in range(8):
@@ -135,69 +130,42 @@ def tile_hypergraphgpslayer_pa_t_kernel(
         def row_sums(c):
             dv = small.tile([P, A], F32, name="dv")
             for a in range(A):
-                junk1 = work.tile([P, N_EDGES], BF16, name="junk1")
-                nc.vector.tensor_scalar(
-                    out=junk1[:],
-                    in0=hc[c][:, a, :],
-                    scalar1=1.0,
-                    scalar2=None,
-                    op0=ALU.mult,
-                    op1=ALU.add,
-                    accum_out=dv[:, a : a + 1],
-                )
+                if a in ROWS_ON_SCALAR:
+                    junk2 = work.tile([P, N_EDGES], BF16, name="junk2")
+                    nc.scalar.activation(
+                        out=junk2[:],
+                        in_=hc[c][:, a, :],
+                        func=ACT.Copy,
+                        accum_out=dv[:, a : a + 1],
+                    )
+                else:
+                    junk1 = work.tile([P, N_EDGES], BF16, name="junk1")
+                    nc.vector.tensor_scalar(
+                        out=junk1[:],
+                        in0=hc[c][:, a, :],
+                        scalar1=1.0,
+                        scalar2=None,
+                        op0=ALU.mult,
+                        op1=ALU.add,
+                        accum_out=dv[:, a : a + 1],
+                    )
             dvm = small.tile([P, A], F32, name="dvm")
             nc.vector.tensor_scalar_max(out=dvm[:], in0=dv[:], scalar1=1.0)
             av = small.tile([P, A], F32, name="av", bufs=N_CHUNKS)
             nc.gpsimd.tensor_tensor(out=av[:], in0=dvm[:], in1=mhalf[:, 0:A], op=ALU.pow)
             avs[c] = av
 
-        def transposes(c):
-            tps[c] = []
-            for a in range(A):
-                q = (A * c + a) % 6
-                tp = psum.tile([P, 4, P], F32, tag=("pa", "pb", "pc")[q // 2], bufs=2, name="tp")
-                hw = hc[c][:, a, :].bitcast(F32)
-                for wb in range(4):
-                    nc.tensor.transpose(tp[:, wb, :], hw[:, P * wb : P * wb + P], ident[:])
-                tps[c].append(tp)
+        x1g = work.tile([P, 2, DIM, 4], BF16, tag="vt", name="x1g", align_bytes=64)
+        wg = work.tile([P, DIM, 4], BF16, tag="msgg", name="wg", align_bytes=64)
 
-        def exits(c):
-            t = big.tile([P, 2, CHUNK, 4], BF16, tag="big%d" % c, name="htg%d" % c, align_bytes=64)
-            htg[c] = t
-            t_w = (
-                t[:]
-                .rearrange("p g n t -> p (g n t)")
-                .bitcast(F32)
-                .rearrange("p (g n u) -> p g n u", g=2, n=CHUNK, u=2)
-            )
-            for a in range(A):
-                nc.scalar.copy(
-                    out=t_w[:, :, P * a : P * a + P, :],
-                    in_=tps[c][a][:].rearrange("p (g u) n -> p g n u", g=2),
-                )
-
-        def spread_a(c):
-            ab_ps = psum.tile([P, A, P], F32, tag="pe", name="ab_ps")
-            for a in range(A):
-                nc.tensor.transpose(
-                    ab_ps[:, a, :], avs[c][:, a : a + 1].to_broadcast([P, P]), ident[:]
-                )
-            t = keep.tile([P, CHUNK], F32, name="abc%d" % c)
-            nc.scalar.copy(out=t[:], in_=ab_ps[:].rearrange("p a n -> p (a n)"))
-            abc[c] = t
-
-        n_tr = 0
         for c in range(N_CHUNKS):
             col_sums(c)
-            if c < ROWS_EARLY:
-                row_sums(c)
-            if c >= 1 and n_tr < TR_EARLY:
-                transposes(n_tr)
-                exits(n_tr)
-                n_tr += 1
-            if c == 8:
-                for z in range(3):
-                    spread_a(z)
+            row_sums(c)
+
+        for g in range(2):
+            nc.scalar.copy(
+                out=x1g[:, g], in_=x1raw[:, 4 * g : 4 * g + 4, :].rearrange("p t d -> p d t")
+            )
 
         de = small.tile([P, 8], F32, name="de")
         nc.vector.tensor_reduce(
@@ -212,65 +180,69 @@ def tile_hypergraphgpslayer_pa_t_kernel(
         nc.vector.tensor_scalar_max(out=dem[:], in0=de[:], scalar1=1.0)
         bnat = small.tile([P, 8], F32, name="bnat")
         nc.gpsimd.tensor_tensor(out=bnat[:], in0=dem[:], in1=mhalf[:], op=ALU.pow)
-        bnat_v = bnat[:].rearrange("p (w h) -> p h w", h=2)
-        b4_ps = psum.tile([P, 2, 4], F32, tag="pe", name="b4_ps")
-        for eo in range(2):
-            for h in range(2):
-                nc.tensor.matmul(
-                    out=b4_ps[:, eo, :],
-                    lhsT=sel[2 * h + eo][:],
-                    rhs=bnat_v[:, h, :],
-                    start=(h == 0),
-                    stop=(h == 1),
+        for h in range(2):
+            b_ps = psum.tile([P, 4, P], F32, tag="pa", bufs=2, name="b_ps")
+            for k in range(4):
+                j = 4 * h + k
+                nc.tensor.transpose(
+                    b_ps[:, k, :], bnat[:, j : j + 1].to_broadcast([P, P]), ident[:]
                 )
-        nc.vector.tensor_copy(
-            out=b4[:].rearrange("p (w e) -> p w e", e=2),
-            in_=b4_ps[:].rearrange("p e w -> p w e"),
-        )
+            dst = b_all[:, 512 * h : 512 * h + 512]
+            nc.vector.tensor_copy(out=dst, in_=b_ps[:].rearrange("p k m -> p (k m)"))
 
-        cps = {}
+        htg = {}
         hq = {}
         msgs = {}
-        mq = {}
         vts = {}
         ys = {}
         stat = {}
 
-        def plane(c, i):
-            if c not in cps:
-                cps[c] = work.tile([P, 2, 4, CHUNK], BF16, tag="cp", name="cp")
-            if i in SCALAR_PLANES:
-                nc.scalar.activation(
-                    out=cps[c][:, i // 4, i % 4, :],
-                    in_=abc[c][:],
-                    func=ACT.Copy,
-                    scale=b4[:, i : i + 1],
-                )
-            else:
-                nc.vector.tensor_scalar(
-                    out=cps[c][:, i // 4, i % 4, :],
-                    in0=abc[c][:],
-                    scalar1=b4[:, i : i + 1],
-                    scalar2=None,
-                    op0=ALU.mult,
-                )
-
-        def planes(c, on_scalar):
-            if c < N_CHUNKS:
-                for i in range(8):
-                    if (i in SCALAR_PLANES) == on_scalar:
-                        plane(c, i)
-
-        def mask_quant(c):
+        def scale(c):
             if c >= N_CHUNKS:
                 return
-            for g in range(2):
-                nc.vector.tensor_tensor(
-                    out=htg[c][:, g],
-                    in0=htg[c][:, g],
-                    in1=cps[c][:, g].rearrange("p t n -> p n t"),
-                    op=ALU.mult,
+            for a in range(A):
+                if c < 2 and a in PLANES_ON_SCALAR:
+                    ab = work.tile([P, N_EDGES], BF16, name="ab")
+                    nc.scalar.activation(
+                        out=ab[:], in_=b_all[:], func=ACT.Copy, scale=avs[c][:, a : a + 1]
+                    )
+                    nc.vector.tensor_tensor(
+                        out=hc[c][:, a, :], in0=hc[c][:, a, :], in1=ab[:], op=ALU.mult
+                    )
+                    continue
+                nc.vector.scalar_tensor_tensor(
+                    out=hc[c][:, a, :],
+                    in0=hc[c][:, a, :],
+                    scalar=avs[c][:, a : a + 1],
+                    in1=b_all[:],
+                    op0=ALU.mult,
+                    op1=ALU.mult,
                 )
+
+        def turn(c):
+            if c >= N_CHUNKS:
+                return
+            t = work.tile([P, 2, CHUNK, 4], BF16, tag="htg", name="htg", align_bytes=64)
+            htg[c] = t
+            t_w = (
+                t[:]
+                .rearrange("p g n t -> p (g n t)")
+                .bitcast(F32)
+                .rearrange("p (g n u) -> p g n u", g=2, n=CHUNK, u=2)
+            )
+            for a in range(A):
+                tp = psum.tile([P, 4, P], F32, tag=("pd", "pe")[a % 2], name="tp")
+                hw = hc[c][:, a, :].bitcast(F32)
+                for wb in range(4):
+                    nc.tensor.transpose(tp[:, wb, :], hw[:, P * wb : P * wb + P], ident[:])
+                nc.scalar.copy(
+                    out=t_w[:, :, P * a : P * a + P, :],
+                    in_=tp[:].rearrange("p (g u) n -> p g n u", g=2),
+                )
+
+        def quant_h(c):
+            if c >= N_CHUNKS:
+                return
             hcod = work.tile([P, 2, CHUNK], U32, name="hcod", align_bytes=64)
             hsc = work.tile([P, 2, CHUNK], U8, name="hsc", align_bytes=64)
             nc.vector.quantize_mx(
@@ -299,7 +271,11 @@ def tile_hypergraphgpslayer_pa_t_kernel(
                             start=(g == 0),
                             stop=(g == 1),
                         )
-                nc.scalar.copy(out=msgg[:, cols, :], in_=m1[:].rearrange("p t n -> p n t"))
+                m1_v = m1[:].rearrange("p t n -> p n t")
+                if a == A - 1:
+                    nc.vector.tensor_copy(out=msgg[:, cols, :], in_=m1_v)
+                else:
+                    nc.scalar.copy(out=msgg[:, cols, :], in_=m1_v)
             msgs[c] = msgg
 
         def second_product(c):
@@ -362,7 +338,14 @@ def tile_hypergraphgpslayer_pa_t_kernel(
             if c < 0 or c >= N_CHUNKS:
                 return
             nm = small.tile([P, A], F32, name="nm")
-            nc.vector.tensor_scalar_mul(out=nm[:], in0=stat[c][0][:], scalar1=-1.0 / DIM)
+            nc.gpsimd.tensor_scalar(
+                out=nm[:],
+                in0=stat[c][0][:],
+                scalar1=-1.0 / DIM,
+                scalar2=0.0,
+                op0=ALU.mult,
+                op1=ALU.add,
+            )
             stat[c].append(nm)
 
         def squares(c):
@@ -375,13 +358,18 @@ def tile_hypergraphgpslayer_pa_t_kernel(
                     out=junk[:],
                     in_=ys[c][:, a, :],
                     func=ACT.Square,
-                    bias=stat[c][1][:, a : a + 1],
-                    scale=1.0,
+                    bias=stat[c][0][:, a : a + 1],
+                    scale=-float(DIM),
                     accum_out=ss[:, a : a + 1],
                 )
             vv = small.tile([P, A], F32, name="vv")
-            nc.vector.tensor_scalar(
-                out=vv[:], in0=ss[:], scalar1=1.0 / DIM, scalar2=LN_EPS, op0=ALU.mult, op1=ALU.add
+            nc.gpsimd.tensor_scalar(
+                out=vv[:],
+                in0=ss[:],
+                scalar1=1.0 / DIM**3,
+                scalar2=LN_EPS,
+                op0=ALU.mult,
+                op1=ALU.add,
             )
             rs = small.tile([P, A], F32, name="rs")
             nc.gpsimd.tensor_tensor(out=rs[:], in0=vv[:], in1=mhalf[:, 0:A], op=ALU.pow)
@@ -396,7 +384,7 @@ def tile_hypergraphgpslayer_pa_t_kernel(
                     out=y[:, a, :],
                     in0=y[:, a, :],
                     scalar=stat[c][1][:, a : a + 1],
-                    in1=g_ps[:],
+                    in1=gb[:, 0, :],
                     op0=ALU.add,
                     op1=ALU.mult,
                 )
@@ -405,7 +393,7 @@ def tile_hypergraphgpslayer_pa_t_kernel(
                     out=y[:, a, :],
                     in0=y[:, a, :],
                     scalar=stat[c][2][:, a : a + 1],
-                    in1=be_ps[:],
+                    in1=gb[:, 1, :],
                     op0=ALU.mult,
                     op1=ALU.add,
                 )
@@ -418,52 +406,30 @@ def tile_hypergraphgpslayer_pa_t_kernel(
                 in_=ys[c][:],
             )
 
-        planes(0, True)
-        planes(0, False)
-
-        x1g = work.tile([P, 2, DIM, 4], BF16, tag="vt", name="x1g", align_bytes=64)
-        for g in range(2):
-            nc.vector.tensor_copy(
-                out=x1g[:, g], in_=x1raw[:, 4 * g : 4 * g + 4, :].rearrange("p t d -> p d t")
-            )
-        wg = work.tile([P, DIM, 4], BF16, tag="msgg", name="wg", align_bytes=64)
-        nc.vector.tensor_copy(out=wg[:], in_=wraw[:].rearrange("p t n -> p n t"))
+        scale(0)
+        turn(0)
+        scale(1)
         nc.vector.quantize_mx(
             out=x1cod[:].rearrange("p g d -> p (g d)").bitcast(FP8X4),
             scales=x1sc[:].rearrange("p g d -> p (g d)"),
             in_=x1g[:].rearrange("p g d t -> p (g d t)"),
         )
+        nc.scalar.copy(out=wg[:], in_=wraw[:].rearrange("p t n -> p n t"))
         nc.vector.quantize_mx(
             out=wcod[:].bitcast(FP8X4),
             scales=wsc[:],
             in_=wg[:].rearrange("p n t -> p (n t)"),
         )
-        planes(1, True)
-        planes(1, False)
-
-        for c in range(ROWS_EARLY, N_CHUNKS):
-            row_sums(c)
-        for c in range(TR_EARLY, N_CHUNKS):
-            transposes(c)
-            exits(c)
-        for c in range(3, N_CHUNKS):
-            spread_a(c)
-
-        g_ps = psum.tile([P, DIM], F32, tag="pd", name="g_ps")
-        nc.tensor.matmul(out=g_ps[:], lhsT=ones_m[:], rhs=vecs[:, 0, :], start=True, stop=True)
-        be_ps = psum.tile([P, DIM], F32, tag="pe", name="be_ps")
-        nc.tensor.matmul(out=be_ps[:], lhsT=ones_m[:], rhs=vecs[:, 1, :], start=True, stop=True)
-
         for i in range(N_CHUNKS + 4):
             second_product(i - 1)
-            mask_quant(i)
+            quant_h(i)
             squares(i - 2)
-            planes(i + 2, False)
+            turn(i + 1)
             residual(i - 1)
             first_product(i)
             gain_shift(i - 4, (0, 1))
             neg_mean(i - 1)
+            scale(i + 2)
             gain_shift(i - 4, (2, 3))
             store(i - 4)
-            planes(i + 2, True)
             load_x0(i + 2)

@@ -66,6 +66,7 @@ def tile_hypergraphgpslayer_pa_t_kernel(
         wsc = const.tile([P, DIM], U8, align_bytes=64)
         b_all = const.tile([P, N_EDGES], F32)
         gb = const.tile([P, 2, DIM], F32)
+        ccol = const.tile([P, 4], F32)
 
         hc = []
 
@@ -100,17 +101,6 @@ def tile_hypergraphgpslayer_pa_t_kernel(
 
         load_x0(0)
         load_x0(1)
-
-        ccol = const.tile([P, 4], F32)
-        bnt_ps = psum.tile([P, P], BF16, tag="pe", name="bnt_ps")
-        nc.tensor.transpose(bnt_ps[:], bn_rows[:], ident_bf[:])
-        nc.vector.tensor_scalar(
-            out=ccol[:], in0=bnt_ps[:, 0:4], scalar1=gcol[:], scalar2=None, op0=ALU.mult
-        )
-        for k in range(2):
-            gb_ps = psum.tile([P, DIM], F32, tag="pb", bufs=2, name="gb_ps")
-            nc.tensor.matmul(out=gb_ps[:], lhsT=ones_m[:], rhs=vecs[:, k, :], start=True, stop=True)
-            nc.scalar.copy(out=gb[:, k, :], in_=gb_ps[:])
 
         de_ps = psum.tile([P, DIM], F32, tag="pd", name="de_ps")
         avs = {}
@@ -189,6 +179,16 @@ def tile_hypergraphgpslayer_pa_t_kernel(
                 )
             dst = b_all[:, 512 * h : 512 * h + 512]
             nc.vector.tensor_copy(out=dst, in_=b_ps[:].rearrange("p k m -> p (k m)"))
+
+        bnt_ps = psum.tile([P, P], BF16, tag="pd", name="bnt_ps")
+        nc.tensor.transpose(bnt_ps[:], bn_rows[:], ident_bf[:])
+        nc.vector.tensor_scalar(
+            out=ccol[:], in0=bnt_ps[:, 0:4], scalar1=gcol[:], scalar2=None, op0=ALU.mult
+        )
+        for k in range(2):
+            gb_ps = psum.tile([P, DIM], F32, tag="pd", name="gb_ps")
+            nc.tensor.matmul(out=gb_ps[:], lhsT=ones_m[:], rhs=vecs[:, k, :], start=True, stop=True)
+            nc.scalar.copy(out=gb[:, k, :], in_=gb_ps[:])
 
         htg = {}
         hq = {}

@@ -102,7 +102,7 @@ def tile_hypergraphgpslayer_pa_t_kernel(
         load_x0(0)
         load_x0(1)
 
-        de_ps = psum.tile([P, DIM], F32, tag="pd", name="de_ps")
+        de_ps = psum.tile([P, DIM], F32, tag="py", bufs=4, name="de_ps")
         avs = {}
 
         def col_sums(c):
@@ -146,7 +146,7 @@ def tile_hypergraphgpslayer_pa_t_kernel(
             avs[c] = av
 
         x1g = work.tile([P, 2, DIM, 4], BF16, tag="vt", name="x1g", align_bytes=64)
-        wg = work.tile([P, DIM, 4], BF16, tag="msgg", name="wg", align_bytes=64)
+        wg = const.tile([P, DIM, 4], BF16, name="wg", align_bytes=64)
 
         for c in range(N_CHUNKS):
             col_sums(c)
@@ -171,7 +171,7 @@ def tile_hypergraphgpslayer_pa_t_kernel(
         bnat = small.tile([P, 8], F32, name="bnat")
         nc.gpsimd.tensor_tensor(out=bnat[:], in0=dem[:], in1=mhalf[:], op=ALU.pow)
         for h in range(2):
-            b_ps = psum.tile([P, 4, P], F32, tag="pa", bufs=2, name="b_ps")
+            b_ps = psum.tile([P, 4, P], F32, tag="px", bufs=4, name="b_ps")
             for k in range(4):
                 j = 4 * h + k
                 nc.tensor.transpose(
@@ -180,25 +180,29 @@ def tile_hypergraphgpslayer_pa_t_kernel(
             dst = b_all[:, 512 * h : 512 * h + 512]
             nc.vector.tensor_copy(out=dst, in_=b_ps[:].rearrange("p k m -> p (k m)"))
 
-        bnt_ps = psum.tile([P, P], BF16, tag="pd", name="bnt_ps")
+        bnt_ps = psum.tile([P, P], BF16, tag="py", bufs=4, name="bnt_ps")
         nc.tensor.transpose(bnt_ps[:], bn_rows[:], ident_bf[:])
         nc.vector.tensor_scalar(
             out=ccol[:], in0=bnt_ps[:, 0:4], scalar1=gcol[:], scalar2=None, op0=ALU.mult
         )
         for k in range(2):
-            gb_ps = psum.tile([P, DIM], F32, tag="pd", name="gb_ps")
+            gb_ps = psum.tile([P, DIM], F32, tag="py", bufs=4, name="gb_ps")
             nc.tensor.matmul(out=gb_ps[:], lhsT=ones_m[:], rhs=vecs[:, k, :], start=True, stop=True)
             nc.scalar.copy(out=gb[:, k, :], in_=gb_ps[:])
 
         htg = {}
         hq = {}
         msgs = {}
+        mqs = {}
         vts = {}
         ys = {}
         stat = {}
 
+        def live(c):
+            return 0 <= c < N_CHUNKS
+
         def scale(c):
-            if c >= N_CHUNKS:
+            if not live(c):
                 return
             for a in range(A):
                 if c < 2 and a in PLANES_ON_SCALAR:
@@ -220,7 +224,7 @@ def tile_hypergraphgpslayer_pa_t_kernel(
                 )
 
         def turn(c):
-            if c >= N_CHUNKS:
+            if not live(c):
                 return
             t = work.tile([P, 2, CHUNK, 4], BF16, tag="htg", name="htg", align_bytes=64)
             htg[c] = t
@@ -231,7 +235,7 @@ def tile_hypergraphgpslayer_pa_t_kernel(
                 .rearrange("p (g n u) -> p g n u", g=2, n=CHUNK, u=2)
             )
             for a in range(A):
-                tp = psum.tile([P, 4, P], F32, tag=("pd", "pe")[a % 2], name="tp")
+                tp = psum.tile([P, 4, P], F32, tag="px", bufs=4, name="tp")
                 hw = hc[c][:, a, :].bitcast(F32)
                 for wb in range(4):
                     nc.tensor.transpose(tp[:, wb, :], hw[:, P * wb : P * wb + P], ident[:])
@@ -241,7 +245,7 @@ def tile_hypergraphgpslayer_pa_t_kernel(
                 )
 
         def quant_h(c):
-            if c >= N_CHUNKS:
+            if not live(c):
                 return
             hcod = work.tile([P, 2, CHUNK], U32, name="hcod", align_bytes=64)
             hsc = work.tile([P, 2, CHUNK], U8, name="hsc", align_bytes=64)
@@ -253,13 +257,13 @@ def tile_hypergraphgpslayer_pa_t_kernel(
             hq[c] = (hcod, hsc)
 
         def first_product(c):
-            if c >= N_CHUNKS:
+            if not live(c):
                 return
             hcod, hsc = hq[c]
             msgg = work.tile([P, CHUNK, 4], BF16, tag="msgg", name="msgg", align_bytes=64)
             for a in range(A):
                 cols = slice(P * a, P * a + P)
-                m1 = psum.tile([P, 4, P], F32, tag="pc", bufs=2, name="m1")
+                m1 = psum.tile([P, 4, P], F32, tag="px", bufs=4, name="m1")
                 for tb in range(4):
                     for g in range(2):
                         nc.tensor.matmul_mx(
@@ -272,14 +276,14 @@ def tile_hypergraphgpslayer_pa_t_kernel(
                             stop=(g == 1),
                         )
                 m1_v = m1[:].rearrange("p t n -> p n t")
-                if a == A - 1:
+                if a == 0 and c % 2 == 1:
                     nc.vector.tensor_copy(out=msgg[:, cols, :], in_=m1_v)
                 else:
                     nc.scalar.copy(out=msgg[:, cols, :], in_=m1_v)
             msgs[c] = msgg
 
-        def second_product(c):
-            if c < 0 or c >= N_CHUNKS:
+        def quant_m(c):
+            if not live(c):
                 return
             mcod = work.tile([P, CHUNK], U32, name="mcod", align_bytes=64)
             msc = work.tile([P, CHUNK], U8, name="msc", align_bytes=64)
@@ -288,9 +292,15 @@ def tile_hypergraphgpslayer_pa_t_kernel(
                 scales=msc[:],
                 in_=msgs[c][:].rearrange("p n t -> p (n t)"),
             )
+            mqs[c] = (mcod, msc)
+
+        def second_product(c):
+            if not live(c):
+                return
+            mcod, msc = mqs[c]
             vt = work.tile([P, 4, CHUNK], F32, tag="vt", name="vt", align_bytes=64)
             for db in range(4):
-                u_ps = psum.tile([P, CHUNK], F32, tag="pb", bufs=2, name="u_ps")
+                u_ps = psum.tile([P, CHUNK], F32, tag="py", bufs=4, name="u_ps")
                 nc.tensor.matmul_mx(
                     out=u_ps[:],
                     lhsT=wcod[:, P * db : P * db + P].bitcast(FP8X4),
@@ -310,18 +320,21 @@ def tile_hypergraphgpslayer_pa_t_kernel(
             vts[c] = vt
 
         def residual(c):
-            if c < 0 or c >= N_CHUNKS:
+            if not live(c):
                 return
             y = big.tile([P, A, DIM], F32, tag="big%d" % c, name="y%d" % c, align_bytes=64)
             sy = small.tile([P, A], F32, name="sy")
+            y_ps = []
             for a in range(A):
-                y_ps = psum.tile([P, DIM], F32, tag="pa", bufs=2, name="y_ps")
+                t = psum.tile([P, DIM], F32, tag="py", bufs=4, name="y_ps")
                 nc.tensor.matmul(
-                    out=y_ps[:], lhsT=ident_bf[:], rhs=x0cs[c][:, a, :], start=True, stop=False
+                    out=t[:], lhsT=ident_bf[:], rhs=x0cs[c][:, a, :], start=True, stop=False
                 )
+                y_ps.append(t)
+            for a in range(A):
                 for db in range(4):
                     nc.tensor.matmul(
-                        out=y_ps[:, P * db : P * db + P],
+                        out=y_ps[a][:, P * db : P * db + P],
                         lhsT=vts[c][:, db, P * a : P * a + P],
                         rhs=ident[:],
                         is_transpose=True,
@@ -329,27 +342,17 @@ def tile_hypergraphgpslayer_pa_t_kernel(
                         stop=(db == 3),
                     )
                 nc.scalar.activation(
-                    out=y[:, a, :], in_=y_ps[:], func=ACT.Copy, accum_out=sy[:, a : a + 1]
+                    out=y[:, a, :], in_=y_ps[a][:], func=ACT.Copy, accum_out=sy[:, a : a + 1]
                 )
-            ys[c] = y
-            stat[c] = [sy]
-
-        def neg_mean(c):
-            if c < 0 or c >= N_CHUNKS:
-                return
             nm = small.tile([P, A], F32, name="nm")
             nc.gpsimd.tensor_scalar(
-                out=nm[:],
-                in0=stat[c][0][:],
-                scalar1=-1.0 / DIM,
-                scalar2=0.0,
-                op0=ALU.mult,
-                op1=ALU.add,
+                out=nm[:], in0=sy[:], scalar1=-1.0 / DIM, scalar2=0.0, op0=ALU.mult, op1=ALU.add
             )
-            stat[c].append(nm)
+            ys[c] = y
+            stat[c] = [sy, nm]
 
         def squares(c):
-            if c < 0 or c >= N_CHUNKS:
+            if not live(c):
                 return
             ss = small.tile([P, A], F32, name="ss")
             for a in range(A):
@@ -376,7 +379,7 @@ def tile_hypergraphgpslayer_pa_t_kernel(
             stat[c].append(rs)
 
         def gain_shift(c, tiles):
-            if c < 0 or c >= N_CHUNKS:
+            if not live(c):
                 return
             y = ys[c]
             for a in tiles:
@@ -399,37 +402,45 @@ def tile_hypergraphgpslayer_pa_t_kernel(
                 )
 
         def store(c):
-            if c < 0 or c >= N_CHUNKS:
+            if not live(c):
                 return
             nc.sync.dma_start(
                 out=out[c * CHUNK : (c + 1) * CHUNK, :].rearrange("(p a) d -> p a d", a=A),
                 in_=ys[c][:],
             )
 
-        scale(0)
-        turn(0)
-        scale(1)
-        nc.vector.quantize_mx(
-            out=x1cod[:].rearrange("p g d -> p (g d)").bitcast(FP8X4),
-            scales=x1sc[:].rearrange("p g d -> p (g d)"),
-            in_=x1g[:].rearrange("p g d t -> p (g d t)"),
-        )
-        nc.scalar.copy(out=wg[:], in_=wraw[:].rearrange("p t n -> p n t"))
-        nc.vector.quantize_mx(
-            out=wcod[:].bitcast(FP8X4),
-            scales=wsc[:],
-            in_=wg[:].rearrange("p n t -> p (n t)"),
-        )
-        for i in range(N_CHUNKS + 4):
-            second_product(i - 1)
-            quant_h(i)
-            squares(i - 2)
-            turn(i + 1)
-            residual(i - 1)
-            first_product(i)
-            gain_shift(i - 4, (0, 1))
-            neg_mean(i - 1)
-            scale(i + 2)
-            gain_shift(i - 4, (2, 3))
-            store(i - 4)
-            load_x0(i + 2)
+        with tc.manual_schedule(
+            engines={mybir.EngineType.PE, mybir.EngineType.Activation, mybir.EngineType.DVE}
+        ):
+            scale(0)
+            turn(0)
+            quant_h(0)
+            nc.vector.quantize_mx(
+                out=x1cod[:].rearrange("p g d -> p (g d)").bitcast(FP8X4),
+                scales=x1sc[:].rearrange("p g d -> p (g d)"),
+                in_=x1g[:].rearrange("p g d t -> p (g d t)"),
+            )
+            scale(1)
+            first_product(0)
+            nc.scalar.copy(out=wg[:], in_=wraw[:].rearrange("p t n -> p n t"))
+            nc.vector.quantize_mx(
+                out=wcod[:].bitcast(FP8X4),
+                scales=wsc[:],
+                in_=wg[:].rearrange("p n t -> p (n t)"),
+            )
+            quant_m(0)
+            for i in range(N_CHUNKS + 1):
+                turn(i + 1)
+                second_product(i)
+                quant_h(i + 1)
+                squares(i - 1)
+                scale(i + 2)
+                gain_shift(i - 2, (3,))
+                store(i - 2)
+                first_product(i + 1)
+                residual(i)
+                quant_m(i + 1)
+                gain_shift(i - 1, (0, 1, 2))
+                load_x0(i + 2)
+            gain_shift(N_CHUNKS - 1, (3,))
+            store(N_CHUNKS - 1)

@@ -65,17 +65,15 @@ def tile_hypergraphgpslayer_pa_t_kernel(
         wcod = const.tile([P, DIM], U32, align_bytes=64)
         wsc = const.tile([P, DIM], U8, align_bytes=64)
         b_all = const.tile([P, N_EDGES], F32)
-        gb = const.tile([P, 2, DIM], F32)
         ccol = const.tile([P, 4], F32)
 
         hc = []
 
         def load_h(c):
             t = big.tile([P, A, N_EDGES], BF16, tag="big%d" % c, name="hc%d" % c, align_bytes=64)
-            nc.sync.dma_start(
-                out=t[:],
-                in_=incidence_1[c * CHUNK : (c + 1) * CHUNK, :].rearrange("(p a) e -> p a e", a=A),
-            )
+            src = incidence_1[c * CHUNK : (c + 1) * CHUNK, :].rearrange("(p a) e -> p a e", a=A)
+            for a0, a1 in ((0, 2), (2, 4)) if c == N_CHUNKS - 1 else ((0, 4),):
+                nc.sync.dma_start(out=t[:, a0:a1], in_=src[:, a0:a1])
             hc.append(t)
 
         for c in range(N_CHUNKS):
@@ -106,16 +104,17 @@ def tile_hypergraphgpslayer_pa_t_kernel(
         avs = {}
 
         def col_sums(c):
-            for j in range(8):
-                col = (c * 8 + j) * NW
-                for a in range(A):
-                    nc.tensor.matmul(
-                        out=de_ps[:, col : col + NW],
-                        lhsT=hc[c][:, a, P * j : P * j + P],
-                        rhs=ones_w[:],
-                        start=(a == 0),
-                        stop=(a == A - 1),
-                    )
+            for g, (a0, a1) in enumerate(((0, 2), (2, 4)) if c == N_CHUNKS - 1 else ((0, 4),)):
+                for j in range(8):
+                    col = ((c + g) * 8 + j) * NW
+                    for a in range(a0, a1):
+                        nc.tensor.matmul(
+                            out=de_ps[:, col : col + NW],
+                            lhsT=hc[c][:, a, P * j : P * j + P],
+                            rhs=ones_w[:],
+                            start=(a == a0),
+                            stop=(a == a1 - 1),
+                        )
 
         def row_sums(c):
             dv = small.tile([P, A], F32, name="dv")
@@ -152,44 +151,6 @@ def tile_hypergraphgpslayer_pa_t_kernel(
             col_sums(c)
             row_sums(c)
 
-        for g in range(2):
-            nc.scalar.copy(
-                out=x1g[:, g], in_=x1raw[:, 4 * g : 4 * g + 4, :].rearrange("p t d -> p d t")
-            )
-
-        de = small.tile([P, 8], F32, name="de")
-        nc.vector.tensor_reduce(
-            out=de[:],
-            in_=de_ps[:, 0 : N_CHUNKS * 8 * NW].rearrange(
-                "p (c j w) -> p j c w", c=N_CHUNKS, j=8, w=NW
-            )[:, :, :, 0],
-            axis=AX.X,
-            op=ALU.add,
-        )
-        dem = small.tile([P, 8], F32, name="dem")
-        nc.vector.tensor_scalar_max(out=dem[:], in0=de[:], scalar1=1.0)
-        bnat = small.tile([P, 8], F32, name="bnat")
-        nc.gpsimd.tensor_tensor(out=bnat[:], in0=dem[:], in1=mhalf[:], op=ALU.pow)
-        for h in range(2):
-            b_ps = psum.tile([P, 4, P], F32, tag="px", bufs=4, name="b_ps")
-            for k in range(4):
-                j = 4 * h + k
-                nc.tensor.transpose(
-                    b_ps[:, k, :], bnat[:, j : j + 1].to_broadcast([P, P]), ident[:]
-                )
-            dst = b_all[:, 512 * h : 512 * h + 512]
-            nc.vector.tensor_copy(out=dst, in_=b_ps[:].rearrange("p k m -> p (k m)"))
-
-        bnt_ps = psum.tile([P, P], BF16, tag="py", bufs=4, name="bnt_ps")
-        nc.tensor.transpose(bnt_ps[:], bn_rows[:], ident_bf[:])
-        nc.vector.tensor_scalar(
-            out=ccol[:], in0=bnt_ps[:, 0:4], scalar1=gcol[:], scalar2=None, op0=ALU.mult
-        )
-        for k in range(2):
-            gb_ps = psum.tile([P, DIM], F32, tag="py", bufs=4, name="gb_ps")
-            nc.tensor.matmul(out=gb_ps[:], lhsT=ones_m[:], rhs=vecs[:, k, :], start=True, stop=True)
-            nc.scalar.copy(out=gb[:, k, :], in_=gb_ps[:])
-
         htg = {}
         hq = {}
         msgs = {}
@@ -201,27 +162,35 @@ def tile_hypergraphgpslayer_pa_t_kernel(
         def live(c):
             return 0 <= c < N_CHUNKS
 
-        def scale(c):
+        abt = {}
+
+        def planes(c, tiles):
             if not live(c):
                 return
-            for a in range(A):
-                if c < 2 and a in PLANES_ON_SCALAR:
-                    ab = work.tile([P, N_EDGES], BF16, name="ab")
-                    nc.scalar.activation(
-                        out=ab[:], in_=b_all[:], func=ACT.Copy, scale=avs[c][:, a : a + 1]
-                    )
-                    nc.vector.tensor_tensor(
-                        out=hc[c][:, a, :], in0=hc[c][:, a, :], in1=ab[:], op=ALU.mult
-                    )
-                    continue
-                nc.vector.scalar_tensor_tensor(
-                    out=hc[c][:, a, :],
-                    in0=hc[c][:, a, :],
-                    scalar=avs[c][:, a : a + 1],
-                    in1=b_all[:],
-                    op0=ALU.mult,
-                    op1=ALU.mult,
+            if c not in abt:
+                abt[c] = work.tile([P, A, N_EDGES], BF16, name="ab", bufs=1)
+            for a in tiles:
+                nc.scalar.activation(
+                    out=abt[c][:, a, :], in_=b_all[:], func=ACT.Copy, scale=avs[c][:, a : a + 1]
                 )
+
+        def scale(c, tiles=(0, 1, 2, 3)):
+            if not live(c):
+                return
+            for a in tiles:
+                if (c < 2 and a in PLANES_ON_SCALAR):
+                    nc.vector.tensor_tensor(
+                        out=hc[c][:, a, :], in0=hc[c][:, a, :], in1=abt[c][:, a, :], op=ALU.mult
+                    )
+                else:
+                    nc.vector.scalar_tensor_tensor(
+                        out=hc[c][:, a, :],
+                        in0=hc[c][:, a, :],
+                        scalar=avs[c][:, a : a + 1],
+                        in1=b_all[:],
+                        op0=ALU.mult,
+                        op1=ALU.mult,
+                    )
 
         def turn(c):
             if not live(c):
@@ -256,12 +225,13 @@ def tile_hypergraphgpslayer_pa_t_kernel(
             )
             hq[c] = (hcod, hsc)
 
-        def first_product(c):
+        m1s = {}
+
+        def first_product(c, tiles):
             if not live(c):
                 return
             hcod, hsc = hq[c]
-            msgg = work.tile([P, CHUNK, 4], BF16, tag="msgg", name="msgg", align_bytes=64)
-            for a in range(A):
+            for a in tiles:
                 cols = slice(P * a, P * a + P)
                 m1 = psum.tile([P, 4, P], F32, tag="px", bufs=4, name="m1")
                 for tb in range(4):
@@ -275,12 +245,15 @@ def tile_hypergraphgpslayer_pa_t_kernel(
                             start=(g == 0),
                             stop=(g == 1),
                         )
-                m1_v = m1[:].rearrange("p t n -> p n t")
-                if a == 0 and c % 2 == 1:
-                    nc.vector.tensor_copy(out=msgg[:, cols, :], in_=m1_v)
-                else:
-                    nc.scalar.copy(out=msgg[:, cols, :], in_=m1_v)
-            msgs[c] = msgg
+                m1s[c, a] = m1
+
+        def message(c, a):
+            if not live(c):
+                return
+            if c not in msgs:
+                msgs[c] = work.tile([P, CHUNK, 4], BF16, tag="msgg", name="msgg", align_bytes=64)
+            copy = nc.vector.tensor_copy if c >= N_CHUNKS - 2 and a < 2 else nc.scalar.copy
+            copy(out=msgs[c][:, P * a : P * a + P, :], in_=m1s[c, a][:].rearrange("p t n -> p n t"))
 
         def quant_m(c):
             if not live(c):
@@ -319,22 +292,28 @@ def tile_hypergraphgpslayer_pa_t_kernel(
                 )
             vts[c] = vt
 
-        def residual(c):
+        yps = {}
+
+        def residual_x(c):
             if not live(c):
                 return
-            y = big.tile([P, A, DIM], F32, tag="big%d" % c, name="y%d" % c, align_bytes=64)
-            sy = small.tile([P, A], F32, name="sy")
-            y_ps = []
             for a in range(A):
                 t = psum.tile([P, DIM], F32, tag="py", bufs=4, name="y_ps")
                 nc.tensor.matmul(
                     out=t[:], lhsT=ident_bf[:], rhs=x0cs[c][:, a, :], start=True, stop=False
                 )
-                y_ps.append(t)
-            for a in range(A):
+                yps[c, a] = t
+
+        def residual_u(c, tiles=(0, 1, 2, 3)):
+            if not live(c):
+                return
+            if c not in ys:
+                ys[c] = big.tile([P, A, DIM], F32, tag="big%d" % c, name="y%d" % c, align_bytes=64)
+                stat[c] = [small.tile([P, A], F32, name="s%d" % q) for q in range(4)]
+            for a in tiles:
                 for db in range(4):
                     nc.tensor.matmul(
-                        out=y_ps[a][:, P * db : P * db + P],
+                        out=yps[c, a][:, P * db : P * db + P],
                         lhsT=vts[c][:, db, P * a : P * a + P],
                         rhs=ident[:],
                         is_transpose=True,
@@ -342,20 +321,27 @@ def tile_hypergraphgpslayer_pa_t_kernel(
                         stop=(db == 3),
                     )
                 nc.scalar.activation(
-                    out=y[:, a, :], in_=y_ps[a][:], func=ACT.Copy, accum_out=sy[:, a : a + 1]
+                    out=ys[c][:, a, :],
+                    in_=yps[c, a][:],
+                    func=ACT.Copy,
+                    accum_out=stat[c][0][:, a : a + 1],
                 )
-            nm = small.tile([P, A], F32, name="nm")
-            nc.gpsimd.tensor_scalar(
-                out=nm[:], in0=sy[:], scalar1=-1.0 / DIM, scalar2=0.0, op0=ALU.mult, op1=ALU.add
-            )
-            ys[c] = y
-            stat[c] = [sy, nm]
 
-        def squares(c):
+        def neg_mean(c, a0, a1):
+            if live(c):
+                nc.gpsimd.tensor_scalar(
+                    out=stat[c][1][:, a0:a1],
+                    in0=stat[c][0][:, a0:a1],
+                    scalar1=-1.0 / DIM,
+                    scalar2=0.0,
+                    op0=ALU.mult,
+                    op1=ALU.add,
+                )
+
+        def squares(c, tiles=(0, 1, 2, 3)):
             if not live(c):
                 return
-            ss = small.tile([P, A], F32, name="ss")
-            for a in range(A):
+            for a in tiles:
                 junk = work.tile([P, DIM], BF16, name="junk")
                 nc.scalar.activation(
                     out=junk[:],
@@ -363,20 +349,24 @@ def tile_hypergraphgpslayer_pa_t_kernel(
                     func=ACT.Square,
                     bias=stat[c][0][:, a : a + 1],
                     scale=-float(DIM),
-                    accum_out=ss[:, a : a + 1],
+                    accum_out=stat[c][2][:, a : a + 1],
                 )
+
+        def inv_std(c, a0, a1):
+            if not live(c):
+                return
             vv = small.tile([P, A], F32, name="vv")
             nc.gpsimd.tensor_scalar(
-                out=vv[:],
-                in0=ss[:],
+                out=vv[:, a0:a1],
+                in0=stat[c][2][:, a0:a1],
                 scalar1=1.0 / DIM**3,
                 scalar2=LN_EPS,
                 op0=ALU.mult,
                 op1=ALU.add,
             )
-            rs = small.tile([P, A], F32, name="rs")
-            nc.gpsimd.tensor_tensor(out=rs[:], in0=vv[:], in1=mhalf[:, 0:A], op=ALU.pow)
-            stat[c].append(rs)
+            nc.gpsimd.tensor_tensor(
+                out=stat[c][3][:, a0:a1], in0=vv[:, a0:a1], in1=mhalf[:, a0:a1], op=ALU.pow
+            )
 
         def gain_shift(c, tiles):
             if not live(c):
@@ -395,52 +385,127 @@ def tile_hypergraphgpslayer_pa_t_kernel(
                 nc.vector.scalar_tensor_tensor(
                     out=y[:, a, :],
                     in0=y[:, a, :],
-                    scalar=stat[c][2][:, a : a + 1],
+                    scalar=stat[c][3][:, a : a + 1],
                     in1=gb[:, 1, :],
                     op0=ALU.mult,
                     op1=ALU.add,
                 )
 
-        def store(c):
+        def store(c, a0=0, a1=A):
             if not live(c):
                 return
             nc.sync.dma_start(
-                out=out[c * CHUNK : (c + 1) * CHUNK, :].rearrange("(p a) d -> p a d", a=A),
-                in_=ys[c][:],
+                out=out[c * CHUNK : (c + 1) * CHUNK, :].rearrange("(p a) d -> p a d", a=A)[:, a0:a1],
+                in_=ys[c][:, a0:a1],
             )
 
         with tc.manual_schedule(
-            engines={mybir.EngineType.PE, mybir.EngineType.Activation, mybir.EngineType.DVE}
+            engines={
+                mybir.EngineType.PE,
+                mybir.EngineType.Activation,
+                mybir.EngineType.DVE,
+                mybir.EngineType.Pool,
+            }
         ):
+            de = small.tile([P, 8], F32, name="de")
+            nc.vector.tensor_reduce(
+                out=de[:],
+                in_=de_ps[:, 0 : (N_CHUNKS + 1) * 8 * NW].rearrange(
+                    "p (c j w) -> p j c w", c=N_CHUNKS + 1, j=8, w=NW
+                )[:, :, :, 0],
+                axis=AX.X,
+                op=ALU.add,
+            )
+            dem = small.tile([P, 8], F32, name="dem")
+            nc.vector.tensor_scalar_max(out=dem[:], in0=de[:], scalar1=1.0)
+            bnat = small.tile([P, 8], F32, name="bnat")
+            nc.gpsimd.tensor_tensor(out=bnat[:], in0=dem[:], in1=mhalf[:], op=ALU.pow)
+            nc.gpsimd.tensor_scalar(
+                out=wg[:],
+                in0=wraw[:].rearrange("p t n -> p n t"),
+                scalar1=1.0,
+                scalar2=0.0,
+                op0=ALU.mult,
+                op1=ALU.add,
+            )
+            nc.scalar.copy(out=x1g[:, 0], in_=x1raw[:, 0:4, :].rearrange("p t d -> p d t"))
+            nc.vector.tensor_copy(out=x1g[:, 1], in_=x1raw[:, 4:8, :].rearrange("p t d -> p d t"))
+            bnt_ps = psum.tile([P, P], BF16, tag="py", bufs=4, name="bnt_ps")
+            nc.tensor.transpose(bnt_ps[:], bn_rows[:], ident_bf[:])
+            nc.vector.tensor_scalar(
+                out=ccol[:], in0=bnt_ps[:, 0:4], scalar1=gcol[:], scalar2=None, op0=ALU.mult
+            )
+            gb = const.tile([P, 2, DIM], F32)
+            for k in range(2):
+                gb_ps = psum.tile([P, DIM], F32, tag="py", bufs=4, name="gb_ps")
+                nc.tensor.matmul(out=gb_ps[:], lhsT=ones_m[:], rhs=vecs[:, k, :], start=True, stop=True)
+                nc.scalar.copy(out=gb[:, k, :], in_=gb_ps[:])
+            for h in range(2):
+                b_ps = psum.tile([P, 4, P], F32, tag="px", bufs=4, name="b_ps")
+                for k in range(4):
+                    j = 4 * h + k
+                    nc.tensor.transpose(
+                        b_ps[:, k, :], bnat[:, j : j + 1].to_broadcast([P, P]), ident[:]
+                    )
+                dst = b_all[:, 512 * h : 512 * h + 512]
+                nc.vector.tensor_copy(out=dst, in_=b_ps[:].rearrange("p k m -> p (k m)"))
+
+            planes(0, PLANES_ON_SCALAR)
             scale(0)
             turn(0)
-            quant_h(0)
             nc.vector.quantize_mx(
                 out=x1cod[:].rearrange("p g d -> p (g d)").bitcast(FP8X4),
                 scales=x1sc[:].rearrange("p g d -> p (g d)"),
                 in_=x1g[:].rearrange("p g d t -> p (g d t)"),
             )
-            scale(1)
-            first_product(0)
-            nc.scalar.copy(out=wg[:], in_=wraw[:].rearrange("p t n -> p n t"))
+            planes(1, PLANES_ON_SCALAR)
+            scale(1, (0,))
+            quant_h(0)
+            scale(1, (1, 2, 3))
+            first_product(0, range(A))
             nc.vector.quantize_mx(
                 out=wcod[:].bitcast(FP8X4),
                 scales=wsc[:],
                 in_=wg[:].rearrange("p n t -> p (n t)"),
             )
+            scale(2, (0,))
+            for a in range(A):
+                message(0, a)
             quant_m(0)
-            for i in range(N_CHUNKS + 1):
+            for i in range(N_CHUNKS):
                 turn(i + 1)
                 second_product(i)
+                if i == 0:
+                    scale(2, (1,))
                 quant_h(i + 1)
                 squares(i - 1)
-                scale(i + 2)
+                inv_std(i - 1, 0, A)
+                if i == 0:
+                    scale(2, (2, 3))
+                else:
+                    scale(i + 3)
                 gain_shift(i - 2, (3,))
                 store(i - 2)
-                first_product(i + 1)
-                residual(i)
+                first_product(i + 1, range(A))
+                for a in range(A):
+                    message(i + 1, a)
+                residual_x(i)
+                if i < N_CHUNKS - 1:
+                    residual_u(i)
+                    neg_mean(i, 0, A)
+                else:
+                    for a in (0, 2):
+                        residual_u(i, (a, a + 1))
+                        neg_mean(i, a, a + 2)
+                        squares(i, (a, a + 1))
+                        inv_std(i, a, a + 2)
                 quant_m(i + 1)
                 gain_shift(i - 1, (0, 1, 2))
+                if i == 0:
+                    scale(3)
                 load_x0(i + 2)
-            gain_shift(N_CHUNKS - 1, (3,))
-            store(N_CHUNKS - 1)
+            gain_shift(N_CHUNKS - 2, (3,))
+            store(N_CHUNKS - 2)
+            for a in (0, 2):
+                gain_shift(N_CHUNKS - 1, (a, a + 1))
+                store(N_CHUNKS - 1, a, a + 2)

@@ -22,6 +22,7 @@ A = 4
 CHUNK = P * A
 N_CHUNKS = N_NODES // CHUNK
 LN_EPS = 1e-5
+WARM = 10
 NW = 2
 ROWS_ON_SCALAR = (3,)
 PLANES_ON_SCALAR = (1, 3)
@@ -234,6 +235,16 @@ def tile_hypergraphgpslayer_pa_t_kernel(
             for a in tiles:
                 cols = slice(P * a, P * a + P)
                 m1 = psum.tile([P, 4, P], F32, tag="px", bufs=4, name="m1")
+                for q in range(WARM if a == 0 else 0):
+                    nc.tensor.matmul_mx(
+                        out=m1[:].rearrange("p t n -> p (t n)"),
+                        lhsT=x1cod[:, 0, 0:P].bitcast(FP8X4),
+                        lhsT_scale=x1sc[:, 0, 0:P],
+                        rhs=x1cod[:, 1, :].bitcast(FP8X4),
+                        rhs_scale=x1sc[:, 1, :],
+                        start=True,
+                        stop=True,
+                    )
                 for tb in range(4):
                     for g in range(2):
                         nc.tensor.matmul_mx(

@@ -23,6 +23,7 @@ CHUNK = P * A
 N_CHUNKS = N_NODES // CHUNK
 LN_EPS = 1e-5
 WARM = 10
+W_LOAD = 6
 NW = 2
 ROWS_ON_SCALAR = (3,)
 PLANES_ON_SCALAR = (1, 3)
@@ -77,16 +78,17 @@ def tile_hypergraphgpslayer_pa_t_kernel(
                 nc.sync.dma_start(out=t[:, a0:a1], in_=src[:, a0:a1])
             hc.append(t)
 
-        for c in range(N_CHUNKS):
+        for c in range(W_LOAD):
+            load_h(c)
+        wraw = work.tile([P, 4, DIM], BF16, tag="msgg", name="wraw", align_bytes=64)
+        nc.sync.dma_start(out=wraw[:], in_=Wn.rearrange("(t p) n -> p t n", p=P))
+        for c in range(W_LOAD, N_CHUNKS):
             load_h(c)
         x1raw = work.tile([P, 8, DIM], BF16, tag="htg", name="x1raw", align_bytes=64)
         nc.sync.dma_start(
             out=x1raw[:].rearrange("p (w e) d -> p w (e d)", e=2),
             in_=x_1_new.rearrange("(w p e) d -> p w (e d)", w=4, p=P, e=2),
         )
-        wraw = work.tile([P, 4, DIM], BF16, tag="msgg", name="wraw", align_bytes=64)
-        nc.sync.dma_start(out=wraw[:], in_=Wn.rearrange("(t p) n -> p t n", p=P))
-
         x0cs = {}
 
         def load_x0(c):
@@ -151,6 +153,21 @@ def tile_hypergraphgpslayer_pa_t_kernel(
         for c in range(N_CHUNKS):
             col_sums(c)
             row_sums(c)
+            if c == W_LOAD:
+                nc.gpsimd.tensor_scalar(
+                    out=wg[:],
+                    in0=wraw[:].rearrange("p t n -> p n t"),
+                    scalar1=1.0,
+                    scalar2=0.0,
+                    op0=ALU.mult,
+                    op1=ALU.add,
+                )
+            if c == W_LOAD + 3:
+                nc.vector.quantize_mx(
+                    out=wcod[:].bitcast(FP8X4),
+                    scales=wsc[:],
+                    in_=wg[:].rearrange("p n t -> p (n t)"),
+                )
 
         htg = {}
         hq = {}
@@ -340,13 +357,11 @@ def tile_hypergraphgpslayer_pa_t_kernel(
 
         def neg_mean(c, a0, a1):
             if live(c):
-                nc.gpsimd.tensor_scalar(
+                nc.scalar.activation(
                     out=stat[c][1][:, a0:a1],
-                    in0=stat[c][0][:, a0:a1],
-                    scalar1=-1.0 / DIM,
-                    scalar2=0.0,
-                    op0=ALU.mult,
-                    op1=ALU.add,
+                    in_=stat[c][0][:, a0:a1],
+                    func=ACT.Copy,
+                    scale=-1.0 / DIM,
                 )
 
         def squares(c, tiles=(0, 1, 2, 3)):
@@ -364,22 +379,16 @@ def tile_hypergraphgpslayer_pa_t_kernel(
                 )
 
         def inv_std(c, a0, a1):
-            if not live(c):
-                return
-            vv = small.tile([P, A], F32, name="vv")
-            nc.gpsimd.tensor_scalar(
-                out=vv[:, a0:a1],
-                in0=stat[c][2][:, a0:a1],
-                scalar1=1.0 / DIM**3,
-                scalar2=LN_EPS,
-                op0=ALU.mult,
-                op1=ALU.add,
-            )
-            nc.gpsimd.tensor_tensor(
-                out=stat[c][3][:, a0:a1], in0=vv[:, a0:a1], in1=mhalf[:, a0:a1], op=ALU.pow
-            )
+            if live(c):
+                nc.scalar.activation(
+                    out=stat[c][3][:, a0:a1],
+                    in_=stat[c][2][:, a0:a1],
+                    func=ACT.Abs_reciprocal_sqrt,
+                    scale=1.0 / DIM**3,
+                    bias=LN_EPS,
+                )
 
-        def gain_shift(c, tiles):
+        def gain(c, tiles):
             if not live(c):
                 return
             y = ys[c]
@@ -392,6 +401,11 @@ def tile_hypergraphgpslayer_pa_t_kernel(
                     op0=ALU.add,
                     op1=ALU.mult,
                 )
+
+        def shift(c, tiles):
+            if not live(c):
+                return
+            y = ys[c]
             for a in tiles:
                 nc.vector.scalar_tensor_tensor(
                     out=y[:, a, :],
@@ -431,14 +445,6 @@ def tile_hypergraphgpslayer_pa_t_kernel(
             nc.vector.tensor_scalar_max(out=dem[:], in0=de[:], scalar1=1.0)
             bnat = small.tile([P, 8], F32, name="bnat")
             nc.gpsimd.tensor_tensor(out=bnat[:], in0=dem[:], in1=mhalf[:], op=ALU.pow)
-            nc.gpsimd.tensor_scalar(
-                out=wg[:],
-                in0=wraw[:].rearrange("p t n -> p n t"),
-                scalar1=1.0,
-                scalar2=0.0,
-                op0=ALU.mult,
-                op1=ALU.add,
-            )
             nc.scalar.copy(out=x1g[:, 0], in_=x1raw[:, 0:4, :].rearrange("p t d -> p d t"))
             nc.vector.tensor_copy(out=x1g[:, 1], in_=x1raw[:, 4:8, :].rearrange("p t d -> p d t"))
             bnt_ps = psum.tile([P, P], BF16, tag="py", bufs=4, name="bnt_ps")
@@ -474,11 +480,6 @@ def tile_hypergraphgpslayer_pa_t_kernel(
             quant_h(0)
             scale(1, (1, 2, 3))
             first_product(0, range(A))
-            nc.vector.quantize_mx(
-                out=wcod[:].bitcast(FP8X4),
-                scales=wsc[:],
-                in_=wg[:].rearrange("p n t -> p (n t)"),
-            )
             scale(2, (0,))
             for a in range(A):
                 message(0, a)
@@ -489,34 +490,46 @@ def tile_hypergraphgpslayer_pa_t_kernel(
                 if i == 0:
                     scale(2, (1,))
                 quant_h(i + 1)
+                neg_mean(i - 1, 0, A)
                 squares(i - 1)
-                inv_std(i - 1, 0, A)
                 if i == 0:
                     scale(2, (2, 3))
                 else:
-                    scale(i + 3)
-                gain_shift(i - 2, (3,))
-                store(i - 2)
+                    scale(i + 3, (0, 1, 2))
+                    gain(i - 2, (3,))
+                    scale(i + 3, (3,))
+                    shift(i - 2, (3,))
+                    store(i - 2)
                 first_product(i + 1, range(A))
-                for a in range(A):
-                    message(i + 1, a)
+                message(i + 1, 0)
+                message(i + 1, 1)
+                message(i + 1, 2)
+                inv_std(i - 1, 0, A)
+                message(i + 1, 3)
                 residual_x(i)
                 if i < N_CHUNKS - 1:
                     residual_u(i)
-                    neg_mean(i, 0, A)
                 else:
-                    for a in (0, 2):
-                        residual_u(i, (a, a + 1))
-                        neg_mean(i, a, a + 2)
-                        squares(i, (a, a + 1))
-                        inv_std(i, a, a + 2)
+                    residual_u(i, (0, 1))
+                    squares(i, (0, 1))
+                    neg_mean(i, 0, 2)
+                    residual_u(i, (2, 3))
+                    inv_std(i, 0, 2)
+                    squares(i, (2, 3))
+                    neg_mean(i, 2, 4)
+                    inv_std(i, 2, 4)
                 quant_m(i + 1)
-                gain_shift(i - 1, (0, 1, 2))
+                gain(i - 1, (0, 1, 2))
+                shift(i - 1, (0, 1, 2))
                 if i == 0:
                     scale(3)
                 load_x0(i + 2)
-            gain_shift(N_CHUNKS - 2, (3,))
+            gain(N_CHUNKS - 2, (3,))
+            gain(N_CHUNKS - 1, (0, 1))
+            shift(N_CHUNKS - 2, (3,))
             store(N_CHUNKS - 2)
-            for a in (0, 2):
-                gain_shift(N_CHUNKS - 1, (a, a + 1))
-                store(N_CHUNKS - 1, a, a + 2)
+            shift(N_CHUNKS - 1, (0, 1))
+            store(N_CHUNKS - 1, 0, 2)
+            gain(N_CHUNKS - 1, (2, 3))
+            shift(N_CHUNKS - 1, (2, 3))
+            store(N_CHUNKS - 1, 2, 4)

@@ -22,11 +22,10 @@ A = 4
 CHUNK = P * A
 N_CHUNKS = N_NODES // CHUNK
 LN_EPS = 1e-5
-WARM = 10
-W_LOAD = 6
+WARM = 8
 NW = 2
 ROWS_ON_SCALAR = (3,)
-PLANES_ON_SCALAR = (1, 3)
+PLANES_ON_SCALAR = {0: (1, 3), 1: (1, 3)}
 
 
 def tile_hypergraphgpslayer_pa_t_kernel(
@@ -78,17 +77,16 @@ def tile_hypergraphgpslayer_pa_t_kernel(
                 nc.sync.dma_start(out=t[:, a0:a1], in_=src[:, a0:a1])
             hc.append(t)
 
-        for c in range(W_LOAD):
-            load_h(c)
-        wraw = work.tile([P, 4, DIM], BF16, tag="msgg", name="wraw", align_bytes=64)
-        nc.sync.dma_start(out=wraw[:], in_=Wn.rearrange("(t p) n -> p t n", p=P))
-        for c in range(W_LOAD, N_CHUNKS):
+        for c in range(N_CHUNKS):
             load_h(c)
         x1raw = work.tile([P, 8, DIM], BF16, tag="htg", name="x1raw", align_bytes=64)
         nc.sync.dma_start(
             out=x1raw[:].rearrange("p (w e) d -> p w (e d)", e=2),
             in_=x_1_new.rearrange("(w p e) d -> p w (e d)", w=4, p=P, e=2),
         )
+        wraw = work.tile([P, 4, DIM], BF16, tag="msgg", name="wraw", align_bytes=64)
+        nc.sync.dma_start(out=wraw[:], in_=Wn.rearrange("(t p) n -> p t n", p=P))
+
         x0cs = {}
 
         def load_x0(c):
@@ -153,21 +151,6 @@ def tile_hypergraphgpslayer_pa_t_kernel(
         for c in range(N_CHUNKS):
             col_sums(c)
             row_sums(c)
-            if c == W_LOAD:
-                nc.gpsimd.tensor_scalar(
-                    out=wg[:],
-                    in0=wraw[:].rearrange("p t n -> p n t"),
-                    scalar1=1.0,
-                    scalar2=0.0,
-                    op0=ALU.mult,
-                    op1=ALU.add,
-                )
-            if c == W_LOAD + 3:
-                nc.vector.quantize_mx(
-                    out=wcod[:].bitcast(FP8X4),
-                    scales=wsc[:],
-                    in_=wg[:].rearrange("p n t -> p (n t)"),
-                )
 
         htg = {}
         hq = {}
@@ -196,7 +179,7 @@ def tile_hypergraphgpslayer_pa_t_kernel(
             if not live(c):
                 return
             for a in tiles:
-                if (c < 2 and a in PLANES_ON_SCALAR):
+                if a in PLANES_ON_SCALAR.get(c, ()):
                     nc.vector.tensor_tensor(
                         out=hc[c][:, a, :], in0=hc[c][:, a, :], in1=abt[c][:, a, :], op=ALU.mult
                     )
@@ -280,7 +263,7 @@ def tile_hypergraphgpslayer_pa_t_kernel(
                 return
             if c not in msgs:
                 msgs[c] = work.tile([P, CHUNK, 4], BF16, tag="msgg", name="msgg", align_bytes=64)
-            copy = nc.vector.tensor_copy if c >= N_CHUNKS - 2 and a < 2 else nc.scalar.copy
+            copy = nc.vector.tensor_copy if c >= N_CHUNKS - 2 and a < 3 or 0 < c < 3 and a < 2 else nc.scalar.copy
             copy(out=msgs[c][:, P * a : P * a + P, :], in_=m1s[c, a][:].rearrange("p t n -> p n t"))
 
         def quant_m(c):
@@ -453,10 +436,11 @@ def tile_hypergraphgpslayer_pa_t_kernel(
                 out=ccol[:], in0=bnt_ps[:, 0:4], scalar1=gcol[:], scalar2=None, op0=ALU.mult
             )
             gb = const.tile([P, 2, DIM], F32)
+            gb_ps = []
             for k in range(2):
-                gb_ps = psum.tile([P, DIM], F32, tag="py", bufs=4, name="gb_ps")
-                nc.tensor.matmul(out=gb_ps[:], lhsT=ones_m[:], rhs=vecs[:, k, :], start=True, stop=True)
-                nc.scalar.copy(out=gb[:, k, :], in_=gb_ps[:])
+                t = psum.tile([P, DIM], F32, tag="py", bufs=4, name="gb_ps")
+                nc.tensor.matmul(out=t[:], lhsT=ones_m[:], rhs=vecs[:, k, :], start=True, stop=True)
+                gb_ps.append(t)
             for h in range(2):
                 b_ps = psum.tile([P, 4, P], F32, tag="px", bufs=4, name="b_ps")
                 for k in range(4):
@@ -464,10 +448,10 @@ def tile_hypergraphgpslayer_pa_t_kernel(
                     nc.tensor.transpose(
                         b_ps[:, k, :], bnat[:, j : j + 1].to_broadcast([P, P]), ident[:]
                     )
-                dst = b_all[:, 512 * h : 512 * h + 512]
-                nc.vector.tensor_copy(out=dst, in_=b_ps[:].rearrange("p k m -> p (k m)"))
+                copy = nc.vector.tensor_copy if h == 0 else nc.scalar.copy
+                copy(out=b_all[:, 512 * h : 512 * h + 512], in_=b_ps[:].rearrange("p k m -> p (k m)"))
 
-            planes(0, PLANES_ON_SCALAR)
+            planes(0, PLANES_ON_SCALAR[0])
             scale(0)
             turn(0)
             nc.vector.quantize_mx(
@@ -475,19 +459,27 @@ def tile_hypergraphgpslayer_pa_t_kernel(
                 scales=x1sc[:].rearrange("p g d -> p (g d)"),
                 in_=x1g[:].rearrange("p g d t -> p (g d t)"),
             )
-            planes(1, PLANES_ON_SCALAR)
-            scale(1, (0,))
+            planes(1, PLANES_ON_SCALAR[1])
+            for k in range(2):
+                nc.scalar.copy(out=gb[:, k, :], in_=gb_ps[k][:])
+            nc.vector.tensor_copy(out=wg[:], in_=wraw[:].rearrange("p t n -> p n t"))
             quant_h(0)
-            scale(1, (1, 2, 3))
+            scale(1)
             first_product(0, range(A))
-            scale(2, (0,))
+            nc.vector.quantize_mx(
+                out=wcod[:].bitcast(FP8X4),
+                scales=wsc[:],
+                in_=wg[:].rearrange("p n t -> p (n t)"),
+            )
             for a in range(A):
                 message(0, a)
             quant_m(0)
+            scale(2, (0,))
             for i in range(N_CHUNKS):
                 turn(i + 1)
                 second_product(i)
                 if i == 0:
+                    planes(2, PLANES_ON_SCALAR.get(2, ()))
                     scale(2, (1,))
                 quant_h(i + 1)
                 neg_mean(i - 1, 0, A)
@@ -507,6 +499,8 @@ def tile_hypergraphgpslayer_pa_t_kernel(
                 inv_std(i - 1, 0, A)
                 message(i + 1, 3)
                 residual_x(i)
+                if i == 0:
+                    planes(3, PLANES_ON_SCALAR.get(3, ()))
                 if i < N_CHUNKS - 1:
                     residual_u(i)
                 else:
@@ -518,8 +512,9 @@ def tile_hypergraphgpslayer_pa_t_kernel(
                     squares(i, (2, 3))
                     neg_mean(i, 2, 4)
                     inv_std(i, 2, 4)
+                gain(i - 1, (0,))
                 quant_m(i + 1)
-                gain(i - 1, (0, 1, 2))
+                gain(i - 1, (1, 2))
                 shift(i - 1, (0, 1, 2))
                 if i == 0:
                     scale(3)
@@ -531,5 +526,6 @@ def tile_hypergraphgpslayer_pa_t_kernel(
             shift(N_CHUNKS - 1, (0, 1))
             store(N_CHUNKS - 1, 0, 2)
             gain(N_CHUNKS - 1, (2, 3))
-            shift(N_CHUNKS - 1, (2, 3))
-            store(N_CHUNKS - 1, 2, 4)
+            for a in (2, 3):
+                shift(N_CHUNKS - 1, (a,))
+                store(N_CHUNKS - 1, a, a + 1)

from contextlib import ExitStack

import concourse.mybir as mybir
from concourse.masks import make_identity

FLOPS = 2 * 6144 * 1024 * 512 + 2 * 6144 * 512 * 512

F32 = mybir.dt.float32
BF16 = mybir.dt.bfloat16
U32 = mybir.dt.uint32
U8 = mybir.dt.uint8
FP8X4 = mybir.dt.float8_e4m3fn_x4
ALU = mybir.AluOpType
ACT = mybir.ActivationFunctionType
AX = mybir.AxisListType

P = 128
N_NODES = 6144
N_EDGES = 1024
DIM = 512
A = 4
CHUNK = P * A
N_CHUNKS = N_NODES // CHUNK
LN_EPS = 1e-5
WARM = 8
NW = 2
ROWS_ON_SCALAR = (3,)
PLANES_ON_SCALAR = {0: (1, 3), 1: (1, 3)}


def tile_hypergraphgpslayer_pa_t_kernel(
    tc, x_0, x_1_new, incidence_1, Wn, bn, ln1_g, ln1_b, gate_local, out
):
    nc = tc.nc
    with ExitStack() as ctx:
        const = ctx.enter_context(tc.tile_pool(name="const", bufs=1))
        big = ctx.enter_context(tc.tile_pool(name="big", bufs=1))
        small = ctx.enter_context(tc.tile_pool(name="small", bufs=8))
        work = ctx.enter_context(tc.tile_pool(name="work", bufs=2))
        psum = ctx.enter_context(tc.psum_pool(name="psum", bufs=1))

        ones_w = const.tile([P, NW], BF16)
        nc.vector.memset(ones_w[:], 1.0)
        ones_m = const.tile([P, P], BF16)
        nc.vector.memset(ones_m[:], 1.0)
        mhalf = const.tile([P, 8], F32)
        nc.vector.memset(mhalf[:], -0.5)
        ident = const.tile([P, P], F32)
        make_identity(nc, ident[:])
        ident_bf = const.tile([P, P], BF16)
        make_identity(nc, ident_bf[:])
        vecs = const.tile([P, 2, DIM], BF16)
        nc.vector.memset(vecs[:], 0.0)
        nc.scalar.dma_start(out=vecs[0:1, 0, :], in_=ln1_g.unsqueeze(0))
        nc.scalar.dma_start(out=vecs[0:1, 1, :], in_=ln1_b.unsqueeze(0))
        bn_rows = const.tile([P, P], BF16)
        nc.vector.memset(bn_rows[:], 0.0)
        nc.scalar.dma_start(out=bn_rows[0:4, :], in_=bn.rearrange("(r q) -> r q", q=P))
        gt = const.tile([P, 1], BF16)
        nc.scalar.dma_start(out=gt[:], in_=gate_local.partition_broadcast(P))
        gcol = const.tile([P, 1], F32)
        nc.scalar.activation(out=gcol[:], in_=gt[:], func=ACT.Tanh)

        x1cod = const.tile([P, 2, DIM], U32, align_bytes=64)
        x1sc = const.tile([P, 2, DIM], U8, align_bytes=64)
        wcod = const.tile([P, DIM], U32, align_bytes=64)
        wsc = const.tile([P, DIM], U8, align_bytes=64)
        b_all = const.tile([P, N_EDGES], F32)
        ccol = const.tile([P, 4], F32)

        hc = []

        def load_h(c):
            t = big.tile([P, A, N_EDGES], BF16, tag="big%d" % c, name="hc%d" % c, align_bytes=64)
            src = incidence_1[c * CHUNK : (c + 1) * CHUNK, :].rearrange("(p a) e -> p a e", a=A)
            for a0, a1 in ((0, 2), (2, 4)) if c == N_CHUNKS - 1 else ((0, 4),):
                nc.sync.dma_start(out=t[:, a0:a1], in_=src[:, a0:a1])
            hc.append(t)

        for c in range(N_CHUNKS):
            load_h(c)
        x1raw = work.tile([P, 8, DIM], BF16, tag="htg", name="x1raw", align_bytes=64)
        nc.sync.dma_start(
            out=x1raw[:].rearrange("p (w e) d -> p w (e d)", e=2),
            in_=x_1_new.rearrange("(w p e) d -> p w (e d)", w=4, p=P, e=2),
        )
        wraw = work.tile([P, 4, DIM], BF16, tag="msgg", name="wraw", align_bytes=64)
        nc.sync.dma_start(out=wraw[:], in_=Wn.rearrange("(t p) n -> p t n", p=P))

        x0cs = {}

        def load_x0(c):
            if c < N_CHUNKS:
                t = work.tile([P, A, DIM], BF16, name="x0c", bufs=3)
                nc.sync.dma_start(
                    out=t[:],
                    in_=x_0[c * CHUNK : (c + 1) * CHUNK, :].rearrange("(p a) d -> p a d", a=A),
                )
                x0cs[c] = t

        load_x0(0)
        load_x0(1)

        de_ps = psum.tile([P, DIM], F32, tag="py", bufs=4, name="de_ps")
        avs = {}

        def col_sums(c):
            for g, (a0, a1) in enumerate(((0, 2), (2, 4)) if c == N_CHUNKS - 1 else ((0, 4),)):
                for j in range(8):
                    col = ((c + g) * 8 + j) * NW
                    for a in range(a0, a1):
                        nc.tensor.matmul(
                            out=de_ps[:, col : col + NW],
                            lhsT=hc[c][:, a, P * j : P * j + P],
                            rhs=ones_w[:],
                            start=(a == a0),
                            stop=(a == a1 - 1),
                        )

        def row_sums(c):
            dv = small.tile([P, A], F32, name="dv")
            for a in range(A):
                if a in ROWS_ON_SCALAR:
                    junk2 = work.tile([P, N_EDGES], BF16, name="junk2")
                    nc.scalar.activation(
                        out=junk2[:],
                        in_=hc[c][:, a, :],
                        func=ACT.Copy,
                        accum_out=dv[:, a : a + 1],
                    )
                else:
                    junk1 = work.tile([P, N_EDGES], BF16, name="junk1")
                    nc.vector.tensor_scalar(
                        out=junk1[:],
                        in0=hc[c][:, a, :],
                        scalar1=1.0,
                        scalar2=None,
                        op0=ALU.mult,
                        op1=ALU.add,
                        accum_out=dv[:, a : a + 1],
                    )
            dvm = small.tile([P, A], F32, name="dvm")
            nc.vector.tensor_scalar_max(out=dvm[:], in0=dv[:], scalar1=1.0)
            av = small.tile([P, A], F32, name="av", bufs=N_CHUNKS)
            nc.gpsimd.tensor_tensor(out=av[:], in0=dvm[:], in1=mhalf[:, 0:A], op=ALU.pow)
            avs[c] = av

        x1g = work.tile([P, 2, DIM, 4], BF16, tag="vt", name="x1g", align_bytes=64)
        wg = const.tile([P, DIM, 4], BF16, name="wg", align_bytes=64)

        for c in range(N_CHUNKS):
            col_sums(c)
            row_sums(c)

        htg = {}
        hq = {}
        msgs = {}
        mqs = {}
        vts = {}
        ys = {}
        stat = {}

        def live(c):
            return 0 <= c < N_CHUNKS

        abt = {}

        def planes(c, tiles):
            if not live(c):
                return
            if c not in abt:
                abt[c] = work.tile([P, A, N_EDGES], BF16, name="ab", bufs=1)
            for a in tiles:
                nc.scalar.activation(
                    out=abt[c][:, a, :], in_=b_all[:], func=ACT.Copy, scale=avs[c][:, a : a + 1]
                )

        def scale(c, tiles=(0, 1, 2, 3)):
            if not live(c):
                return
            for a in tiles:
                if a in PLANES_ON_SCALAR.get(c, ()):
                    nc.vector.tensor_tensor(
                        out=hc[c][:, a, :], in0=hc[c][:, a, :], in1=abt[c][:, a, :], op=ALU.mult
                    )
                else:
                    nc.vector.scalar_tensor_tensor(
                        out=hc[c][:, a, :],
                        in0=hc[c][:, a, :],
                        scalar=avs[c][:, a : a + 1],
                        in1=b_all[:],
                        op0=ALU.mult,
                        op1=ALU.mult,
                    )

        def turn(c):
            if not live(c):
                return
            t = work.tile([P, 2, CHUNK, 4], BF16, tag="htg", name="htg", align_bytes=64)
            htg[c] = t
            t_w = (
                t[:]
                .rearrange("p g n t -> p (g n t)")
                .bitcast(F32)
                .rearrange("p (g n u) -> p g n u", g=2, n=CHUNK, u=2)
            )
            for a in range(A):
                tp = psum.tile([P, 4, P], F32, tag="px", bufs=4, name="tp")
                hw = hc[c][:, a, :].bitcast(F32)
                for wb in range(4):
                    nc.tensor.transpose(tp[:, wb, :], hw[:, P * wb : P * wb + P], ident[:])
                nc.scalar.copy(
                    out=t_w[:, :, P * a : P * a + P, :],
                    in_=tp[:].rearrange("p (g u) n -> p g n u", g=2),
                )

        def quant_h(c):
            if not live(c):
                return
            hcod = work.tile([P, 2, CHUNK], U32, name="hcod", align_bytes=64)
            hsc = work.tile([P, 2, CHUNK], U8, name="hsc", align_bytes=64)
            nc.vector.quantize_mx(
                out=hcod[:].rearrange("p g n -> p (g n)").bitcast(FP8X4),
                scales=hsc[:].rearrange("p g n -> p (g n)"),
                in_=htg[c][:].rearrange("p g n t -> p (g n t)"),
            )
            hq[c] = (hcod, hsc)

        m1s = {}

        def first_product(c, tiles):
            if not live(c):
                return
            hcod, hsc = hq[c]
            for a in tiles:
                cols = slice(P * a, P * a + P)
                m1 = psum.tile([P, 4, P], F32, tag="px", bufs=4, name="m1")
                for q in range(WARM if a == 0 else 0):
                    nc.tensor.matmul_mx(
                        out=m1[:].rearrange("p t n -> p (t n)"),
                        lhsT=x1cod[:, 0, 0:P].bitcast(FP8X4),
                        lhsT_scale=x1sc[:, 0, 0:P],
                        rhs=x1cod[:, 1, :].bitcast(FP8X4),
                        rhs_scale=x1sc[:, 1, :],
                        start=True,
                        stop=True,
                    )
                for tb in range(4):
                    for g in range(2):
                        nc.tensor.matmul_mx(
                            out=m1[:, tb, :],
                            lhsT=x1cod[:, g, P * tb : P * tb + P].bitcast(FP8X4),
                            lhsT_scale=x1sc[:, g, P * tb : P * tb + P],
                            rhs=hcod[:, g, cols].bitcast(FP8X4),
                            rhs_scale=hsc[:, g, cols],
                            start=(g == 0),
                            stop=(g == 1),
                        )
                m1s[c, a] = m1

        def message(c, a):
            if not live(c):
                return
            if c not in msgs:
                msgs[c] = work.tile([P, CHUNK, 4], BF16, tag="msgg", name="msgg", align_bytes=64)
            copy = nc.vector.tensor_copy if c >= N_CHUNKS - 2 and a < 3 or 0 < c < 3 and a < 2 else nc.scalar.copy
            copy(out=msgs[c][:, P * a : P * a + P, :], in_=m1s[c, a][:].rearrange("p t n -> p n t"))

        def quant_m(c):
            if not live(c):
                return
            mcod = work.tile([P, CHUNK], U32, name="mcod", align_bytes=64)
            msc = work.tile([P, CHUNK], U8, name="msc", align_bytes=64)
            nc.vector.quantize_mx(
                out=mcod[:].bitcast(FP8X4),
                scales=msc[:],
                in_=msgs[c][:].rearrange("p n t -> p (n t)"),
            )
            mqs[c] = (mcod, msc)

        def second_product(c):
            if not live(c):
                return
            mcod, msc = mqs[c]
            vt = work.tile([P, 4, CHUNK], F32, tag="vt", name="vt", align_bytes=64)
            for db in range(4):
                u_ps = psum.tile([P, CHUNK], F32, tag="py", bufs=4, name="u_ps")
                nc.tensor.matmul_mx(
                    out=u_ps[:],
                    lhsT=wcod[:, P * db : P * db + P].bitcast(FP8X4),
                    lhsT_scale=wsc[:, P * db : P * db + P],
                    rhs=mcod[:].bitcast(FP8X4),
                    rhs_scale=msc[:],
                    start=True,
                    stop=True,
                )
                nc.scalar.activation(
                    out=vt[:, db, :],
                    in_=u_ps[:],
                    func=ACT.Identity,
                    bias=ccol[:, db : db + 1],
                    scale=gcol[:],
                )
            vts[c] = vt

        yps = {}

        def residual_x(c):
            if not live(c):
                return
            for a in range(A):
                t = psum.tile([P, DIM], F32, tag="py", bufs=4, name="y_ps")
                nc.tensor.matmul(
                    out=t[:], lhsT=ident_bf[:], rhs=x0cs[c][:, a, :], start=True, stop=False
                )
                yps[c, a] = t

        def residual_u(c, tiles=(0, 1, 2, 3)):
            if not live(c):
                return
            if c not in ys:
                ys[c] = big.tile([P, A, DIM], F32, tag="big%d" % c, name="y%d" % c, align_bytes=64)
                stat[c] = [small.tile([P, A], F32, name="s%d" % q) for q in range(4)]
            for a in tiles:
                for db in range(4):
                    nc.tensor.matmul(
                        out=yps[c, a][:, P * db : P * db + P],
                        lhsT=vts[c][:, db, P * a : P * a + P],
                        rhs=ident[:],
                        is_transpose=True,
                        start=False,
                        stop=(db == 3),
                    )
                nc.scalar.activation(
                    out=ys[c][:, a, :],
                    in_=yps[c, a][:],
                    func=ACT.Copy,
                    accum_out=stat[c][0][:, a : a + 1],
                )

        def neg_mean(c, a0, a1):
            if live(c):
                nc.scalar.activation(
                    out=stat[c][1][:, a0:a1],
                    in_=stat[c][0][:, a0:a1],
                    func=ACT.Copy,
                    scale=-1.0 / DIM,
                )

        def squares(c, tiles=(0, 1, 2, 3)):
            if not live(c):
                return
            for a in tiles:
                junk = work.tile([P, DIM], BF16, name="junk")
                nc.scalar.activation(
                    out=junk[:],
                    in_=ys[c][:, a, :],
                    func=ACT.Square,
                    bias=stat[c][0][:, a : a + 1],
                    scale=-float(DIM),
                    accum_out=stat[c][2][:, a : a + 1],
                )

        def inv_std(c, a0, a1):
            if live(c):
                nc.scalar.activation(
                    out=stat[c][3][:, a0:a1],
                    in_=stat[c][2][:, a0:a1],
                    func=ACT.Abs_reciprocal_sqrt,
                    scale=1.0 / DIM**3,
                    bias=LN_EPS,
                )

        def gain(c, tiles):
            if not live(c):
                return
            y = ys[c]
            for a in tiles:
                nc.vector.scalar_tensor_tensor(
                    out=y[:, a, :],
                    in0=y[:, a, :],
                    scalar=stat[c][1][:, a : a + 1],
                    in1=gb[:, 0, :],
                    op0=ALU.add,
                    op1=ALU.mult,
                )

        def shift(c, tiles):
            if not live(c):
                return
            y = ys[c]
            for a in tiles:
                nc.vector.scalar_tensor_tensor(
                    out=y[:, a, :],
                    in0=y[:, a, :],
                    scalar=stat[c][3][:, a : a + 1],
                    in1=gb[:, 1, :],
                    op0=ALU.mult,
                    op1=ALU.add,
                )

        def store(c, a0=0, a1=A):
            if not live(c):
                return
            nc.sync.dma_start(
                out=out[c * CHUNK : (c + 1) * CHUNK, :].rearrange("(p a) d -> p a d", a=A)[:, a0:a1],
                in_=ys[c][:, a0:a1],
            )

        with tc.manual_schedule(
            engines={
                mybir.EngineType.PE,
                mybir.EngineType.Activation,
                mybir.EngineType.DVE,
                mybir.EngineType.Pool,
            }
        ):
            de = small.tile([P, 8], F32, name="de")
            nc.vector.tensor_reduce(
                out=de[:],
                in_=de_ps[:, 0 : (N_CHUNKS + 1) * 8 * NW].rearrange(
                    "p (c j w) -> p j c w", c=N_CHUNKS + 1, j=8, w=NW
                )[:, :, :, 0],
                axis=AX.X,
                op=ALU.add,
            )
            dem = small.tile([P, 8], F32, name="dem")
            nc.vector.tensor_scalar_max(out=dem[:], in0=de[:], scalar1=1.0)
            bnat = small.tile([P, 8], F32, name="bnat")
            nc.gpsimd.tensor_tensor(out=bnat[:], in0=dem[:], in1=mhalf[:], op=ALU.pow)
            nc.scalar.copy(out=x1g[:, 0], in_=x1raw[:, 0:4, :].rearrange("p t d -> p d t"))
            nc.vector.tensor_copy(out=x1g[:, 1], in_=x1raw[:, 4:8, :].rearrange("p t d -> p d t"))
            bnt_ps = psum.tile([P, P], BF16, tag="py", bufs=4, name="bnt_ps")
            nc.tensor.transpose(bnt_ps[:], bn_rows[:], ident_bf[:])
            nc.vector.tensor_scalar(
                out=ccol[:], in0=bnt_ps[:, 0:4], scalar1=gcol[:], scalar2=None, op0=ALU.mult
            )
            gb = const.tile([P, 2, DIM], F32)
            gb_ps = []
            for k in range(2):
                t = psum.tile([P, DIM], F32, tag="py", bufs=4, name="gb_ps")
                nc.tensor.matmul(out=t[:], lhsT=ones_m[:], rhs=vecs[:, k, :], start=True, stop=True)
                gb_ps.append(t)
            for h in range(2):
                b_ps = psum.tile([P, 4, P], F32, tag="px", bufs=4, name="b_ps")
                for k in range(4):
                    j = 4 * h + k
                    nc.tensor.transpose(
                        b_ps[:, k, :], bnat[:, j : j + 1].to_broadcast([P, P]), ident[:]
                    )
                copy = nc.vector.tensor_copy if h == 0 else nc.scalar.copy
                copy(out=b_all[:, 512 * h : 512 * h + 512], in_=b_ps[:].rearrange("p k m -> p (k m)"))

            planes(0, PLANES_ON_SCALAR[0])
            scale(0)
            turn(0)
            nc.vector.quantize_mx(
                out=x1cod[:].rearrange("p g d -> p (g d)").bitcast(FP8X4),
                scales=x1sc[:].rearrange("p g d -> p (g d)"),
                in_=x1g[:].rearrange("p g d t -> p (g d t)"),
            )
            planes(1, PLANES_ON_SCALAR[1])
            for k in range(2):
                nc.scalar.copy(out=gb[:, k, :], in_=gb_ps[k][:])
            nc.vector.tensor_copy(out=wg[:], in_=wraw[:].rearrange("p t n -> p n t"))
            quant_h(0)
            scale(1)
            first_product(0, range(A))
            nc.vector.quantize_mx(
                out=wcod[:].bitcast(FP8X4),
                scales=wsc[:],
                in_=wg[:].rearrange("p n t -> p (n t)"),
            )
            for a in range(A):
                message(0, a)
            quant_m(0)
            scale(2, (0,))
            for i in range(N_CHUNKS):
                turn(i + 1)
                second_product(i)
                if i == 0:
                    planes(2, PLANES_ON_SCALAR.get(2, ()))
                    scale(2, (1,))
                quant_h(i + 1)
                neg_mean(i - 1, 0, A)
                squares(i - 1)
                if i == 0:
                    scale(2, (2, 3))
                else:
                    scale(i + 3, (0, 1, 2))
                    gain(i - 2, (3,))
                    scale(i + 3, (3,))
                    shift(i - 2, (3,))
                    store(i - 2)
                first_product(i + 1, range(A))
                message(i + 1, 0)
                message(i + 1, 1)
                message(i + 1, 2)
                inv_std(i - 1, 0, A)
                message(i + 1, 3)
                residual_x(i)
                if i == 0:
                    planes(3, PLANES_ON_SCALAR.get(3, ()))
                if i < N_CHUNKS - 1:
                    residual_u(i)
                else:
                    residual_u(i, (0, 1))
                    squares(i, (0, 1))
                    neg_mean(i, 0, 2)
                    residual_u(i, (2, 3))
                    inv_std(i, 0, 2)
                    squares(i, (2, 3))
                    neg_mean(i, 2, 4)
                    inv_std(i, 2, 4)
                gain(i - 1, (0,))
                quant_m(i + 1)
                gain(i - 1, (1, 2))
                shift(i - 1, (0, 1, 2))
                if i == 0:
                    scale(3)
                load_x0(i + 2)
            gain(N_CHUNKS - 2, (3,))
            gain(N_CHUNKS - 1, (0, 1))
            shift(N_CHUNKS - 2, (3,))
            store(N_CHUNKS - 2)
            shift(N_CHUNKS - 1, (0, 1))
            store(N_CHUNKS - 1, 0, 2)
            gain(N_CHUNKS - 1, (2, 3))
            for a in (2, 3):
                shift(N_CHUNKS - 1, (a,))
                store(N_CHUNKS - 1, a, a + 1)
